import numpy as np
import ml_dtypes


def mxq(x, axis, fmt="e4m3"):
    dtype, down = {"e4m3": (ml_dtypes.float8_e4m3fn, 7), "e5m2": (ml_dtypes.float8_e5m2, 14)}[fmt]
    v = np.moveaxis(np.asarray(x, np.float32).astype(ml_dtypes.bfloat16).astype(np.float64), axis, -1)
    blocks = v.reshape(v.shape[:-1] + (-1, 32))
    amax = np.abs(blocks).max(-1, keepdims=True)
    byte = np.maximum(np.where(amax > 0, np.frexp(amax)[1] - 1 + 127, 0) - down, 1)
    scale = np.exp2(byte - 127.0)
    codes = (blocks / scale).astype(np.float32).astype(dtype).astype(np.float64)
    return np.moveaxis((codes * scale).reshape(v.shape), -1, axis)


WIDE = False


def mx_kscale(k):
    if not WIDE:
        return np.ones(k)
    levels = np.array([10, -10, 5, -5, 0])
    a = np.random.permutation(np.resize(levels, k // 512 * 4)).reshape(k // 512, 4)
    idx = np.arange(k)
    return np.exp2(a[idx // 512, idx % 128 // 32])


BF16 = ml_dtypes.bfloat16


def bf(x):
    return np.asarray(x, np.float32).astype(BF16)


def f64(x):
    return np.asarray(x).astype(np.float64)


B, S, D, H, N = 1, 512, 2048, 16, 2048
DH = D // H
NEG = -1e9
ALIBI_BIAS_MAX = 8.0


def gen_slopes(n_heads):
    n = 1
    while n < n_heads:
        n *= 2
    m = np.arange(1, n + 1, dtype=np.float64) * (ALIBI_BIAS_MAX / n)
    slopes = 1.0 / np.power(2.0, m)
    if n != n_heads:
        slopes = np.concatenate([slopes[1::2], slopes[::2]])[:n_heads]
    return slopes.reshape(1, n_heads, 1, 1)


def alibi_bias(n_heads, seq_len):
    ab = np.arange(1 - seq_len, 1, dtype=np.float64).reshape(1, 1, 1, seq_len)
    return ab * gen_slopes(n_heads)


def setup_inputs():
    t = mx_kscale(D)
    blocked = np.random.random_sample((S, S)) < 0.5
    m = np.where(blocked, NEG, 0.25 * np.random.standard_normal((S, S)))
    v_level = np.random.standard_normal((H, DH))
    return {"xq": bf(np.random.standard_normal((B, S, H, DH)) * 1.25),
            "xk": bf(np.random.standard_normal((B, S, H, DH)) * 1.25),
            "xv": bf((v_level + 0.75 * np.random.standard_normal((B, S, H, DH))) * t.reshape(H, DH)),
            "mask": bf(m[None, None]),
            "w_out": bf(np.random.standard_normal((D, N)) * 1.25 / np.sqrt(D) / t[:, None])}


def reference(xq, xk, xv, mask, w_out):
    q = f64(xq).transpose(0, 2, 1, 3)
    kt = f64(xk).transpose(0, 2, 3, 1)
    v = f64(xv).transpose(0, 2, 1, 3)
    scores = q @ kt / np.sqrt(DH)
    scores = scores + alibi_bias(H, S)[..., :S] + f64(mask)
    e = np.exp(scores - scores.max(-1, keepdims=True))
    o = (mxq(e, 3, "e4m3") @ mxq(v, 2, "e4m3")) / e.sum(-1, keepdims=True)
    o = o.transpose(0, 2, 1, 3).reshape(B, S, D)
    return mxq(o, 2, "e4m3") @ mxq(f64(w_out), 0, "e4m3")

@@ -1,0 +1,278 @@
+import math
+from contextlib import ExitStack
+
+import concourse.mybir as mybir
+from concourse.masks import make_identity
+
+F32 = mybir.dt.float32
+BF16 = mybir.dt.bfloat16
+I32 = mybir.dt.int32
+U32 = mybir.dt.uint32
+U8 = mybir.dt.uint8
+FP8X4 = mybir.dt.float8_e4m3fn_x4
+ALU = mybir.AluOpType
+ACT = mybir.ActivationFunctionType
+AXIS = mybir.AxisListType
+
+P = 128
+PACK = 4
+K_PASS = P * PACK
+SEQ = 512
+HEADS = 16
+HEAD_DIM = 128
+FEATURES = HEADS * HEAD_DIM
+N_OUT = 2048
+SEQ_TILES = SEQ // P
+GROUP_HEADS = K_PASS // HEAD_DIM
+GROUPS = HEADS // GROUP_HEADS
+BLOCK_TILES = 2
+BLOCK = BLOCK_TILES * P
+BLOCKS = SEQ // BLOCK
+N_TILE = 512
+N_TILES = N_OUT // N_TILE
+SQRT_DIM = math.sqrt(HEAD_DIM)
+
+FLOPS = 2 * 2 * HEADS * SEQ * SEQ * HEAD_DIM + 2 * SEQ * FEATURES * N_OUT
+
+
+def tile_mptattentionfused_pa_kernel(tc, xq, xk, xv, mask, w_out, out):
+    nc = tc.nc
+    xq_rows = xq.rearrange("b (t p) h d -> p (b t) (h d)", p=P)
+    xk_rows = xk.rearrange("b (t p) h d -> p (b t) (h d)", p=P)
+    xv_rows = xv.rearrange("b (u p e) h d -> p (b u) e (h d)", p=P, e=2)
+    w_rows = w_out.rearrange("(g u p e) n -> g p u e n", u=2, p=P, e=2)
+    mask_rows = mask.rearrange("a b (t p) j -> p (a b t) j", p=P)
+    out_rows = out.rearrange("b (t p) n -> (b t) p n", p=P)
+
+    with ExitStack() as stack:
+        keep = stack.enter_context(tc.tile_pool(name="keep", bufs=1))
+        work = stack.enter_context(tc.tile_pool(name="work", bufs=2))
+        psum = stack.enter_context(tc.psum_pool(name="psum", bufs=1))
+
+        ident_bf = keep.tile([P, P], BF16)
+        make_identity(nc, ident_bf[:])
+        ident_f = keep.tile([P, P], F32)
+        make_identity(nc, ident_f[:])
+
+        key_dist_i = keep.tile([P, SEQ_TILES], I32)
+        nc.gpsimd.iota(key_dist_i[:], pattern=[[P, SEQ_TILES]], base=1 - SEQ, channel_multiplier=1)
+        key_dist = keep.tile([P, SEQ_TILES], F32)
+        nc.vector.tensor_copy(out=key_dist[:], in_=key_dist_i[:])
+        alibi = keep.tile([P, HEADS, SEQ_TILES], F32)
+        for h in range(HEADS):
+            slope = 2.0 ** (-(h + 1) / 2)
+            nc.vector.tensor_scalar_mul(out=alibi[:, h, :], in0=key_dist[:], scalar1=slope * SQRT_DIM)
+
+        mask_sb = work.tile([P, SEQ_TILES, SEQ], BF16, bufs=1)
+        nc.sync.dma_start(out=mask_sb[:], in_=mask_rows)
+        mask_t = keep.tile([P, SEQ_TILES, SEQ], F32)
+        for t in range(SEQ_TILES):
+            mask_ps = psum.tile([P, SEQ_TILES, P], BF16, tag="tr", bufs=2)
+            for it in range(SEQ_TILES):
+                nc.tensor.transpose(mask_ps[:, it, :], mask_sb[:, it, t * P : (t + 1) * P], ident_bf[:])
+            nc.scalar.mul(
+                out=mask_t[:, t, :], in_=mask_ps[:].rearrange("p a i -> p (a i)"), mul=SQRT_DIM
+            )
+
+        def quantise_columns(raw, cols, codes, scales):
+            grouped = work.tile([P, N_TILE, PACK], BF16, tag="grouped", bufs=3, align_bytes=64)
+            nc.gpsimd.tensor_scalar(
+                out=grouped[:],
+                in0=raw[:, :, cols].rearrange("p t c -> p c t"),
+                scalar1=1.0,
+                scalar2=0.0,
+                op0=ALU.mult,
+                op1=ALU.add,
+            )
+            nc.vector.quantize_mx(
+                out=codes.bitcast(FP8X4), scales=scales, in_=grouped[:].rearrange("p c t -> p (c t)")
+            )
+
+        xk_raw = []
+        xq_raw = []
+        w_raw = []
+
+        def load_heads(g):
+            cols = slice(g * K_PASS, (g + 1) * K_PASS)
+            k_tile = work.tile([P, SEQ_TILES, K_PASS], BF16, tag="xk_raw", bufs=2, name="xk_raw%d" % g)
+            nc.sync.dma_start(out=k_tile[:], in_=xk_rows[:, :, cols])
+            xk_raw.append(k_tile)
+            q_tile = work.tile([P, SEQ_TILES, K_PASS], BF16, tag="xq_raw", bufs=2, name="xq_raw%d" % g)
+            nc.sync.dma_start(out=q_tile[:], in_=xq_rows[:, :, cols])
+            xq_raw.append(q_tile)
+
+        def load_weights(g):
+            w_tile = work.tile([P, PACK, N_OUT], BF16, tag="raw", bufs=3, name="w_raw%d" % g)
+            nc.sync.dma_start(out=w_tile[:].rearrange("p (u e) n -> p u e n", e=2), in_=w_rows[g])
+            w_raw.append(w_tile)
+
+        load_heads(0)
+        xv_raw = work.tile([P, PACK, FEATURES], BF16, tag="raw", bufs=3)
+        nc.sync.dma_start(out=xv_raw[:].rearrange("p (u e) f -> p u e f", e=2), in_=xv_rows)
+        load_heads(1)
+        load_weights(0)
+        load_heads(2)
+        load_weights(1)
+        load_heads(3)
+        load_weights(2)
+        load_weights(3)
+
+        v_codes = keep.tile([P, FEATURES], U32, align_bytes=64)
+        v_scales = keep.tile([P, FEATURES], U8, align_bytes=64)
+        for g in range(GROUPS):
+            cols = slice(g * N_TILE, (g + 1) * N_TILE)
+            quantise_columns(xv_raw, cols, v_codes[:, cols], v_scales[:, cols])
+
+        w_codes = keep.tile([P, GROUPS, N_OUT], U32, align_bytes=64)
+        w_scales = keep.tile([P, GROUPS, N_OUT], U8, align_bytes=64)
+
+        qk_t = keep.tile([P, HEADS, 2 * SEQ], BF16)
+
+        def transpose_head(h):
+            g, a = divmod(h, GROUP_HEADS)
+            cols = slice(a * HEAD_DIM, (a + 1) * HEAD_DIM)
+            qk_ps = psum.tile([P, 2 * SEQ_TILES, P], BF16, tag="tr", bufs=2)
+            for t in range(SEQ_TILES):
+                nc.tensor.transpose(qk_ps[:, t, :], xk_raw[g][:, t, cols], ident_bf[:])
+            for t in range(SEQ_TILES):
+                nc.tensor.transpose(qk_ps[:, SEQ_TILES + t, :], xq_raw[g][:, t, cols], ident_bf[:])
+            nc.scalar.copy(out=qk_t[:, h, :], in_=qk_ps[:].rearrange("p a i -> p (a i)"))
+
+        def to_mx_rows(words_ps, codes, scales, tag):
+            grouped = work.tile([P, BLOCK_TILES, P, PACK], BF16, tag=tag, bufs=2, align_bytes=64)
+            flat = grouped[:].rearrange("p q i t -> p (q i t)")
+            nc.scalar.copy(
+                out=flat.bitcast(F32).rearrange("p (q i u) -> p q i u", q=BLOCK_TILES, u=2),
+                in_=words_ps[:].rearrange("p q u i -> p q i u"),
+            )
+            nc.vector.quantize_mx(out=codes.bitcast(FP8X4), scales=scales, in_=flat)
+
+        def project(o_codes, o_scales, blk, q, n):
+            acc = psum.tile([P, N_TILE], F32, tag="acc", bufs=2)
+            rows = slice(q * P, (q + 1) * P)
+            cols = slice(n * N_TILE, (n + 1) * N_TILE)
+            for g in range(GROUPS):
+                nc.tensor.matmul_mx(
+                    out=acc[:],
+                    lhsT=o_codes[:, g, rows].bitcast(FP8X4),
+                    lhsT_scale=o_scales[:, g, rows],
+                    rhs=w_codes[:, g, cols].bitcast(FP8X4),
+                    rhs_scale=w_scales[:, g, cols],
+                    start=(g == 0),
+                    stop=(g == GROUPS - 1),
+                )
+            result = work.tile([P, N_TILE], F32, tag="result", bufs=3)
+            nc.scalar.copy(out=result[:], in_=acc[:])
+            nc.sync.dma_start(out=out_rows[blk * BLOCK_TILES + q][:, cols], in_=result[:])
+
+        done = None
+        for blk in range(BLOCKS):
+            o_codes = work.tile([P, GROUPS, BLOCK], U32, tag="o_codes", bufs=2, align_bytes=64)
+            o_scales = work.tile([P, GROUPS, BLOCK], U8, tag="o_scales", bufs=2, align_bytes=64)
+            for h in range(HEADS):
+                g, a = divmod(h, GROUP_HEADS)
+                pair, b = divmod(a, 2)
+                if blk == 0:
+                    transpose_head(h)
+
+                bias_t = work.tile([P, SEQ_TILES, BLOCK], F32, tag="bias_t", bufs=2)
+                for t in range(SEQ_TILES):
+                    nc.vector.tensor_scalar_add(
+                        out=bias_t[:, t, :],
+                        in0=mask_t[:, t, blk * BLOCK : (blk + 1) * BLOCK],
+                        scalar1=alibi[:, h, t : t + 1],
+                    )
+
+                if b == 0:
+                    row_sum = work.tile([P, BLOCK_TILES, 2], F32, tag="row_sum", bufs=2)
+                    pv_ps = psum.tile([P, BLOCK_TILES, 2, HEAD_DIM], F32, tag="pv", bufs=1)
+                if a == 0:
+                    o_sb = work.tile([P, BLOCK_TILES, K_PASS], BF16, tag="o_sb", bufs=2)
+
+                e_ps = psum.tile([P, BLOCK_TILES, 2, P], F32, tag="tr", bufs=2)
+                for q in range(BLOCK_TILES):
+                    it = blk * BLOCK_TILES + q
+                    s_ps = psum.tile([P, SEQ], F32, tag="s", bufs=3)
+                    nc.tensor.matmul(
+                        out=s_ps[:],
+                        lhsT=qk_t[:, h, SEQ + it * P : SEQ + (it + 1) * P],
+                        rhs=qk_t[:, h, 0:SEQ],
+                        start=True,
+                        stop=False,
+                    )
+                    for t in range(SEQ_TILES):
+                        nc.tensor.matmul(
+                            out=s_ps[:, t * P : (t + 1) * P],
+                            lhsT=bias_t[:, t, q * P : (q + 1) * P],
+                            rhs=ident_f[:],
+                            is_transpose=True,
+                            start=False,
+                            stop=(t == SEQ_TILES - 1),
+                        )
+                    row_max = work.tile([P, 1], F32, tag="row_max", bufs=4)
+                    nc.vector.tensor_reduce(out=row_max[:], in_=s_ps[:], axis=AXIS.X, op=ALU.max)
+                    shift = work.tile([P, 1], F32, tag="shift", bufs=4)
+                    nc.vector.tensor_scalar_mul(out=shift[:], in0=row_max[:], scalar1=-1.0 / SQRT_DIM)
+                    e_sb = work.tile([P, SEQ], BF16, tag="e_sb", bufs=4)
+                    nc.scalar.activation(
+                        out=e_sb[:],
+                        in_=s_ps[:],
+                        func=ACT.Exp,
+                        bias=shift[:],
+                        scale=1.0 / SQRT_DIM,
+                        accum_out=row_sum[:, q, b : b + 1],
+                    )
+                    for u in range(2):
+                        nc.tensor.transpose(
+                            e_ps[:, q, u, :], e_sb[:].bitcast(F32)[:, u * P : (u + 1) * P], ident_f[:]
+                        )
+
+                e_codes = work.tile([P, BLOCK], U32, tag="e_codes", bufs=2, align_bytes=64)
+                e_scales = work.tile([P, BLOCK], U8, tag="e_scales", bufs=2, align_bytes=64)
+                to_mx_rows(e_ps, e_codes[:], e_scales[:], "e_grouped")
+                for q in range(BLOCK_TILES):
+                    rows = slice(q * P, (q + 1) * P)
+                    cols = slice(h * HEAD_DIM, (h + 1) * HEAD_DIM)
+                    nc.tensor.matmul_mx(
+                        out=pv_ps[:, q, b, :],
+                        lhsT=e_codes[:, rows].bitcast(FP8X4),
+                        lhsT_scale=e_scales[:, rows],
+                        rhs=v_codes[:, cols].bitcast(FP8X4),
+                        rhs_scale=v_scales[:, cols],
+                        start=True,
+                        stop=True,
+                    )
+
+                if b == 1:
+                    inv_sum = work.tile([P, BLOCK_TILES, 2], F32, tag="inv_sum", bufs=2)
+                    nc.vector.reciprocal(out=inv_sum[:], in_=row_sum[:])
+                    nc.vector.tensor_tensor(
+                        out=o_sb[:, :, pair * 2 * HEAD_DIM : (pair + 1) * 2 * HEAD_DIM].rearrange(
+                            "p q (b d) -> p q b d", b=2
+                        ),
+                        in0=pv_ps[:],
+                        in1=inv_sum[:].unsqueeze(3).to_broadcast([P, BLOCK_TILES, 2, HEAD_DIM]),
+                        op=ALU.mult,
+                    )
+
+                if a == GROUP_HEADS - 1:
+                    o_ps = psum.tile([P, BLOCK_TILES, 2, P], F32, tag="tr", bufs=2)
+                    for q in range(BLOCK_TILES):
+                        for u in range(2):
+                            nc.tensor.transpose(
+                                o_ps[:, q, u, :],
+                                o_sb[:, q, :].bitcast(F32)[:, u * P : (u + 1) * P],
+                                ident_f[:],
+                            )
+                    to_mx_rows(o_ps, o_codes[:, g, :], o_scales[:, g, :], "o_grouped")
+
+                if blk == 0:
+                    cols = slice(a * N_TILE, (a + 1) * N_TILE)
+                    quantise_columns(w_raw[g], cols, w_codes[:, g, cols], w_scales[:, g, cols])
+                elif h < BLOCK_TILES * N_TILES:
+                    project(done[0], done[1], blk - 1, h // N_TILES, h % N_TILES)
+            done = (o_codes, o_scales)
+
+        for q in range(BLOCK_TILES):
+            for n in range(N_TILES):
+                project(done[0], done[1], BLOCKS - 1, q, n)

@@ -30,6 +30,7 @@ BLOCK = BLOCK_TILES * P
 BLOCKS = SEQ // BLOCK
 N_TILE = 512
 N_TILES = N_OUT // N_TILE
+UNITS = BLOCKS * HEADS
 SQRT_DIM = math.sqrt(HEAD_DIM)
 
 FLOPS = 2 * 2 * HEADS * SEQ * SEQ * HEAD_DIM + 2 * SEQ * FEATURES * N_OUT
@@ -48,6 +49,37 @@ def tile_mptattentionfused_pa_kernel(tc, xq, xk, xv, mask, w_out, out):
         keep = stack.enter_context(tc.tile_pool(name="keep", bufs=1))
         work = stack.enter_context(tc.tile_pool(name="work", bufs=2))
         psum = stack.enter_context(tc.psum_pool(name="psum", bufs=1))
+        stack.enter_context(tc.manual_schedule())
+
+        mask_sb = work.tile([P, SEQ_TILES, SEQ], BF16, bufs=1)
+        nc.sync.dma_start(out=mask_sb[:], in_=mask_rows)
+        xk_raw = []
+        xq_raw = []
+        k_first_raw = []
+
+        def load_heads(g):
+            cols = slice(g * K_PASS, (g + 1) * K_PASS)
+            k_tile = work.tile([P, SEQ_TILES, K_PASS], BF16, tag="xk_raw", bufs=2, name="xk_raw%d" % g)
+            nc.sync.dma_start(out=k_tile[:], in_=xk_rows[:, :, cols])
+            xk_raw.append(k_tile)
+            q_tile = work.tile([P, SEQ_TILES, K_PASS], BF16, tag="xq_raw", bufs=2, name="xq_raw%d" % g)
+            nc.sync.dma_start(out=q_tile[:], in_=xq_rows[:, :, cols])
+            xq_raw.append(q_tile)
+
+        def load_k_first(rows, name):
+            raw = work.tile([P, PACK, N_OUT], BF16, tag="raw", bufs=3, name=name)
+            nc.sync.dma_start(out=raw[:].rearrange("p (u e) n -> p u e n", e=2), in_=rows)
+            k_first_raw.append(raw)
+
+        load_heads(0)
+        load_k_first(xv_rows, "xv_raw")
+        load_heads(1)
+        load_k_first(w_rows[0], "w_raw0")
+        load_heads(2)
+        load_k_first(w_rows[1], "w_raw1")
+        load_heads(3)
+        load_k_first(w_rows[2], "w_raw2")
+        load_k_first(w_rows[3], "w_raw3")
 
         ident_bf = keep.tile([P, P], BF16)
         make_identity(nc, ident_bf[:])
@@ -63,8 +95,6 @@ def tile_mptattentionfused_pa_kernel(tc, xq, xk, xv, mask, w_out, out):
             slope = 2.0 ** (-(h + 1) / 2)
             nc.vector.tensor_scalar_mul(out=alibi[:, h, :], in0=key_dist[:], scalar1=slope * SQRT_DIM)
 
-        mask_sb = work.tile([P, SEQ_TILES, SEQ], BF16, bufs=1)
-        nc.sync.dma_start(out=mask_sb[:], in_=mask_rows)
         mask_t = keep.tile([P, SEQ_TILES, SEQ], F32)
         for t in range(SEQ_TILES):
             mask_ps = psum.tile([P, SEQ_TILES, P], BF16, tag="tr", bufs=2)
@@ -74,59 +104,38 @@ def tile_mptattentionfused_pa_kernel(tc, xq, xk, xv, mask, w_out, out):
                 out=mask_t[:, t, :], in_=mask_ps[:].rearrange("p a i -> p (a i)"), mul=SQRT_DIM
             )
 
-        def quantise_columns(raw, cols, codes, scales):
+        k_first_codes = keep.tile([P, 1 + GROUPS, N_OUT], U32, align_bytes=64)
+        k_first_scales = keep.tile([P, 1 + GROUPS, N_OUT], U8, align_bytes=64)
+        qk_t = keep.tile([P, HEADS, 2 * SEQ], BF16)
+
+        bias_of = {}
+        scores_of = {}
+        e_of = {}
+        e_grouped_of = {}
+        e_mx_of = {}
+        sums_of = {}
+        pv_of = {}
+        o_of = {}
+        o_grouped_of = {}
+        o_mx_of = {}
+
+        def quantise_k_first(c):
+            r, n = divmod(c, N_TILES)
+            cols = slice(n * N_TILE, (n + 1) * N_TILE)
             grouped = work.tile([P, N_TILE, PACK], BF16, tag="grouped", bufs=3, align_bytes=64)
             nc.gpsimd.tensor_scalar(
                 out=grouped[:],
-                in0=raw[:, :, cols].rearrange("p t c -> p c t"),
+                in0=k_first_raw[r][:, :, cols].rearrange("p t c -> p c t"),
                 scalar1=1.0,
                 scalar2=0.0,
                 op0=ALU.mult,
                 op1=ALU.add,
             )
             nc.vector.quantize_mx(
-                out=codes.bitcast(FP8X4), scales=scales, in_=grouped[:].rearrange("p c t -> p (c t)")
+                out=k_first_codes[:, r, cols].bitcast(FP8X4),
+                scales=k_first_scales[:, r, cols],
+                in_=grouped[:].rearrange("p c t -> p (c t)"),
             )
-
-        xk_raw = []
-        xq_raw = []
-        w_raw = []
-
-        def load_heads(g):
-            cols = slice(g * K_PASS, (g + 1) * K_PASS)
-            k_tile = work.tile([P, SEQ_TILES, K_PASS], BF16, tag="xk_raw", bufs=2, name="xk_raw%d" % g)
-            nc.sync.dma_start(out=k_tile[:], in_=xk_rows[:, :, cols])
-            xk_raw.append(k_tile)
-            q_tile = work.tile([P, SEQ_TILES, K_PASS], BF16, tag="xq_raw", bufs=2, name="xq_raw%d" % g)
-            nc.sync.dma_start(out=q_tile[:], in_=xq_rows[:, :, cols])
-            xq_raw.append(q_tile)
-
-        def load_weights(g):
-            w_tile = work.tile([P, PACK, N_OUT], BF16, tag="raw", bufs=3, name="w_raw%d" % g)
-            nc.sync.dma_start(out=w_tile[:].rearrange("p (u e) n -> p u e n", e=2), in_=w_rows[g])
-            w_raw.append(w_tile)
-
-        load_heads(0)
-        xv_raw = work.tile([P, PACK, FEATURES], BF16, tag="raw", bufs=3)
-        nc.sync.dma_start(out=xv_raw[:].rearrange("p (u e) f -> p u e f", e=2), in_=xv_rows)
-        load_heads(1)
-        load_weights(0)
-        load_heads(2)
-        load_weights(1)
-        load_heads(3)
-        load_weights(2)
-        load_weights(3)
-
-        v_codes = keep.tile([P, FEATURES], U32, align_bytes=64)
-        v_scales = keep.tile([P, FEATURES], U8, align_bytes=64)
-        for g in range(GROUPS):
-            cols = slice(g * N_TILE, (g + 1) * N_TILE)
-            quantise_columns(xv_raw, cols, v_codes[:, cols], v_scales[:, cols])
-
-        w_codes = keep.tile([P, GROUPS, N_OUT], U32, align_bytes=64)
-        w_scales = keep.tile([P, GROUPS, N_OUT], U8, align_bytes=64)
-
-        qk_t = keep.tile([P, HEADS, 2 * SEQ], BF16)
 
         def transpose_head(h):
             g, a = divmod(h, GROUP_HEADS)
@@ -138,17 +147,136 @@ def tile_mptattentionfused_pa_kernel(tc, xq, xk, xv, mask, w_out, out):
                 nc.tensor.transpose(qk_ps[:, SEQ_TILES + t, :], xq_raw[g][:, t, cols], ident_bf[:])
             nc.scalar.copy(out=qk_t[:, h, :], in_=qk_ps[:].rearrange("p a i -> p (a i)"))
 
-        def to_mx_rows(words_ps, codes, scales, tag):
-            grouped = work.tile([P, BLOCK_TILES, P, PACK], BF16, tag=tag, bufs=2, align_bytes=64)
-            flat = grouped[:].rearrange("p q i t -> p (q i t)")
+        def build_bias(n):
+            blk, h = divmod(n, HEADS)
+            bias_t = work.tile([P, SEQ_TILES, BLOCK], F32, tag="bias_t", bufs=3)
+            for t in range(SEQ_TILES):
+                nc.vector.tensor_scalar_add(
+                    out=bias_t[:, t, :],
+                    in0=mask_t[:, t, blk * BLOCK : (blk + 1) * BLOCK],
+                    scalar1=alibi[:, h, t : t + 1],
+                )
+            bias_of[n] = bias_t
+
+        def scores(n):
+            blk, h = divmod(n, HEADS)
+            scores_of[n] = []
+            for q in range(BLOCK_TILES):
+                it = blk * BLOCK_TILES + q
+                s_ps = psum.tile([P, SEQ], F32, tag="s", bufs=5)
+                nc.tensor.matmul(
+                    out=s_ps[:],
+                    lhsT=qk_t[:, h, SEQ + it * P : SEQ + (it + 1) * P],
+                    rhs=qk_t[:, h, 0:SEQ],
+                    start=True,
+                    stop=False,
+                )
+                for t in range(SEQ_TILES):
+                    nc.tensor.matmul(
+                        out=s_ps[:, t * P : (t + 1) * P],
+                        lhsT=bias_of[n][:, t, q * P : (q + 1) * P],
+                        rhs=ident_f[:],
+                        is_transpose=True,
+                        start=False,
+                        stop=(t == SEQ_TILES - 1),
+                    )
+                scores_of[n].append(s_ps)
+
+        def softmax(n):
+            b = n % 2
+            if b == 0:
+                sums_of[n // 2] = work.tile([P, BLOCK_TILES, 2], F32, tag="row_sum", bufs=3, name="row_sum")
+            e_of[n] = []
+            for q in range(BLOCK_TILES):
+                s_ps = scores_of[n][q]
+                row_max = work.tile([P, 1], F32, tag="row_max", bufs=4)
+                nc.vector.tensor_reduce(out=row_max[:], in_=s_ps[:], axis=AXIS.X, op=ALU.max)
+                shift = work.tile([P, 1], F32, tag="shift", bufs=4)
+                nc.vector.tensor_scalar_mul(out=shift[:], in0=row_max[:], scalar1=-1.0 / SQRT_DIM)
+                e_sb = work.tile([P, SEQ], BF16, tag="e_sb", bufs=4)
+                nc.scalar.activation(
+                    out=e_sb[:],
+                    in_=s_ps[:],
+                    func=ACT.Exp,
+                    bias=shift[:],
+                    scale=1.0 / SQRT_DIM,
+                    accum_out=sums_of[n // 2][:, q, b : b + 1],
+                )
+                e_of[n].append(e_sb)
+
+        def rows_to_partitions(rows_of_tile, tag):
+            words_ps = psum.tile([P, BLOCK_TILES, 2, P], F32, tag="tr", bufs=2)
+            for q in range(BLOCK_TILES):
+                for u in range(2):
+                    nc.tensor.transpose(
+                        words_ps[:, q, u, :],
+                        rows_of_tile[q].bitcast(F32)[:, u * P : (u + 1) * P],
+                        ident_f[:],
+                    )
+            grouped = work.tile([P, BLOCK_TILES * P * PACK], BF16, tag=tag, bufs=2, align_bytes=64)
             nc.scalar.copy(
-                out=flat.bitcast(F32).rearrange("p (q i u) -> p q i u", q=BLOCK_TILES, u=2),
+                out=grouped[:].bitcast(F32).rearrange("p (q i u) -> p q i u", q=BLOCK_TILES, u=2),
                 in_=words_ps[:].rearrange("p q u i -> p q i u"),
             )
-            nc.vector.quantize_mx(out=codes.bitcast(FP8X4), scales=scales, in_=flat)
+            return grouped
 
-        def project(o_codes, o_scales, blk, q, n):
-            acc = psum.tile([P, N_TILE], F32, tag="acc", bufs=2)
+        def quantise_e(n):
+            e_codes = work.tile([P, BLOCK], U32, tag="e_codes", bufs=2, align_bytes=64)
+            e_scales = work.tile([P, BLOCK], U8, tag="e_scales", bufs=2, align_bytes=64)
+            nc.vector.quantize_mx(out=e_codes[:].bitcast(FP8X4), scales=e_scales[:], in_=e_grouped_of[n][:])
+            e_mx_of[n] = (e_codes, e_scales)
+
+        def weighted_values(n):
+            h = n % HEADS
+            a = h % GROUP_HEADS
+            pair, b = divmod(a, 2)
+            if b == 0:
+                pv_of[n // 2] = psum.tile([P, BLOCK_TILES, 2, HEAD_DIM], F32, tag="pv", bufs=1, name="pv_ps")
+            if a == 0:
+                o_of[n // GROUP_HEADS] = work.tile([P, BLOCK_TILES, K_PASS], BF16, tag="o_sb", bufs=2, name="o_sb")
+            pv_ps = pv_of[n // 2]
+            e_codes, e_scales = e_mx_of[n]
+            cols = slice(h * HEAD_DIM, (h + 1) * HEAD_DIM)
+            for q in range(BLOCK_TILES):
+                rows = slice(q * P, (q + 1) * P)
+                nc.tensor.matmul_mx(
+                    out=pv_ps[:, q, b, :],
+                    lhsT=e_codes[:, rows].bitcast(FP8X4),
+                    lhsT_scale=e_scales[:, rows],
+                    rhs=k_first_codes[:, 0, cols].bitcast(FP8X4),
+                    rhs_scale=k_first_scales[:, 0, cols],
+                    start=True,
+                    stop=True,
+                )
+            if b == 1:
+                inv_sum = work.tile([P, BLOCK_TILES, 2], F32, tag="inv_sum", bufs=2)
+                nc.vector.reciprocal(out=inv_sum[:], in_=sums_of[n // 2][:])
+                o_sb = o_of[n // GROUP_HEADS]
+                nc.vector.tensor_tensor(
+                    out=o_sb[:, :, pair * 2 * HEAD_DIM : (pair + 1) * 2 * HEAD_DIM].rearrange(
+                        "p q (b d) -> p q b d", b=2
+                    ),
+                    in0=pv_ps[:],
+                    in1=inv_sum[:].unsqueeze(3).to_broadcast([P, BLOCK_TILES, 2, HEAD_DIM]),
+                    op=ALU.mult,
+                )
+
+        def quantise_o(n):
+            blk, h = divmod(n, HEADS)
+            g = h // GROUP_HEADS
+            if g == 0:
+                o_codes = work.tile([P, GROUPS, BLOCK], U32, tag="o_codes", bufs=2, align_bytes=64)
+                o_scales = work.tile([P, GROUPS, BLOCK], U8, tag="o_scales", bufs=2, align_bytes=64)
+                o_mx_of[blk] = (o_codes, o_scales)
+            o_codes, o_scales = o_mx_of[blk]
+            nc.vector.quantize_mx(
+                out=o_codes[:, g, :].bitcast(FP8X4), scales=o_scales[:, g, :], in_=o_grouped_of[n][:]
+            )
+
+        def project(blk, tile_index, copy):
+            q, n = divmod(tile_index, N_TILES)
+            o_codes, o_scales = o_mx_of[blk]
+            acc = psum.tile([P, N_TILE], F32, tag="s", bufs=5)
             rows = slice(q * P, (q + 1) * P)
             cols = slice(n * N_TILE, (n + 1) * N_TILE)
             for g in range(GROUPS):
@@ -156,123 +284,47 @@ def tile_mptattentionfused_pa_kernel(tc, xq, xk, xv, mask, w_out, out):
                     out=acc[:],
                     lhsT=o_codes[:, g, rows].bitcast(FP8X4),
                     lhsT_scale=o_scales[:, g, rows],
-                    rhs=w_codes[:, g, cols].bitcast(FP8X4),
-                    rhs_scale=w_scales[:, g, cols],
+                    rhs=k_first_codes[:, 1 + g, cols].bitcast(FP8X4),
+                    rhs_scale=k_first_scales[:, 1 + g, cols],
                     start=(g == 0),
                     stop=(g == GROUPS - 1),
                 )
             result = work.tile([P, N_TILE], F32, tag="result", bufs=3)
-            nc.scalar.copy(out=result[:], in_=acc[:])
+            copy(out=result[:], in_=acc[:])
             nc.sync.dma_start(out=out_rows[blk * BLOCK_TILES + q][:, cols], in_=result[:])
 
-        done = None
-        for blk in range(BLOCKS):
-            o_codes = work.tile([P, GROUPS, BLOCK], U32, tag="o_codes", bufs=2, align_bytes=64)
-            o_scales = work.tile([P, GROUPS, BLOCK], U8, tag="o_scales", bufs=2, align_bytes=64)
-            for h in range(HEADS):
-                g, a = divmod(h, GROUP_HEADS)
-                pair, b = divmod(a, 2)
-                if blk == 0:
-                    transpose_head(h)
+        K_FIRST_CHUNKS = (1 + GROUPS) * N_TILES
+        BLOCK_OUT_TILES = BLOCK_TILES * N_TILES
+        transpose_head(0)
+        transpose_head(1)
+        build_bias(0)
+        build_bias(1)
+        for i in range(UNITS + 3):
+            if 0 <= i - 1 < UNITS:
+                e_grouped_of[i - 1] = rows_to_partitions([e[:] for e in e_of[i - 1]], "e_grouped")
+            if i < UNITS:
+                scores(i)
+                softmax(i)
+            last_of_group = 0 <= i - 3 and (i - 3) % GROUP_HEADS == GROUP_HEADS - 1
+            if last_of_group:
+                o_sb = o_of[(i - 3) // GROUP_HEADS]
+                o_grouped_of[i - 3] = rows_to_partitions(
+                    [o_sb[:, q, :] for q in range(BLOCK_TILES)], "o_grouped"
+                )
+            if i + 2 < HEADS:
+                transpose_head(i + 2)
+            if i + 2 < UNITS:
+                build_bias(i + 2)
+            if 0 <= i - 2 < UNITS:
+                weighted_values(i - 2)
+            if 0 <= i - (HEADS + 3) < BLOCK_OUT_TILES:
+                project(0, i - (HEADS + 3), nc.scalar.copy)
+            if 0 <= i - 1 < K_FIRST_CHUNKS:
+                quantise_k_first(i - 1)
+            if 0 <= i - 1 < UNITS:
+                quantise_e(i - 1)
+            if last_of_group:
+                quantise_o(i - 3)
 
-                bias_t = work.tile([P, SEQ_TILES, BLOCK], F32, tag="bias_t", bufs=2)
-                for t in range(SEQ_TILES):
-                    nc.vector.tensor_scalar_add(
-                        out=bias_t[:, t, :],
-                        in0=mask_t[:, t, blk * BLOCK : (blk + 1) * BLOCK],
-                        scalar1=alibi[:, h, t : t + 1],
-                    )
-
-                if b == 0:
-                    row_sum = work.tile([P, BLOCK_TILES, 2], F32, tag="row_sum", bufs=2)
-                    pv_ps = psum.tile([P, BLOCK_TILES, 2, HEAD_DIM], F32, tag="pv", bufs=1)
-                if a == 0:
-                    o_sb = work.tile([P, BLOCK_TILES, K_PASS], BF16, tag="o_sb", bufs=2)
-
-                e_ps = psum.tile([P, BLOCK_TILES, 2, P], F32, tag="tr", bufs=2)
-                for q in range(BLOCK_TILES):
-                    it = blk * BLOCK_TILES + q
-                    s_ps = psum.tile([P, SEQ], F32, tag="s", bufs=3)
-                    nc.tensor.matmul(
-                        out=s_ps[:],
-                        lhsT=qk_t[:, h, SEQ + it * P : SEQ + (it + 1) * P],
-                        rhs=qk_t[:, h, 0:SEQ],
-                        start=True,
-                        stop=False,
-                    )
-                    for t in range(SEQ_TILES):
-                        nc.tensor.matmul(
-                            out=s_ps[:, t * P : (t + 1) * P],
-                            lhsT=bias_t[:, t, q * P : (q + 1) * P],
-                            rhs=ident_f[:],
-                            is_transpose=True,
-                            start=False,
-                            stop=(t == SEQ_TILES - 1),
-                        )
-                    row_max = work.tile([P, 1], F32, tag="row_max", bufs=4)
-                    nc.vector.tensor_reduce(out=row_max[:], in_=s_ps[:], axis=AXIS.X, op=ALU.max)
-                    shift = work.tile([P, 1], F32, tag="shift", bufs=4)
-                    nc.vector.tensor_scalar_mul(out=shift[:], in0=row_max[:], scalar1=-1.0 / SQRT_DIM)
-                    e_sb = work.tile([P, SEQ], BF16, tag="e_sb", bufs=4)
-                    nc.scalar.activation(
-                        out=e_sb[:],
-                        in_=s_ps[:],
-                        func=ACT.Exp,
-                        bias=shift[:],
-                        scale=1.0 / SQRT_DIM,
-                        accum_out=row_sum[:, q, b : b + 1],
-                    )
-                    for u in range(2):
-                        nc.tensor.transpose(
-                            e_ps[:, q, u, :], e_sb[:].bitcast(F32)[:, u * P : (u + 1) * P], ident_f[:]
-                        )
-
-                e_codes = work.tile([P, BLOCK], U32, tag="e_codes", bufs=2, align_bytes=64)
-                e_scales = work.tile([P, BLOCK], U8, tag="e_scales", bufs=2, align_bytes=64)
-                to_mx_rows(e_ps, e_codes[:], e_scales[:], "e_grouped")
-                for q in range(BLOCK_TILES):
-                    rows = slice(q * P, (q + 1) * P)
-                    cols = slice(h * HEAD_DIM, (h + 1) * HEAD_DIM)
-                    nc.tensor.matmul_mx(
-                        out=pv_ps[:, q, b, :],
-                        lhsT=e_codes[:, rows].bitcast(FP8X4),
-                        lhsT_scale=e_scales[:, rows],
-                        rhs=v_codes[:, cols].bitcast(FP8X4),
-                        rhs_scale=v_scales[:, cols],
-                        start=True,
-                        stop=True,
-                    )
-
-                if b == 1:
-                    inv_sum = work.tile([P, BLOCK_TILES, 2], F32, tag="inv_sum", bufs=2)
-                    nc.vector.reciprocal(out=inv_sum[:], in_=row_sum[:])
-                    nc.vector.tensor_tensor(
-                        out=o_sb[:, :, pair * 2 * HEAD_DIM : (pair + 1) * 2 * HEAD_DIM].rearrange(
-                            "p q (b d) -> p q b d", b=2
-                        ),
-                        in0=pv_ps[:],
-                        in1=inv_sum[:].unsqueeze(3).to_broadcast([P, BLOCK_TILES, 2, HEAD_DIM]),
-                        op=ALU.mult,
-                    )
-
-                if a == GROUP_HEADS - 1:
-                    o_ps = psum.tile([P, BLOCK_TILES, 2, P], F32, tag="tr", bufs=2)
-                    for q in range(BLOCK_TILES):
-                        for u in range(2):
-                            nc.tensor.transpose(
-                                o_ps[:, q, u, :],
-                                o_sb[:, q, :].bitcast(F32)[:, u * P : (u + 1) * P],
-                                ident_f[:],
-                            )
-                    to_mx_rows(o_ps, o_codes[:, g, :], o_scales[:, g, :], "o_grouped")
-
-                if blk == 0:
-                    cols = slice(a * N_TILE, (a + 1) * N_TILE)
-                    quantise_columns(w_raw[g], cols, w_codes[:, g, cols], w_scales[:, g, cols])
-                elif h < BLOCK_TILES * N_TILES:
-                    project(done[0], done[1], blk - 1, h // N_TILES, h % N_TILES)
-            done = (o_codes, o_scales)
-
-        for q in range(BLOCK_TILES):
-            for n in range(N_TILES):
-                project(done[0], done[1], BLOCKS - 1, q, n)
+        for tile_index in range(BLOCK_OUT_TILES):
+            project(1, tile_index, nc.scalar.copy if tile_index % 2 == 0 else nc.vector.tensor_copy)

@@ -185,7 +185,7 @@ def tile_mptattentionfused_pa_kernel(tc, xq, xk, xv, mask, w_out, out):
         def softmax(n):
             b = n % 2
             if b == 0:
-                sums_of[n // 2] = work.tile([P, BLOCK_TILES, 2], F32, tag="row_sum", bufs=3, name="row_sum")
+                sums_of[n // 2] = work.tile([P, BLOCK_TILES, 2], F32, tag="row_sum", bufs=4, name="row_sum")
             e_of[n] = []
             for q in range(BLOCK_TILES):
                 s_ps = scores_of[n][q]
@@ -193,7 +193,7 @@ def tile_mptattentionfused_pa_kernel(tc, xq, xk, xv, mask, w_out, out):
                 nc.vector.tensor_reduce(out=row_max[:], in_=s_ps[:], axis=AXIS.X, op=ALU.max)
                 shift = work.tile([P, 1], F32, tag="shift", bufs=4)
                 nc.vector.tensor_scalar_mul(out=shift[:], in0=row_max[:], scalar1=-1.0 / SQRT_DIM)
-                e_sb = work.tile([P, SEQ], BF16, tag="e_sb", bufs=4)
+                e_sb = work.tile([P, SEQ], BF16, tag="e_sb", bufs=6)
                 nc.scalar.activation(
                     out=e_sb[:],
                     in_=s_ps[:],
@@ -299,32 +299,32 @@ def tile_mptattentionfused_pa_kernel(tc, xq, xk, xv, mask, w_out, out):
         transpose_head(1)
         build_bias(0)
         build_bias(1)
-        for i in range(UNITS + 3):
-            if 0 <= i - 1 < UNITS:
-                e_grouped_of[i - 1] = rows_to_partitions([e[:] for e in e_of[i - 1]], "e_grouped")
+        for i in range(UNITS + 4):
+            if 0 <= i - 2 < UNITS:
+                e_grouped_of[i - 2] = rows_to_partitions([e[:] for e in e_of[i - 2]], "e_grouped")
             if i < UNITS:
                 scores(i)
                 softmax(i)
-            last_of_group = 0 <= i - 3 and (i - 3) % GROUP_HEADS == GROUP_HEADS - 1
+            last_of_group = 0 <= i - 4 and (i - 4) % GROUP_HEADS == GROUP_HEADS - 1
             if last_of_group:
-                o_sb = o_of[(i - 3) // GROUP_HEADS]
-                o_grouped_of[i - 3] = rows_to_partitions(
+                o_sb = o_of[(i - 4) // GROUP_HEADS]
+                o_grouped_of[i - 4] = rows_to_partitions(
                     [o_sb[:, q, :] for q in range(BLOCK_TILES)], "o_grouped"
                 )
             if i + 2 < HEADS:
                 transpose_head(i + 2)
             if i + 2 < UNITS:
                 build_bias(i + 2)
-            if 0 <= i - 2 < UNITS:
-                weighted_values(i - 2)
-            if 0 <= i - (HEADS + 3) < BLOCK_OUT_TILES:
-                project(0, i - (HEADS + 3), nc.scalar.copy)
+            if 0 <= i - 3 < UNITS:
+                weighted_values(i - 3)
+            if 0 <= i - (HEADS + 4) < BLOCK_OUT_TILES:
+                project(0, i - (HEADS + 4), nc.scalar.copy)
             if 0 <= i - 1 < K_FIRST_CHUNKS:
                 quantise_k_first(i - 1)
-            if 0 <= i - 1 < UNITS:
-                quantise_e(i - 1)
+            if 0 <= i - 2 < UNITS:
+                quantise_e(i - 2)
             if last_of_group:
-                quantise_o(i - 3)
+                quantise_o(i - 4)
 
         for tile_index in range(BLOCK_OUT_TILES):
             project(1, tile_index, nc.scalar.copy if tile_index % 2 == 0 else nc.vector.tensor_copy)

@@ -59,25 +59,25 @@ def tile_mptattentionfused_pa_kernel(tc, xq, xk, xv, mask, w_out, out):
 
         def load_heads(g):
             cols = slice(g * K_PASS, (g + 1) * K_PASS)
-            k_tile = work.tile([P, SEQ_TILES, K_PASS], BF16, tag="xk_raw", bufs=2, name="xk_raw%d" % g)
+            k_tile = work.tile([P, SEQ_TILES, K_PASS], BF16, tag="xk_raw", bufs=3, name="xk_raw%d" % g)
             nc.sync.dma_start(out=k_tile[:], in_=xk_rows[:, :, cols])
             xk_raw.append(k_tile)
-            q_tile = work.tile([P, SEQ_TILES, K_PASS], BF16, tag="xq_raw", bufs=2, name="xq_raw%d" % g)
+            q_tile = work.tile([P, SEQ_TILES, K_PASS], BF16, tag="xq_raw", bufs=3, name="xq_raw%d" % g)
             nc.sync.dma_start(out=q_tile[:], in_=xq_rows[:, :, cols])
             xq_raw.append(q_tile)
 
         def load_k_first(rows, name):
-            raw = work.tile([P, PACK, N_OUT], BF16, tag="raw", bufs=3, name=name)
+            raw = work.tile([P, PACK, N_OUT], BF16, tag="raw", bufs=2, name=name)
             nc.sync.dma_start(out=raw[:].rearrange("p (u e) n -> p u e n", e=2), in_=rows)
             k_first_raw.append(raw)
 
         load_heads(0)
         load_k_first(xv_rows, "xv_raw")
         load_heads(1)
-        load_k_first(w_rows[0], "w_raw0")
         load_heads(2)
-        load_k_first(w_rows[1], "w_raw1")
+        load_k_first(w_rows[0], "w_raw0")
         load_heads(3)
+        load_k_first(w_rows[1], "w_raw1")
         load_k_first(w_rows[2], "w_raw2")
         load_k_first(w_rows[3], "w_raw3")
 
@@ -97,7 +97,7 @@ def tile_mptattentionfused_pa_kernel(tc, xq, xk, xv, mask, w_out, out):
 
         mask_t = keep.tile([P, SEQ_TILES, SEQ], F32)
         for t in range(SEQ_TILES):
-            mask_ps = psum.tile([P, SEQ_TILES, P], BF16, tag="tr", bufs=2)
+            mask_ps = psum.tile([P, SEQ_TILES, P], BF16, tag="tr", bufs=3)
             for it in range(SEQ_TILES):
                 nc.tensor.transpose(mask_ps[:, it, :], mask_sb[:, it, t * P : (t + 1) * P], ident_bf[:])
             nc.scalar.mul(
@@ -140,7 +140,7 @@ def tile_mptattentionfused_pa_kernel(tc, xq, xk, xv, mask, w_out, out):
         def transpose_head(h):
             g, a = divmod(h, GROUP_HEADS)
             cols = slice(a * HEAD_DIM, (a + 1) * HEAD_DIM)
-            qk_ps = psum.tile([P, 2 * SEQ_TILES, P], BF16, tag="tr", bufs=2)
+            qk_ps = psum.tile([P, 2 * SEQ_TILES, P], BF16, tag="tr", bufs=3)
             for t in range(SEQ_TILES):
                 nc.tensor.transpose(qk_ps[:, t, :], xk_raw[g][:, t, cols], ident_bf[:])
             for t in range(SEQ_TILES):
@@ -163,7 +163,7 @@ def tile_mptattentionfused_pa_kernel(tc, xq, xk, xv, mask, w_out, out):
             scores_of[n] = []
             for q in range(BLOCK_TILES):
                 it = blk * BLOCK_TILES + q
-                s_ps = psum.tile([P, SEQ], F32, tag="s", bufs=5)
+                s_ps = psum.tile([P, SEQ], F32, tag="s", bufs=4)
                 nc.tensor.matmul(
                     out=s_ps[:],
                     lhsT=qk_t[:, h, SEQ + it * P : SEQ + (it + 1) * P],
@@ -205,7 +205,7 @@ def tile_mptattentionfused_pa_kernel(tc, xq, xk, xv, mask, w_out, out):
                 e_of[n].append(e_sb)
 
         def rows_to_partitions(rows_of_tile, tag):
-            words_ps = psum.tile([P, BLOCK_TILES, 2, P], F32, tag="tr", bufs=2)
+            words_ps = psum.tile([P, BLOCK_TILES, 2, P], F32, tag="tr", bufs=3)
             for q in range(BLOCK_TILES):
                 for u in range(2):
                     nc.tensor.transpose(
@@ -276,7 +276,7 @@ def tile_mptattentionfused_pa_kernel(tc, xq, xk, xv, mask, w_out, out):
         def project(blk, tile_index, copy):
             q, n = divmod(tile_index, N_TILES)
             o_codes, o_scales = o_mx_of[blk]
-            acc = psum.tile([P, N_TILE], F32, tag="s", bufs=5)
+            acc = psum.tile([P, N_TILE], F32, tag="s", bufs=4)
             rows = slice(q * P, (q + 1) * P)
             cols = slice(n * N_TILE, (n + 1) * N_TILE)
             for g in range(GROUPS):
@@ -289,12 +289,14 @@ def tile_mptattentionfused_pa_kernel(tc, xq, xk, xv, mask, w_out, out):
                     start=(g == 0),
                     stop=(g == GROUPS - 1),
                 )
-            result = work.tile([P, N_TILE], F32, tag="result", bufs=3)
+            result = work.tile([P, N_TILE], F32, tag="result", bufs=8)
             copy(out=result[:], in_=acc[:])
             nc.sync.dma_start(out=out_rows[blk * BLOCK_TILES + q][:, cols], in_=result[:])
 
         K_FIRST_CHUNKS = (1 + GROUPS) * N_TILES
         BLOCK_OUT_TILES = BLOCK_TILES * N_TILES
+        FIRST_PROJECTION = 26
+        next_chunk = 0
         transpose_head(0)
         transpose_head(1)
         build_bias(0)
@@ -317,10 +319,11 @@ def tile_mptattentionfused_pa_kernel(tc, xq, xk, xv, mask, w_out, out):
                 build_bias(i + 2)
             if 0 <= i - 3 < UNITS:
                 weighted_values(i - 3)
-            if 0 <= i - (HEADS + 4) < BLOCK_OUT_TILES:
-                project(0, i - (HEADS + 4), nc.scalar.copy)
-            if 0 <= i - 1 < K_FIRST_CHUNKS:
-                quantise_k_first(i - 1)
+            if 0 <= i - FIRST_PROJECTION < BLOCK_OUT_TILES:
+                project(0, i - FIRST_PROJECTION, nc.scalar.copy)
+            if i >= 2 and i % 4 != 3 and next_chunk < K_FIRST_CHUNKS:
+                quantise_k_first(next_chunk)
+                next_chunk += 1
             if 0 <= i - 2 < UNITS:
                 quantise_e(i - 2)
             if last_of_group:

@@ -22,16 +22,23 @@ HEADS = 16
 HEAD_DIM = 128
 FEATURES = HEADS * HEAD_DIM
 N_OUT = 2048
-SEQ_TILES = SEQ // P
+TILES = SEQ // P
 GROUP_HEADS = K_PASS // HEAD_DIM
 GROUPS = HEADS // GROUP_HEADS
-BLOCK_TILES = 2
-BLOCK = BLOCK_TILES * P
-BLOCKS = SEQ // BLOCK
+PAIR = 2
+PAIRS = HEADS // PAIR
+UNITS = TILES * PAIRS
+HALF_UNITS = 4
+HALF_HEADS = HALF_UNITS * PAIR
+HALF_GROUPS = HALF_HEADS // GROUP_HEADS
 N_TILE = 512
 N_TILES = N_OUT // N_TILE
-UNITS = BLOCKS * HEADS
 SQRT_DIM = math.sqrt(HEAD_DIM)
+PRODUCT_UNITS = 16
+GROUPED_BUFS = {"gpsimd": 1, "vector": 2, "scalar": 3}
+WIDTH = {"gpsimd": 256, "vector": 128, "scalar": 128}
+ENGINE_ROUNDS = (("vector", 0, 20), ("gpsimd", 0, 40), ("scalar", 0, 40))
+BROADCAST_UNITS = 8
 
 FLOPS = 2 * 2 * HEADS * SEQ * SEQ * HEAD_DIM + 2 * SEQ * FEATURES * N_OUT
 
@@ -51,196 +58,310 @@ def tile_mptattentionfused_pa_kernel(tc, xq, xk, xv, mask, w_out, out):
         psum = stack.enter_context(tc.psum_pool(name="psum", bufs=1))
         stack.enter_context(tc.manual_schedule())
 
-        mask_sb = work.tile([P, SEQ_TILES, SEQ], BF16, bufs=1)
-        nc.sync.dma_start(out=mask_sb[:], in_=mask_rows)
-        xk_raw = []
-        xq_raw = []
+        mask_sb = keep.tile([P, TILES, SEQ], BF16)
+        k_raw = []
+        q_raw = {}
         k_first_raw = []
 
-        def load_heads(g):
-            cols = slice(g * K_PASS, (g + 1) * K_PASS)
-            k_tile = work.tile([P, SEQ_TILES, K_PASS], BF16, tag="xk_raw", bufs=3, name="xk_raw%d" % g)
-            nc.sync.dma_start(out=k_tile[:], in_=xk_rows[:, :, cols])
-            xk_raw.append(k_tile)
-            q_tile = work.tile([P, SEQ_TILES, K_PASS], BF16, tag="xq_raw", bufs=3, name="xq_raw%d" % g)
-            nc.sync.dma_start(out=q_tile[:], in_=xq_rows[:, :, cols])
-            xq_raw.append(q_tile)
+        def load_k(g):
+            tile = work.tile([P, TILES, K_PASS], BF16, tag="k_raw", bufs=3, name="k_raw%d" % g)
+            nc.sync.dma_start(out=tile[:], in_=xk_rows[:, :, g * K_PASS : (g + 1) * K_PASS])
+            k_raw.append(tile)
 
-        def load_k_first(rows, name):
-            raw = work.tile([P, PACK, N_OUT], BF16, tag="raw", bufs=2, name=name)
-            nc.sync.dma_start(out=raw[:].rearrange("p (u e) n -> p u e n", e=2), in_=rows)
+        def load_q(j):
+            it, half = divmod(j, 2)
+            width = HALF_HEADS * HEAD_DIM
+            tile = work.tile([P, width], BF16, tag="q_raw", bufs=4, name="q_raw%d" % j)
+            nc.sync.dma_start(out=tile[:], in_=xq_rows[:, it, half * width : (half + 1) * width])
+            q_raw[j] = tile
+
+        def load_chunk(rows, name):
+            raw = work.tile([P, PACK, N_TILE], BF16, tag="raw", bufs=8, name=name)
+            for u in range(2):
+                nc.sync.dma_start(out=raw[:, 2 * u : 2 * u + 2, :], in_=rows[:, u, :, :])
             k_first_raw.append(raw)
 
-        load_heads(0)
-        load_k_first(xv_rows, "xv_raw")
-        load_heads(1)
-        load_heads(2)
-        load_k_first(w_rows[0], "w_raw0")
-        load_heads(3)
-        load_k_first(w_rows[1], "w_raw1")
-        load_k_first(w_rows[2], "w_raw2")
-        load_k_first(w_rows[3], "w_raw3")
+        def load_xv(c):
+            load_chunk(xv_rows[:, :, :, c * N_TILE : (c + 1) * N_TILE], "xv_raw%d" % c)
+
+        nc.sync.dma_start(out=mask_sb[:, 0, :], in_=mask_rows[:, 0, :])
+        load_k(0)
+        load_q(0)
+        load_xv(0)
+        load_k(1)
+        load_xv(1)
+        load_q(1)
+        load_k(2)
+        load_xv(2)
+        load_k(3)
+        load_xv(3)
+        nc.sync.dma_start(out=mask_sb[:, 1:TILES, :], in_=mask_rows[:, 1:TILES, :])
+        load_q(2)
+        load_q(3)
+        for n in range(N_TILES):
+            for g in range(GROUPS):
+                load_chunk(w_rows[g][:, :, :, n * N_TILE : (n + 1) * N_TILE], "w_raw%d_%d" % (n, g))
+            load_q(4 + n)
 
         ident_bf = keep.tile([P, P], BF16)
         make_identity(nc, ident_bf[:])
         ident_f = keep.tile([P, P], F32)
         make_identity(nc, ident_f[:])
+        ones = keep.tile([P, 1], F32)
+        nc.gpsimd.memset(ones[:], 1.0)
 
-        key_dist_i = keep.tile([P, SEQ_TILES], I32)
-        nc.gpsimd.iota(key_dist_i[:], pattern=[[P, SEQ_TILES]], base=1 - SEQ, channel_multiplier=1)
-        key_dist = keep.tile([P, SEQ_TILES], F32)
-        nc.vector.tensor_copy(out=key_dist[:], in_=key_dist_i[:])
-        alibi = keep.tile([P, HEADS, SEQ_TILES], F32)
+        amp = keep.tile([P, HEADS], F32)
         for h in range(HEADS):
-            slope = 2.0 ** (-(h + 1) / 2)
-            nc.vector.tensor_scalar_mul(out=alibi[:, h, :], in0=key_dist[:], scalar1=slope * SQRT_DIM)
+            nc.scalar.mul(out=amp[:, h : h + 1], in_=ones[:], mul=2.0 ** (-(h + 1) / 2) * SQRT_DIM)
 
-        mask_t = keep.tile([P, SEQ_TILES, SEQ], F32)
-        for t in range(SEQ_TILES):
-            mask_ps = psum.tile([P, SEQ_TILES, P], BF16, tag="tr", bufs=3)
-            for it in range(SEQ_TILES):
-                nc.tensor.transpose(mask_ps[:, it, :], mask_sb[:, it, t * P : (t + 1) * P], ident_bf[:])
-            nc.scalar.mul(
-                out=mask_t[:, t, :], in_=mask_ps[:].rearrange("p a i -> p (a i)"), mul=SQRT_DIM
+        key_dist_i = keep.tile([P, TILES], I32)
+        nc.gpsimd.iota(key_dist_i[:], pattern=[[P, TILES]], base=1 - SEQ, channel_multiplier=1)
+        key_dist = keep.tile([P, TILES], F32)
+        nc.vector.tensor_copy(out=key_dist[:], in_=key_dist_i[:])
+        dist_i = keep.tile([P, SEQ], I32)
+        nc.gpsimd.iota(dist_i[:], pattern=[[1, SEQ]], base=1 - SEQ, channel_multiplier=0)
+        part_i = keep.tile([P, 1], I32)
+        nc.gpsimd.iota(part_i[:], pattern=[[1, 1]], base=0, channel_multiplier=1)
+
+        dist = keep.tile([P, SEQ], F32)
+        nc.vector.tensor_copy(out=dist[:], in_=dist_i[:])
+        part = keep.tile([P, 1], F32)
+        nc.vector.tensor_copy(out=part[:], in_=part_i[:])
+        dist_bf = keep.tile([P, SEQ], BF16)
+        nc.vector.tensor_copy(out=dist_bf[:], in_=dist[:])
+        select = []
+        for m in range(3):
+            low = keep.tile([P, 1], F32, name="low%d" % m)
+            nc.vector.tensor_single_scalar(out=low[:], in_=part[:], scalar=float(m), op=ALU.is_equal)
+            select.append(low)
+        nc.vector.tensor_tensor(
+            out=dist_bf[64:P, :], in0=dist[64:P, :], in1=dist_bf[64:P, :], op=ALU.subtract
+        )
+        both = []
+        for m in range(3):
+            sel = keep.tile([P, 1], F32, name="sel%d" % m)
+            nc.vector.scalar_tensor_tensor(
+                out=sel[:], in0=part[:], scalar=float(64 + m), in1=select[m][:], op0=ALU.is_equal, op1=ALU.add
             )
+            both.append(sel)
+        amp_hi = keep.tile([P, HEADS], BF16)
+        nc.vector.tensor_copy(out=amp_hi[:], in_=amp[:])
+        amp_rest = keep.tile([P, HEADS], F32)
+        nc.vector.tensor_tensor(out=amp_rest[:], in0=amp[:], in1=amp_hi[:], op=ALU.subtract)
+        amp_mid = keep.tile([P, HEADS], BF16)
+        nc.vector.tensor_copy(out=amp_mid[:], in_=amp_rest[:])
+        amp_last = keep.tile([P, HEADS], F32)
+        nc.vector.tensor_tensor(out=amp_last[:], in0=amp_rest[:], in1=amp_mid[:], op=ALU.subtract)
+        coef_a = keep.tile([P, HEADS], F32)
+        nc.vector.tensor_scalar_mul(out=coef_a[:], in0=amp_hi[:], scalar1=both[0][:])
+        coef_b = keep.tile([P, HEADS], F32)
+        nc.vector.scalar_tensor_tensor(
+            out=coef_b[:], in0=amp_mid[:], scalar=both[1][:], in1=coef_a[:], op0=ALU.mult, op1=ALU.add
+        )
+        coef = keep.tile([P, HEADS], BF16)
+        nc.vector.scalar_tensor_tensor(
+            out=coef[:], in0=amp_last[:], scalar=both[2][:], in1=coef_b[:], op0=ALU.mult, op1=ALU.add
+        )
+        alibi = keep.tile([P, HEADS, TILES], F32)
+        nc.vector.tensor_tensor(
+            out=alibi[:],
+            in0=amp[:].unsqueeze(2).to_broadcast([P, HEADS, TILES]),
+            in1=key_dist[:].unsqueeze(1).to_broadcast([P, HEADS, TILES]),
+            op=ALU.mult,
+        )
 
         k_first_codes = keep.tile([P, 1 + GROUPS, N_OUT], U32, align_bytes=64)
         k_first_scales = keep.tile([P, 1 + GROUPS, N_OUT], U8, align_bytes=64)
-        qk_t = keep.tile([P, HEADS, 2 * SEQ], BF16)
+        k_t = keep.tile([P, HEADS, SEQ], BF16)
+        mask_t = keep.tile([P, TILES, TILES, P], F32)
 
+        grouped_of = {}
+        q_t_of = {}
         bias_of = {}
         scores_of = {}
+        row_max_of = {}
+        shift_of = {}
         e_of = {}
         e_grouped_of = {}
         e_mx_of = {}
         sums_of = {}
+        inv_of = {}
         pv_of = {}
         o_of = {}
         o_grouped_of = {}
         o_mx_of = {}
 
-        def quantise_k_first(c):
-            r, n = divmod(c, N_TILES)
-            cols = slice(n * N_TILE, (n + 1) * N_TILE)
-            grouped = work.tile([P, N_TILE, PACK], BF16, tag="grouped", bufs=3, align_bytes=64)
-            nc.gpsimd.tensor_scalar(
-                out=grouped[:],
-                in0=k_first_raw[r][:, :, cols].rearrange("p t c -> p c t"),
-                scalar1=1.0,
-                scalar2=0.0,
-                op0=ALU.mult,
-                op1=ALU.add,
+        def transpose_mask(it):
+            mask_ps = psum.tile([P, TILES, P], BF16, tag="tr", bufs=3, name="mask_ps")
+            for t in range(TILES):
+                nc.tensor.transpose(mask_ps[:, t, :], mask_sb[:, it, t * P : (t + 1) * P], ident_bf[:])
+            nc.scalar.mul(out=mask_t[:, it, :, :], in_=mask_ps[:], mul=SQRT_DIM)
+
+        def regroup(c, first, width, engine):
+            grouped = work.tile(
+                [P, width, PACK], BF16, tag="grouped_" + engine, bufs=GROUPED_BUFS[engine], align_bytes=64, name="grouped"
             )
+            rows = k_first_raw[c][:, :, first : first + width].rearrange("p t c -> p c t")
+            if engine == "gpsimd":
+                nc.gpsimd.tensor_scalar(
+                    out=grouped[:], in0=rows, scalar1=1.0, scalar2=0.0, op0=ALU.mult, op1=ALU.add
+                )
+            elif engine == "vector":
+                nc.vector.tensor_copy(out=grouped[:], in_=rows)
+            else:
+                nc.scalar.copy(out=grouped[:], in_=rows)
+            grouped_of[c, first] = grouped
+
+        def quantise_chunk(c, first, width):
+            if c < N_TILES:
+                r, n = 0, c
+            else:
+                n, g = divmod(c - N_TILES, GROUPS)
+                r = 1 + g
+            cols = slice(n * N_TILE + first, n * N_TILE + first + width)
             nc.vector.quantize_mx(
                 out=k_first_codes[:, r, cols].bitcast(FP8X4),
                 scales=k_first_scales[:, r, cols],
-                in_=grouped[:].rearrange("p c t -> p (c t)"),
+                in_=grouped_of[c, first][:].rearrange("p c t -> p (c t)"),
             )
 
-        def transpose_head(h):
-            g, a = divmod(h, GROUP_HEADS)
-            cols = slice(a * HEAD_DIM, (a + 1) * HEAD_DIM)
-            qk_ps = psum.tile([P, 2 * SEQ_TILES, P], BF16, tag="tr", bufs=3)
-            for t in range(SEQ_TILES):
-                nc.tensor.transpose(qk_ps[:, t, :], xk_raw[g][:, t, cols], ident_bf[:])
-            for t in range(SEQ_TILES):
-                nc.tensor.transpose(qk_ps[:, SEQ_TILES + t, :], xq_raw[g][:, t, cols], ident_bf[:])
-            nc.scalar.copy(out=qk_t[:, h, :], in_=qk_ps[:].rearrange("p a i -> p (a i)"))
+        def transpose_k(pair):
+            g, a = divmod(pair * PAIR, GROUP_HEADS)
+            k_ps = psum.tile([P, PAIR, TILES, P], BF16, tag="tr", bufs=3, name="k_ps")
+            for b in range(PAIR):
+                cols = slice((a + b) * HEAD_DIM, (a + b + 1) * HEAD_DIM)
+                for t in range(TILES):
+                    nc.tensor.transpose(k_ps[:, b, t, :], k_raw[g][:, t, cols], ident_bf[:])
+            nc.scalar.copy(
+                out=k_t[:, pair * PAIR : (pair + 1) * PAIR, :],
+                in_=k_ps[:].rearrange("p b t j -> p b (t j)"),
+            )
+
+        def transpose_q(j):
+            q_ps = psum.tile([P, HALF_HEADS, P], BF16, tag="tr", bufs=3, name="q_ps")
+            for a in range(HALF_HEADS):
+                nc.tensor.transpose(q_ps[:, a, :], q_raw[j][:, a * HEAD_DIM : (a + 1) * HEAD_DIM], ident_bf[:])
+            q_t = work.tile([P, HALF_HEADS, P], BF16, tag="q_t", bufs=3, name="q_t")
+            nc.scalar.copy(out=q_t[:], in_=q_ps[:])
+            q_t_of[j] = q_t
+
+        def bias_form(n, b):
+            if n < PRODUCT_UNITS and b == 0:
+                return "product"
+            return "broadcast" if n < BROADCAST_UNITS else "built"
 
         def build_bias(n):
-            blk, h = divmod(n, HEADS)
-            bias_t = work.tile([P, SEQ_TILES, BLOCK], F32, tag="bias_t", bufs=3)
-            for t in range(SEQ_TILES):
-                nc.vector.tensor_scalar_add(
-                    out=bias_t[:, t, :],
-                    in0=mask_t[:, t, blk * BLOCK : (blk + 1) * BLOCK],
-                    scalar1=alibi[:, h, t : t + 1],
-                )
-            bias_of[n] = bias_t
+            it, pair = divmod(n, PAIRS)
+            heads = [b for b in range(PAIR) if bias_form(n, b) == "built"]
+            if not heads:
+                return
+            bias_of[n] = work.tile([P, PAIR, TILES, P], F32, tag="bias_t", bufs=3, name="bias_t")
+            for b in heads:
+                for t in range(TILES):
+                    nc.vector.tensor_scalar_add(
+                        out=bias_of[n][:, b, t, :],
+                        in0=mask_t[:, it, t, :],
+                        scalar1=alibi[:, pair * PAIR + b, t : t + 1],
+                    )
 
         def scores(n):
-            blk, h = divmod(n, HEADS)
+            it, pair = divmod(n, PAIRS)
             scores_of[n] = []
-            for q in range(BLOCK_TILES):
-                it = blk * BLOCK_TILES + q
-                s_ps = psum.tile([P, SEQ], F32, tag="s", bufs=4)
+            for b in range(PAIR):
+                h = pair * PAIR + b
+                s_ps = psum.tile([P, SEQ], F32, tag="s", bufs=4, name="s_ps")
+                form = bias_form(n, b)
                 nc.tensor.matmul(
                     out=s_ps[:],
-                    lhsT=qk_t[:, h, SEQ + it * P : SEQ + (it + 1) * P],
-                    rhs=qk_t[:, h, 0:SEQ],
+                    lhsT=q_t_of[n // HALF_UNITS][:, h % HALF_HEADS, :],
+                    rhs=k_t[:, h, :],
                     start=True,
                     stop=False,
                 )
-                for t in range(SEQ_TILES):
+                if form == "product":
+                    nc.tensor.matmul(
+                        out=s_ps[:],
+                        lhsT=coef[:, h : h + 1].to_broadcast([P, P]),
+                        rhs=dist_bf[:],
+                        start=False,
+                        stop=False,
+                    )
+                added = []
+                for t in range(TILES):
+                    if form == "broadcast":
+                        added.append((t, alibi[:, h, t : t + 1].to_broadcast([P, P])))
+                    added.append((t, bias_of[n][:, b, t, :] if form == "built" else mask_t[:, it, t, :]))
+                for m, (t, rows) in enumerate(added):
                     nc.tensor.matmul(
                         out=s_ps[:, t * P : (t + 1) * P],
-                        lhsT=bias_of[n][:, t, q * P : (q + 1) * P],
+                        lhsT=rows,
                         rhs=ident_f[:],
                         is_transpose=True,
                         start=False,
-                        stop=(t == SEQ_TILES - 1),
+                        stop=(m == len(added) - 1),
                     )
                 scores_of[n].append(s_ps)
 
-        def softmax(n):
-            b = n % 2
-            if b == 0:
-                sums_of[n // 2] = work.tile([P, BLOCK_TILES, 2], F32, tag="row_sum", bufs=4, name="row_sum")
+        def row_maxima(n):
+            row_max = work.tile([P, PAIR], F32, tag="row_max", bufs=3, name="row_max")
+            for b in range(PAIR):
+                nc.vector.tensor_reduce(out=row_max[:, b : b + 1], in_=scores_of[n][b][:], axis=AXIS.X, op=ALU.max)
+            row_max_of[n] = row_max
+
+        def shifts(n):
+            shift = work.tile([P, PAIR], F32, tag="shift", bufs=3, name="shift")
+            nc.vector.tensor_scalar_mul(out=shift[:], in0=row_max_of[n][:], scalar1=-1.0 / SQRT_DIM)
+            shift_of[n] = shift
+
+        def exponentials(n):
+            sums_of[n] = work.tile([P, PAIR], F32, tag="row_sum", bufs=6, name="row_sum")
             e_of[n] = []
-            for q in range(BLOCK_TILES):
-                s_ps = scores_of[n][q]
-                row_max = work.tile([P, 1], F32, tag="row_max", bufs=4)
-                nc.vector.tensor_reduce(out=row_max[:], in_=s_ps[:], axis=AXIS.X, op=ALU.max)
-                shift = work.tile([P, 1], F32, tag="shift", bufs=4)
-                nc.vector.tensor_scalar_mul(out=shift[:], in0=row_max[:], scalar1=-1.0 / SQRT_DIM)
-                e_sb = work.tile([P, SEQ], BF16, tag="e_sb", bufs=6)
+            for b in range(PAIR):
+                e_sb = work.tile([P, SEQ], BF16, tag="e_sb", bufs=6, name="e_sb")
                 nc.scalar.activation(
                     out=e_sb[:],
-                    in_=s_ps[:],
+                    in_=scores_of[n][b][:],
                     func=ACT.Exp,
-                    bias=shift[:],
+                    bias=shift_of[n][:, b : b + 1],
                     scale=1.0 / SQRT_DIM,
-                    accum_out=sums_of[n // 2][:, q, b : b + 1],
+                    accum_out=sums_of[n][:, b : b + 1],
                 )
                 e_of[n].append(e_sb)
 
-        def rows_to_partitions(rows_of_tile, tag):
-            words_ps = psum.tile([P, BLOCK_TILES, 2, P], F32, tag="tr", bufs=3)
-            for q in range(BLOCK_TILES):
+        def rows_to_words(rows):
+            words_ps = psum.tile([P, 2, 2, P], F32, tag="tr", bufs=3, name="words_ps")
+            for a in range(2):
                 for u in range(2):
                     nc.tensor.transpose(
-                        words_ps[:, q, u, :],
-                        rows_of_tile[q].bitcast(F32)[:, u * P : (u + 1) * P],
-                        ident_f[:],
+                        words_ps[:, a, u, :], rows[a].bitcast(F32)[:, u * P : (u + 1) * P], ident_f[:]
                     )
-            grouped = work.tile([P, BLOCK_TILES * P * PACK], BF16, tag=tag, bufs=2, align_bytes=64)
+            return words_ps
+
+        def words_to_grouped(words_ps, tag):
+            grouped = work.tile([P, 2 * P * PACK], BF16, tag=tag, bufs=2, align_bytes=64, name=tag)
             nc.scalar.copy(
-                out=grouped[:].bitcast(F32).rearrange("p (q i u) -> p q i u", q=BLOCK_TILES, u=2),
-                in_=words_ps[:].rearrange("p q u i -> p q i u"),
+                out=grouped[:].bitcast(F32).rearrange("p (a i u) -> p a i u", a=2, u=2),
+                in_=words_ps[:].rearrange("p a u i -> p a i u"),
             )
             return grouped
 
         def quantise_e(n):
-            e_codes = work.tile([P, BLOCK], U32, tag="e_codes", bufs=2, align_bytes=64)
-            e_scales = work.tile([P, BLOCK], U8, tag="e_scales", bufs=2, align_bytes=64)
+            e_codes = work.tile([P, PAIR * P], U32, tag="e_codes", bufs=2, align_bytes=64, name="e_codes")
+            e_scales = work.tile([P, PAIR * P], U8, tag="e_scales", bufs=2, align_bytes=64, name="e_scales")
             nc.vector.quantize_mx(out=e_codes[:].bitcast(FP8X4), scales=e_scales[:], in_=e_grouped_of[n][:])
             e_mx_of[n] = (e_codes, e_scales)
 
         def weighted_values(n):
-            h = n % HEADS
-            a = h % GROUP_HEADS
-            pair, b = divmod(a, 2)
-            if b == 0:
-                pv_of[n // 2] = psum.tile([P, BLOCK_TILES, 2, HEAD_DIM], F32, tag="pv", bufs=1, name="pv_ps")
-            if a == 0:
-                o_of[n // GROUP_HEADS] = work.tile([P, BLOCK_TILES, K_PASS], BF16, tag="o_sb", bufs=2, name="o_sb")
-            pv_ps = pv_of[n // 2]
+            k, m = divmod(n, 2)
+            if m == 0:
+                pv_of[k] = psum.tile([P, 2, PAIR, HEAD_DIM], F32, tag="pv", bufs=1, name="pv_ps")
             e_codes, e_scales = e_mx_of[n]
-            cols = slice(h * HEAD_DIM, (h + 1) * HEAD_DIM)
-            for q in range(BLOCK_TILES):
-                rows = slice(q * P, (q + 1) * P)
+            for b in range(PAIR):
+                h = (n % PAIRS) * PAIR + b
+                rows = slice(b * P, (b + 1) * P)
+                cols = slice(h * HEAD_DIM, (h + 1) * HEAD_DIM)
                 nc.tensor.matmul_mx(
-                    out=pv_ps[:, q, b, :],
+                    out=pv_of[k][:, m, b, :],
                     lhsT=e_codes[:, rows].bitcast(FP8X4),
                     lhsT_scale=e_scales[:, rows],
                     rhs=k_first_codes[:, 0, cols].bitcast(FP8X4),
@@ -248,86 +369,151 @@ def tile_mptattentionfused_pa_kernel(tc, xq, xk, xv, mask, w_out, out):
                     start=True,
                     stop=True,
                 )
-            if b == 1:
-                inv_sum = work.tile([P, BLOCK_TILES, 2], F32, tag="inv_sum", bufs=2)
-                nc.vector.reciprocal(out=inv_sum[:], in_=sums_of[n // 2][:])
-                o_sb = o_of[n // GROUP_HEADS]
-                nc.vector.tensor_tensor(
-                    out=o_sb[:, :, pair * 2 * HEAD_DIM : (pair + 1) * 2 * HEAD_DIM].rearrange(
-                        "p q (b d) -> p q b d", b=2
-                    ),
-                    in0=pv_ps[:],
-                    in1=inv_sum[:].unsqueeze(3).to_broadcast([P, BLOCK_TILES, 2, HEAD_DIM]),
-                    op=ALU.mult,
-                )
 
-        def quantise_o(n):
-            blk, h = divmod(n, HEADS)
-            g = h // GROUP_HEADS
-            if g == 0:
-                o_codes = work.tile([P, GROUPS, BLOCK], U32, tag="o_codes", bufs=2, align_bytes=64)
-                o_scales = work.tile([P, GROUPS, BLOCK], U8, tag="o_scales", bufs=2, align_bytes=64)
-                o_mx_of[blk] = (o_codes, o_scales)
-            o_codes, o_scales = o_mx_of[blk]
-            nc.vector.quantize_mx(
-                out=o_codes[:, g, :].bitcast(FP8X4), scales=o_scales[:, g, :], in_=o_grouped_of[n][:]
+        def invert_sums(n):
+            inv_sum = work.tile([P, PAIR], F32, tag="inv_sum", bufs=3, name="inv_sum")
+            nc.vector.reciprocal(out=inv_sum[:], in_=sums_of[n][:])
+            inv_of[n] = inv_sum
+
+        def normalise(n):
+            k, m = divmod(n, 2)
+            j, u = divmod(n, HALF_UNITS)
+            if u == 0:
+                o_of[j] = work.tile([P, HALF_HEADS, HEAD_DIM], BF16, tag="o_sb", bufs=2, name="o_sb")
+            nc.vector.tensor_tensor(
+                out=o_of[j][:, u * PAIR : (u + 1) * PAIR, :],
+                in0=pv_of[k][:, m, :, :],
+                in1=inv_of[n][:].unsqueeze(2).to_broadcast([P, PAIR, HEAD_DIM]),
+                op=ALU.mult,
             )
 
-        def project(blk, tile_index, copy):
-            q, n = divmod(tile_index, N_TILES)
-            o_codes, o_scales = o_mx_of[blk]
-            acc = psum.tile([P, N_TILE], F32, tag="s", bufs=4)
-            rows = slice(q * P, (q + 1) * P)
+        def quantise_o(j):
+            it, half = divmod(j, 2)
+            if half == 0:
+                o_codes = work.tile([P, GROUPS * P], U32, tag="o_codes", bufs=3, align_bytes=64, name="o_codes")
+                o_scales = work.tile([P, GROUPS * P], U8, tag="o_scales", bufs=3, align_bytes=64, name="o_scales")
+                o_mx_of[it] = (o_codes, o_scales)
+            o_codes, o_scales = o_mx_of[it]
+            cols = slice(half * HALF_GROUPS * P, (half + 1) * HALF_GROUPS * P)
+            nc.vector.quantize_mx(
+                out=o_codes[:, cols].bitcast(FP8X4), scales=o_scales[:, cols], in_=o_grouped_of[j][:]
+            )
+
+        acc_of = {}
+
+        def project(it, n, groups, tag, bufs):
+            o_codes, o_scales = o_mx_of[it]
+            if groups[0] == 0:
+                acc_of[it, n] = psum.tile([P, N_TILE], F32, tag=tag, bufs=bufs, name="acc")
             cols = slice(n * N_TILE, (n + 1) * N_TILE)
-            for g in range(GROUPS):
+            for g in groups:
+                rows = slice(g * P, (g + 1) * P)
                 nc.tensor.matmul_mx(
-                    out=acc[:],
-                    lhsT=o_codes[:, g, rows].bitcast(FP8X4),
-                    lhsT_scale=o_scales[:, g, rows],
+                    out=acc_of[it, n][:],
+                    lhsT=o_codes[:, rows].bitcast(FP8X4),
+                    lhsT_scale=o_scales[:, rows],
                     rhs=k_first_codes[:, 1 + g, cols].bitcast(FP8X4),
                     rhs_scale=k_first_scales[:, 1 + g, cols],
                     start=(g == 0),
                     stop=(g == GROUPS - 1),
                 )
-            result = work.tile([P, N_TILE], F32, tag="result", bufs=8)
-            copy(out=result[:], in_=acc[:])
-            nc.sync.dma_start(out=out_rows[blk * BLOCK_TILES + q][:, cols], in_=result[:])
 
-        K_FIRST_CHUNKS = (1 + GROUPS) * N_TILES
-        BLOCK_OUT_TILES = BLOCK_TILES * N_TILES
-        FIRST_PROJECTION = 26
+        def store(it, n, copy):
+            result = work.tile([P, N_TILE], F32, tag="result", bufs=6, name="result")
+            copy(out=result[:], in_=acc_of[it, n][:])
+            nc.sync.dma_start(out=out_rows[it][:, n * N_TILE : (n + 1) * N_TILE], in_=result[:])
+
+        CHUNKS = (1 + GROUPS) * N_TILES
+        ALL = tuple(range(GROUPS))
+        HALF_CHUNK = N_TILE // 2
+        project_in = {}
+        for it, first, step in ((0, 15, 3), (1, 23, 3), (2, 32, 1)):
+            for n in range(N_TILES):
+                r = first + step * n
+                while r in project_in:
+                    r += 1
+                project_in[r] = (it, n)
+        jobs = {"gpsimd": {}, "vector": {}, "scalar": {}}
+        in_hand = {"gpsimd": None, "vector": None, "scalar": None}
         next_chunk = 0
-        transpose_head(0)
-        transpose_head(1)
-        build_bias(0)
-        build_bias(1)
-        for i in range(UNITS + 4):
-            if 0 <= i - 2 < UNITS:
-                e_grouped_of[i - 2] = rows_to_partitions([e[:] for e in e_of[i - 2]], "e_grouped")
-            if i < UNITS:
-                scores(i)
-                softmax(i)
-            last_of_group = 0 <= i - 4 and (i - 4) % GROUP_HEADS == GROUP_HEADS - 1
-            if last_of_group:
-                o_sb = o_of[(i - 4) // GROUP_HEADS]
-                o_grouped_of[i - 4] = rows_to_partitions(
-                    [o_sb[:, q, :] for q in range(BLOCK_TILES)], "o_grouped"
-                )
-            if i + 2 < HEADS:
-                transpose_head(i + 2)
-            if i + 2 < UNITS:
-                build_bias(i + 2)
-            if 0 <= i - 3 < UNITS:
-                weighted_values(i - 3)
-            if 0 <= i - FIRST_PROJECTION < BLOCK_OUT_TILES:
-                project(0, i - FIRST_PROJECTION, nc.scalar.copy)
-            if i >= 2 and i % 4 != 3 and next_chunk < K_FIRST_CHUNKS:
-                quantise_k_first(next_chunk)
-                next_chunk += 1
-            if 0 <= i - 2 < UNITS:
-                quantise_e(i - 2)
-            if last_of_group:
-                quantise_o(i - 4)
+        last_round_of = {}
+        for r in range(60):
+            for engine, first_round, last_round in ENGINE_ROUNDS:
+                if not first_round <= r < last_round and in_hand[engine] is None:
+                    continue
+                if in_hand[engine] is None and next_chunk < CHUNKS:
+                    in_hand[engine] = (next_chunk, 0)
+                    next_chunk += 1
+                if in_hand[engine] is not None:
+                    c, first = in_hand[engine]
+                    width = WIDTH[engine]
+                    jobs[engine][r] = (c, first, width)
+                    last_round_of[c] = r
+                    in_hand[engine] = (c, first + width) if first + width < N_TILE else None
 
-        for tile_index in range(BLOCK_OUT_TILES):
-            project(1, tile_index, nc.scalar.copy if tile_index % 2 == 0 else nc.vector.tensor_copy)
+        o_words_of = {}
+        e_words_of = {}
+        transpose_mask(0)
+        transpose_k(0)
+        transpose_q(0)
+        transpose_k(1)
+        for r in range(UNITS + 7):
+            if 0 <= r - 3 < UNITS:
+                e_grouped_of[r - 3] = words_to_grouped(e_words_of[r - 3], "e_grouped")
+            if r >= 9 and (r - 9) % HALF_UNITS == 0 and (r - 9) // HALF_UNITS < 2 * TILES:
+                j = (r - 9) // HALF_UNITS
+                o_grouped_of[j] = words_to_grouped(o_words_of[j], "o_grouped")
+            if r - 1 in project_in:
+                store(*project_in[r - 1], nc.scalar.copy)
+            if r + 2 < PAIRS:
+                transpose_k(r + 2)
+            if r % HALF_UNITS == 1 and r // HALF_UNITS + 1 < 2 * TILES:
+                transpose_q(r // HALF_UNITS + 1)
+            if r in (2, 3, 4):
+                transpose_mask(r - 1)
+            if r < UNITS:
+                scores(r)
+            if 0 <= r - 2 < UNITS:
+                e_words_of[r - 2] = rows_to_words([e[:] for e in e_of[r - 2]])
+            if 0 <= r - 1 < UNITS:
+                row_maxima(r - 1)
+            if r in jobs["gpsimd"]:
+                regroup(*jobs["gpsimd"][r], "gpsimd")
+            if 0 <= r - 5 < UNITS:
+                normalise(r - 5)
+            if 0 <= r - 1 < UNITS:
+                shifts(r - 1)
+                exponentials(r - 1)
+            if r in jobs["scalar"]:
+                regroup(*jobs["scalar"][r], "scalar")
+            if r >= 8 and (r - 8) % HALF_UNITS == 0 and (r - 8) // HALF_UNITS < 2 * TILES:
+                j = (r - 8) // HALF_UNITS
+                o_words_of[j] = rows_to_words(
+                    [o_of[j][:, a * GROUP_HEADS : (a + 1) * GROUP_HEADS, :].rearrange("p h d -> p (h d)") for a in range(2)]
+                )
+            if 0 <= r - 4 < UNITS:
+                invert_sums(r - 4)
+            if r - 1 in jobs["vector"]:
+                quantise_chunk(*jobs["vector"][r - 1])
+            if r + 2 < UNITS:
+                build_bias(r + 2)
+            if r >= 9 and (r - 9) % HALF_UNITS == 0 and (r - 9) // HALF_UNITS < 2 * TILES:
+                quantise_o((r - 9) // HALF_UNITS)
+            if 0 <= r - 3 < UNITS:
+                quantise_e(r - 3)
+            if r in jobs["vector"]:
+                regroup(*jobs["vector"][r], "vector")
+            if r - 1 in jobs["scalar"]:
+                quantise_chunk(*jobs["scalar"][r - 1])
+            if r in jobs["gpsimd"]:
+                quantise_chunk(*jobs["gpsimd"][r])
+            if 0 <= r - 4 < UNITS:
+                weighted_values(r - 4)
+            if r in project_in:
+                project(*project_in[r], ALL, "tr", 3)
+            if 34 <= r < 38:
+                project(TILES - 1, r - 34, ALL[:2], "s", 4)
+
+        for n in range(N_TILES):
+            project(TILES - 1, n, ALL[2:], "s", 4)
+            store(TILES - 1, n, nc.scalar.copy if n % 2 == 0 else nc.vector.tensor_copy)

@@ -34,11 +34,28 @@ HALF_GROUPS = HALF_HEADS // GROUP_HEADS
 N_TILE = 512
 N_TILES = N_OUT // N_TILE
 SQRT_DIM = math.sqrt(HEAD_DIM)
-PRODUCT_UNITS = 16
+PRODUCT_BOTH = 0
+PRODUCT_UNITS = 18
+WARM = 3
+BE = 6
+WR = ()
+WARM2 = 2
+SPLIT = True
+PRODF = True
+TB = 2
+STORE_FIRST = True
+EARLY = 99
+BC_STEP = 99
+WHOLE_FROM = 34
+Q_PHASE = 2
+H3 = 34
+GS, SS, SE, VE = 2, 99, 99, 16
+MASK_ROUNDS = (3, 9, 17)
+V_OUT = 33
 GROUPED_BUFS = {"gpsimd": 1, "vector": 2, "scalar": 3}
 WIDTH = {"gpsimd": 256, "vector": 128, "scalar": 128}
-ENGINE_ROUNDS = (("vector", 0, 20), ("gpsimd", 0, 40), ("scalar", 0, 40))
-BROADCAST_UNITS = 8
+ENGINE_ROUNDS = (("vector", 0, VE), ("gpsimd", GS, 40), ("scalar", SS, SE))
+BROADCAST_UNITS = 18
 
 FLOPS = 2 * 2 * HEADS * SEQ * SEQ * HEAD_DIM + 2 * SEQ * FEATURES * N_OUT
 
@@ -63,10 +80,12 @@ def tile_mptattentionfused_pa_kernel(tc, xq, xk, xv, mask, w_out, out):
         q_raw = {}
         k_first_raw = []
 
-        def load_k(g):
-            tile = work.tile([P, TILES, K_PASS], BF16, tag="k_raw", bufs=3, name="k_raw%d" % g)
-            nc.sync.dma_start(out=tile[:], in_=xk_rows[:, :, g * K_PASS : (g + 1) * K_PASS])
-            k_raw.append(tile)
+        def load_k(pair, pairs):
+            width = PAIR * HEAD_DIM
+            tile = work.tile([P, TILES, pairs * width], BF16, tag="k_raw%d" % pairs, bufs=2, name="k_raw")
+            nc.sync.dma_start(out=tile[:], in_=xk_rows[:, :, pair * width : (pair + pairs) * width])
+            for m in range(pairs):
+                k_raw.append(tile[:, :, m * width : (m + 1) * width])
 
         def load_q(j):
             it, half = divmod(j, 2)
@@ -85,15 +104,16 @@ def tile_mptattentionfused_pa_kernel(tc, xq, xk, xv, mask, w_out, out):
             load_chunk(xv_rows[:, :, :, c * N_TILE : (c + 1) * N_TILE], "xv_raw%d" % c)
 
         nc.sync.dma_start(out=mask_sb[:, 0, :], in_=mask_rows[:, 0, :])
-        load_k(0)
+        load_k(0, 1)
         load_q(0)
+        load_k(1, 1)
         load_xv(0)
-        load_k(1)
+        load_k(2, 2)
         load_xv(1)
         load_q(1)
-        load_k(2)
+        load_k(4, 2)
         load_xv(2)
-        load_k(3)
+        load_k(6, 2)
         load_xv(3)
         nc.sync.dma_start(out=mask_sb[:, 1:TILES, :], in_=mask_rows[:, 1:TILES, :])
         load_q(2)
@@ -103,25 +123,23 @@ def tile_mptattentionfused_pa_kernel(tc, xq, xk, xv, mask, w_out, out):
                 load_chunk(w_rows[g][:, :, :, n * N_TILE : (n + 1) * N_TILE], "w_raw%d_%d" % (n, g))
             load_q(4 + n)
 
-        ident_bf = keep.tile([P, P], BF16)
-        make_identity(nc, ident_bf[:])
-        ident_f = keep.tile([P, P], F32)
-        make_identity(nc, ident_f[:])
         ones = keep.tile([P, 1], F32)
-        nc.gpsimd.memset(ones[:], 1.0)
-
-        amp = keep.tile([P, HEADS], F32)
-        for h in range(HEADS):
-            nc.scalar.mul(out=amp[:, h : h + 1], in_=ones[:], mul=2.0 ** (-(h + 1) / 2) * SQRT_DIM)
-
-        key_dist_i = keep.tile([P, TILES], I32)
-        nc.gpsimd.iota(key_dist_i[:], pattern=[[P, TILES]], base=1 - SEQ, channel_multiplier=1)
-        key_dist = keep.tile([P, TILES], F32)
-        nc.vector.tensor_copy(out=key_dist[:], in_=key_dist_i[:])
+        nc.vector.memset(ones[:], 1.0)
         dist_i = keep.tile([P, SEQ], I32)
         nc.gpsimd.iota(dist_i[:], pattern=[[1, SEQ]], base=1 - SEQ, channel_multiplier=0)
         part_i = keep.tile([P, 1], I32)
         nc.gpsimd.iota(part_i[:], pattern=[[1, 1]], base=0, channel_multiplier=1)
+        key_dist_i = keep.tile([P, TILES], I32)
+        nc.gpsimd.iota(key_dist_i[:], pattern=[[P, TILES]], base=1 - SEQ, channel_multiplier=1)
+        ident_f = keep.tile([P, P], F32)
+        make_identity(nc, ident_f[:])
+        ident_bf = keep.tile([P, P], BF16)
+        make_identity(nc, ident_bf[:])
+
+        amp = keep.tile([P, HEADS], F32)
+        for h in range(HEADS):
+            nc.scalar.mul(out=amp[:, h : h + 1], in_=ones[:], mul=2.0 ** (-(h + 1) / 2) * SQRT_DIM)
+        key_dist = keep.tile([P, TILES], F32)
 
         dist = keep.tile([P, SEQ], F32)
         nc.vector.tensor_copy(out=dist[:], in_=dist_i[:])
@@ -162,6 +180,7 @@ def tile_mptattentionfused_pa_kernel(tc, xq, xk, xv, mask, w_out, out):
         nc.vector.scalar_tensor_tensor(
             out=coef[:], in0=amp_last[:], scalar=both[2][:], in1=coef_b[:], op0=ALU.mult, op1=ALU.add
         )
+        nc.vector.tensor_copy(out=key_dist[:], in_=key_dist_i[:])
         alibi = keep.tile([P, HEADS, TILES], F32)
         nc.vector.tensor_tensor(
             out=alibi[:],
@@ -176,6 +195,7 @@ def tile_mptattentionfused_pa_kernel(tc, xq, xk, xv, mask, w_out, out):
         mask_t = keep.tile([P, TILES, TILES, P], F32)
 
         grouped_of = {}
+        copies = []
         q_t_of = {}
         bias_of = {}
         scores_of = {}
@@ -192,10 +212,10 @@ def tile_mptattentionfused_pa_kernel(tc, xq, xk, xv, mask, w_out, out):
         o_mx_of = {}
 
         def transpose_mask(it):
-            mask_ps = psum.tile([P, TILES, P], BF16, tag="tr", bufs=3, name="mask_ps")
+            mask_ps = psum.tile([P, TILES, P], BF16, tag="tr", bufs=2, name="mask_ps")
             for t in range(TILES):
                 nc.tensor.transpose(mask_ps[:, t, :], mask_sb[:, it, t * P : (t + 1) * P], ident_bf[:])
-            nc.scalar.mul(out=mask_t[:, it, :, :], in_=mask_ps[:], mul=SQRT_DIM)
+            copies.append(lambda copy: nc.scalar.mul(out=mask_t[:, it, :, :], in_=mask_ps[:], mul=SQRT_DIM))
 
         def regroup(c, first, width, engine):
             grouped = work.tile(
@@ -226,29 +246,32 @@ def tile_mptattentionfused_pa_kernel(tc, xq, xk, xv, mask, w_out, out):
             )
 
         def transpose_k(pair):
-            g, a = divmod(pair * PAIR, GROUP_HEADS)
-            k_ps = psum.tile([P, PAIR, TILES, P], BF16, tag="tr", bufs=3, name="k_ps")
+            k_ps = psum.tile([P, PAIR, TILES, P], BF16, tag="tr", bufs=2, name="k_ps")
             for b in range(PAIR):
-                cols = slice((a + b) * HEAD_DIM, (a + b + 1) * HEAD_DIM)
+                cols = slice(b * HEAD_DIM, (b + 1) * HEAD_DIM)
                 for t in range(TILES):
-                    nc.tensor.transpose(k_ps[:, b, t, :], k_raw[g][:, t, cols], ident_bf[:])
-            nc.scalar.copy(
-                out=k_t[:, pair * PAIR : (pair + 1) * PAIR, :],
-                in_=k_ps[:].rearrange("p b t j -> p b (t j)"),
+                    nc.tensor.transpose(k_ps[:, b, t, :], k_raw[pair][:, t, cols], ident_bf[:])
+            copies.append(
+                lambda copy: copy(
+                    out=k_t[:, pair * PAIR : (pair + 1) * PAIR, :],
+                    in_=k_ps[:].rearrange("p b t j -> p b (t j)"),
+                )
             )
 
         def transpose_q(j):
-            q_ps = psum.tile([P, HALF_HEADS, P], BF16, tag="tr", bufs=3, name="q_ps")
+            q_ps = psum.tile([P, HALF_HEADS, P], BF16, tag="tr", bufs=2, name="q_ps")
             for a in range(HALF_HEADS):
                 nc.tensor.transpose(q_ps[:, a, :], q_raw[j][:, a * HEAD_DIM : (a + 1) * HEAD_DIM], ident_bf[:])
             q_t = work.tile([P, HALF_HEADS, P], BF16, tag="q_t", bufs=3, name="q_t")
-            nc.scalar.copy(out=q_t[:], in_=q_ps[:])
             q_t_of[j] = q_t
+            copies.append(lambda copy: copy(out=q_t[:], in_=q_ps[:]))
 
         def bias_form(n, b):
-            if n < PRODUCT_UNITS and b == 0:
+            if n < PRODUCT_BOTH or (b == 1 and n < PRODUCT_UNITS):
                 return "product"
-            return "broadcast" if n < BROADCAST_UNITS else "built"
+            if b == 0 and BE <= n < BROADCAST_UNITS:
+                return "broadcast"
+            return "built"
 
         def build_bias(n):
             it, pair = divmod(n, PAIRS)
@@ -258,49 +281,54 @@ def tile_mptattentionfused_pa_kernel(tc, xq, xk, xv, mask, w_out, out):
             bias_of[n] = work.tile([P, PAIR, TILES, P], F32, tag="bias_t", bufs=3, name="bias_t")
             for b in heads:
                 for t in range(TILES):
-                    nc.vector.tensor_scalar_add(
-                        out=bias_of[n][:, b, t, :],
-                        in0=mask_t[:, it, t, :],
-                        scalar1=alibi[:, pair * PAIR + b, t : t + 1],
-                    )
+                    out_t = bias_of[n][:, b, t, :]
+                    alibi_t = alibi[:, pair * PAIR + b, t : t + 1]
+                    if b == 1 and t >= TB:
+                        nc.scalar.activation(out=out_t, in_=mask_t[:, it, t, :], func=ACT.Identity, bias=alibi_t)
+                    else:
+                        nc.vector.tensor_scalar_add(out=out_t, in0=mask_t[:, it, t, :], scalar1=alibi_t)
 
-        def scores(n):
+        def multiply_scores(n, b):
+            h = (n % PAIRS) * PAIR + b
+            s_ps = psum.tile([P, SEQ], F32, tag="s", bufs=4, name="s_ps")
+            nc.tensor.matmul(
+                out=s_ps[:],
+                lhsT=q_t_of[n // HALF_UNITS][:, h % HALF_HEADS, :],
+                rhs=k_t[:, h, :],
+                start=True,
+                stop=False,
+            )
+            scores_of.setdefault(n, []).append(s_ps)
+
+        def add_bias(n, b):
             it, pair = divmod(n, PAIRS)
-            scores_of[n] = []
-            for b in range(PAIR):
-                h = pair * PAIR + b
-                s_ps = psum.tile([P, SEQ], F32, tag="s", bufs=4, name="s_ps")
-                form = bias_form(n, b)
+            form = bias_form(n, b)
+            added = []
+            for t in range(TILES):
+                if form == "broadcast":
+                    added.append((t, alibi[:, pair * PAIR + b, t : t + 1].to_broadcast([P, P])))
+                added.append((t, bias_of[n][:, b, t, :] if form == "built" else mask_t[:, it, t, :]))
+            for m, (t, rows) in enumerate(added):
                 nc.tensor.matmul(
-                    out=s_ps[:],
-                    lhsT=q_t_of[n // HALF_UNITS][:, h % HALF_HEADS, :],
-                    rhs=k_t[:, h, :],
-                    start=True,
-                    stop=False,
+                    out=scores_of[n][b][:, t * P : (t + 1) * P],
+                    lhsT=rows,
+                    rhs=ident_f[:],
+                    is_transpose=True,
+                    start=False,
+                    stop=((PRODF or form != "product") and m == len(added) - 1),
                 )
-                if form == "product":
+
+        def close_scores(n):
+            for b in range(PAIR):
+                if bias_form(n, b) == "product":
+                    h = (n % PAIRS) * PAIR + b
                     nc.tensor.matmul(
-                        out=s_ps[:],
+                        out=scores_of[n][b][:],
                         lhsT=coef[:, h : h + 1].to_broadcast([P, P]),
                         rhs=dist_bf[:],
                         start=False,
-                        stop=False,
+                        stop=not PRODF,
                     )
-                added = []
-                for t in range(TILES):
-                    if form == "broadcast":
-                        added.append((t, alibi[:, h, t : t + 1].to_broadcast([P, P])))
-                    added.append((t, bias_of[n][:, b, t, :] if form == "built" else mask_t[:, it, t, :]))
-                for m, (t, rows) in enumerate(added):
-                    nc.tensor.matmul(
-                        out=s_ps[:, t * P : (t + 1) * P],
-                        lhsT=rows,
-                        rhs=ident_f[:],
-                        is_transpose=True,
-                        start=False,
-                        stop=(m == len(added) - 1),
-                    )
-                scores_of[n].append(s_ps)
 
         def row_maxima(n):
             row_max = work.tile([P, PAIR], F32, tag="row_max", bufs=3, name="row_max")
@@ -310,7 +338,7 @@ def tile_mptattentionfused_pa_kernel(tc, xq, xk, xv, mask, w_out, out):
 
         def shifts(n):
             shift = work.tile([P, PAIR], F32, tag="shift", bufs=3, name="shift")
-            nc.vector.tensor_scalar_mul(out=shift[:], in0=row_max_of[n][:], scalar1=-1.0 / SQRT_DIM)
+            nc.scalar.mul(out=shift[:], in_=row_max_of[n][:], mul=-1.0 / SQRT_DIM)
             shift_of[n] = shift
 
         def exponentials(n):
@@ -329,7 +357,7 @@ def tile_mptattentionfused_pa_kernel(tc, xq, xk, xv, mask, w_out, out):
                 e_of[n].append(e_sb)
 
         def rows_to_words(rows):
-            words_ps = psum.tile([P, 2, 2, P], F32, tag="tr", bufs=3, name="words_ps")
+            words_ps = psum.tile([P, 2, 2, P], F32, tag="tr", bufs=2, name="words_ps")
             for a in range(2):
                 for u in range(2):
                     nc.tensor.transpose(
@@ -390,8 +418,8 @@ def tile_mptattentionfused_pa_kernel(tc, xq, xk, xv, mask, w_out, out):
         def quantise_o(j):
             it, half = divmod(j, 2)
             if half == 0:
-                o_codes = work.tile([P, GROUPS * P], U32, tag="o_codes", bufs=3, align_bytes=64, name="o_codes")
-                o_scales = work.tile([P, GROUPS * P], U8, tag="o_scales", bufs=3, align_bytes=64, name="o_scales")
+                o_codes = work.tile([P, GROUPS * P], U32, tag="o_codes", bufs=4, align_bytes=64, name="o_codes")
+                o_scales = work.tile([P, GROUPS * P], U8, tag="o_scales", bufs=4, align_bytes=64, name="o_scales")
                 o_mx_of[it] = (o_codes, o_scales)
             o_codes, o_scales = o_mx_of[it]
             cols = slice(half * HALF_GROUPS * P, (half + 1) * HALF_GROUPS * P)
@@ -423,16 +451,13 @@ def tile_mptattentionfused_pa_kernel(tc, xq, xk, xv, mask, w_out, out):
             copy(out=result[:], in_=acc_of[it, n][:])
             nc.sync.dma_start(out=out_rows[it][:, n * N_TILE : (n + 1) * N_TILE], in_=result[:])
 
+        def store_tiles(r, copy):
+            if r in project_in and project_in[r][1][-1] == GROUPS - 1:
+                store(*project_in[r][0], copy)
+
         CHUNKS = (1 + GROUPS) * N_TILES
         ALL = tuple(range(GROUPS))
         HALF_CHUNK = N_TILE // 2
-        project_in = {}
-        for it, first, step in ((0, 15, 3), (1, 23, 3), (2, 32, 1)):
-            for n in range(N_TILES):
-                r = first + step * n
-                while r in project_in:
-                    r += 1
-                project_in[r] = (it, n)
         jobs = {"gpsimd": {}, "vector": {}, "scalar": {}}
         in_hand = {"gpsimd": None, "vector": None, "scalar": None}
         next_chunk = 0
@@ -451,68 +476,123 @@ def tile_mptattentionfused_pa_kernel(tc, xq, xk, xv, mask, w_out, out):
                     last_round_of[c] = r
                     in_hand[engine] = (c, first + width) if first + width < N_TILE else None
 
+        project_in = {}
+        waiting = sorted(
+            (max(PAIRS * it + 14, 2 + max(last_round_of[N_TILES + GROUPS * n + g] for g in range(GROUPS))), it, n)
+            for it in range(TILES - 1)
+            for n in range(N_TILES)
+        )
+        r = 0
+        while waiting:
+            if waiting[0][0] <= r:
+                ready, it, n = waiting.pop(0)
+                if r + 1 + len(waiting) < WHOLE_FROM:
+                    project_in[r] = ((it, n), ALL[:2])
+                    project_in[r + 1] = ((it, n), ALL[2:])
+                    r += 1
+                else:
+                    project_in[r] = ((it, n), ALL)
+            r += 1
+
+        assert max(project_in) < UNITS + 7
         o_words_of = {}
         e_words_of = {}
+        if WARM:
+            warm = psum.tile([P, P], F32, tag="pv", bufs=1, name="warm")
+            for m in range(WARM):
+                nc.tensor.matmul(out=warm[:], lhsT=ident_f[:], rhs=ident_f[:], start=True, stop=True)
         transpose_mask(0)
         transpose_k(0)
         transpose_q(0)
-        transpose_k(1)
+        for m in range(WARM2):
+            nc.tensor.matmul(out=warm[:], lhsT=ident_f[:], rhs=ident_f[:], start=True, stop=True)
+        for n, move in enumerate(copies):
+            move(nc.vector.tensor_copy if n == 2 else nc.scalar.copy)
+        copies.clear()
+        build_bias(0)
         for r in range(UNITS + 7):
+            if r <= V_OUT and STORE_FIRST:
+                store_tiles(r - 1, nc.scalar.copy)
             if 0 <= r - 3 < UNITS:
                 e_grouped_of[r - 3] = words_to_grouped(e_words_of[r - 3], "e_grouped")
+            for move in copies:
+                move(nc.scalar.copy)
+            copies.clear()
             if r >= 9 and (r - 9) % HALF_UNITS == 0 and (r - 9) // HALF_UNITS < 2 * TILES:
                 j = (r - 9) // HALF_UNITS
                 o_grouped_of[j] = words_to_grouped(o_words_of[j], "o_grouped")
-            if r - 1 in project_in:
-                store(*project_in[r - 1], nc.scalar.copy)
-            if r + 2 < PAIRS:
-                transpose_k(r + 2)
-            if r % HALF_UNITS == 1 and r // HALF_UNITS + 1 < 2 * TILES:
-                transpose_q(r // HALF_UNITS + 1)
-            if r in (2, 3, 4):
-                transpose_mask(r - 1)
-            if r < UNITS:
-                scores(r)
-            if 0 <= r - 2 < UNITS:
-                e_words_of[r - 2] = rows_to_words([e[:] for e in e_of[r - 2]])
-            if 0 <= r - 1 < UNITS:
-                row_maxima(r - 1)
+            if r <= V_OUT and not STORE_FIRST:
+                store_tiles(r - 1, nc.scalar.copy)
             if r in jobs["gpsimd"]:
                 regroup(*jobs["gpsimd"][r], "gpsimd")
             if 0 <= r - 5 < UNITS:
                 normalise(r - 5)
             if 0 <= r - 1 < UNITS:
+                row_maxima(r - 1)
+            if 0 <= r - 1 < UNITS:
                 shifts(r - 1)
                 exponentials(r - 1)
             if r in jobs["scalar"]:
                 regroup(*jobs["scalar"][r], "scalar")
-            if r >= 8 and (r - 8) % HALF_UNITS == 0 and (r - 8) // HALF_UNITS < 2 * TILES:
-                j = (r - 8) // HALF_UNITS
-                o_words_of[j] = rows_to_words(
-                    [o_of[j][:, a * GROUP_HEADS : (a + 1) * GROUP_HEADS, :].rearrange("p h d -> p (h d)") for a in range(2)]
-                )
             if 0 <= r - 4 < UNITS:
                 invert_sums(r - 4)
             if r - 1 in jobs["vector"]:
                 quantise_chunk(*jobs["vector"][r - 1])
-            if r + 2 < UNITS:
-                build_bias(r + 2)
-            if r >= 9 and (r - 9) % HALF_UNITS == 0 and (r - 9) // HALF_UNITS < 2 * TILES:
-                quantise_o((r - 9) // HALF_UNITS)
+            if r + 1 < UNITS:
+                build_bias(r + 1)
             if 0 <= r - 3 < UNITS:
                 quantise_e(r - 3)
             if r in jobs["vector"]:
                 regroup(*jobs["vector"][r], "vector")
             if r - 1 in jobs["scalar"]:
                 quantise_chunk(*jobs["scalar"][r - 1])
+            if r >= 9 and (r - 9) % HALF_UNITS == 0 and (r - 9) // HALF_UNITS < 2 * TILES:
+                quantise_o((r - 9) // HALF_UNITS)
             if r in jobs["gpsimd"]:
                 quantise_chunk(*jobs["gpsimd"][r])
+            if r < UNITS and not SPLIT:
+                multiply_scores(r, 0)
+            for m in range(WR[r] if r < len(WR) else 0):
+                nc.tensor.matmul(out=warm[:], lhsT=ident_f[:], rhs=ident_f[:], start=True, stop=True)
+            if r < UNITS and SPLIT:
+                multiply_scores(r, 0)
+                add_bias(r, 0)
+                if 0 <= r - 2 < UNITS:
+                    e_words_of[r - 2] = rows_to_words([e[:] for e in e_of[r - 2]])
+                multiply_scores(r, 1)
             if 0 <= r - 4 < UNITS:
                 weighted_values(r - 4)
             if r in project_in:
-                project(*project_in[r], ALL, "tr", 3)
-            if 34 <= r < 38:
-                project(TILES - 1, r - 34, ALL[:2], "s", 4)
+                project(*project_in[r][0], project_in[r][1], "acc", 1)
+            if H3 <= r < H3 + 4:
+                project(TILES - 1, r - H3, ALL[:2], "s", 4)
+            if r < UNITS and SPLIT:
+                if PRODF:
+                    close_scores(r)
+                add_bias(r, 1)
+            elif r < UNITS:
+                multiply_scores(r, 1)
+                add_bias(r, 0)
+                add_bias(r, 1)
+            if 0 <= r - 2 < UNITS and r - 2 not in e_words_of:
+                e_words_of[r - 2] = rows_to_words([e[:] for e in e_of[r - 2]])
+            if r >= 8 and (r - 8) % HALF_UNITS == 0 and (r - 8) // HALF_UNITS < 2 * TILES:
+                j = (r - 8) // HALF_UNITS
+                o_words_of[j] = rows_to_words(
+                    [o_of[j][:, a * GROUP_HEADS : (a + 1) * GROUP_HEADS, :].rearrange("p h d -> p (h d)") for a in range(2)]
+                )
+            if r == 0:
+                transpose_k(1)
+            if r + 2 < PAIRS:
+                transpose_k(r + 2)
+            if r % HALF_UNITS == Q_PHASE and r // HALF_UNITS + 1 < 2 * TILES:
+                transpose_q(r // HALF_UNITS + 1)
+            if r in MASK_ROUNDS:
+                transpose_mask(1 + MASK_ROUNDS.index(r))
+            if r < UNITS and not (SPLIT and PRODF):
+                close_scores(r)
+            if r >= V_OUT:
+                store_tiles(r, nc.vector.tensor_copy)
 
         for n in range(N_TILES):
             project(TILES - 1, n, ALL[2:], "s", 4)

@@ -34,15 +34,18 @@ HALF_GROUPS = HALF_HEADS // GROUP_HEADS
 N_TILE = 512
 N_TILES = N_OUT // N_TILE
 SQRT_DIM = math.sqrt(HEAD_DIM)
-PRODUCT_BOTH = 0
-PRODUCT_UNITS = 18
+P0 = 2
+PX = ()
 WARM = 3
+EARLYP = True
+SSTEP, SPH = 2, 0
 BE = 6
 WR = ()
 WARM2 = 2
 SPLIT = True
 PRODF = True
 TB = 2
+TBN = 99
 STORE_FIRST = True
 EARLY = 99
 BC_STEP = 99
@@ -141,46 +144,11 @@ def tile_mptattentionfused_pa_kernel(tc, xq, xk, xv, mask, w_out, out):
             nc.scalar.mul(out=amp[:, h : h + 1], in_=ones[:], mul=2.0 ** (-(h + 1) / 2) * SQRT_DIM)
         key_dist = keep.tile([P, TILES], F32)
 
-        dist = keep.tile([P, SEQ], F32)
-        nc.vector.tensor_copy(out=dist[:], in_=dist_i[:])
+        nc.vector.tensor_copy(out=key_dist[:], in_=key_dist_i[:])
         part = keep.tile([P, 1], F32)
         nc.vector.tensor_copy(out=part[:], in_=part_i[:])
-        dist_bf = keep.tile([P, SEQ], BF16)
-        nc.vector.tensor_copy(out=dist_bf[:], in_=dist[:])
-        select = []
-        for m in range(3):
-            low = keep.tile([P, 1], F32, name="low%d" % m)
-            nc.vector.tensor_single_scalar(out=low[:], in_=part[:], scalar=float(m), op=ALU.is_equal)
-            select.append(low)
-        nc.vector.tensor_tensor(
-            out=dist_bf[64:P, :], in0=dist[64:P, :], in1=dist_bf[64:P, :], op=ALU.subtract
-        )
-        both = []
-        for m in range(3):
-            sel = keep.tile([P, 1], F32, name="sel%d" % m)
-            nc.vector.scalar_tensor_tensor(
-                out=sel[:], in0=part[:], scalar=float(64 + m), in1=select[m][:], op0=ALU.is_equal, op1=ALU.add
-            )
-            both.append(sel)
-        amp_hi = keep.tile([P, HEADS], BF16)
-        nc.vector.tensor_copy(out=amp_hi[:], in_=amp[:])
-        amp_rest = keep.tile([P, HEADS], F32)
-        nc.vector.tensor_tensor(out=amp_rest[:], in0=amp[:], in1=amp_hi[:], op=ALU.subtract)
-        amp_mid = keep.tile([P, HEADS], BF16)
-        nc.vector.tensor_copy(out=amp_mid[:], in_=amp_rest[:])
-        amp_last = keep.tile([P, HEADS], F32)
-        nc.vector.tensor_tensor(out=amp_last[:], in0=amp_rest[:], in1=amp_mid[:], op=ALU.subtract)
-        coef_a = keep.tile([P, HEADS], F32)
-        nc.vector.tensor_scalar_mul(out=coef_a[:], in0=amp_hi[:], scalar1=both[0][:])
-        coef_b = keep.tile([P, HEADS], F32)
-        nc.vector.scalar_tensor_tensor(
-            out=coef_b[:], in0=amp_mid[:], scalar=both[1][:], in1=coef_a[:], op0=ALU.mult, op1=ALU.add
-        )
-        coef = keep.tile([P, HEADS], BF16)
-        nc.vector.scalar_tensor_tensor(
-            out=coef[:], in0=amp_last[:], scalar=both[2][:], in1=coef_b[:], op0=ALU.mult, op1=ALU.add
-        )
-        nc.vector.tensor_copy(out=key_dist[:], in_=key_dist_i[:])
+        dist = keep.tile([P, SEQ], F32)
+        nc.vector.tensor_copy(out=dist[:], in_=dist_i[:])
         alibi = keep.tile([P, HEADS, TILES], F32)
         nc.vector.tensor_tensor(
             out=alibi[:],
@@ -188,6 +156,37 @@ def tile_mptattentionfused_pa_kernel(tc, xq, xk, xv, mask, w_out, out):
             in1=key_dist[:].unsqueeze(1).to_broadcast([P, HEADS, TILES]),
             op=ALU.mult,
         )
+
+        dist_bf = keep.tile([P, SEQ], BF16)
+        nc.vector.tensor_copy(out=dist_bf[:], in_=dist[:])
+        rows_of = []
+        for m in range(3):
+            low = keep.tile([P, 1], F32, name="low%d" % m)
+            nc.gpsimd.tensor_single_scalar(out=low[:], in_=part[:], scalar=float(m), op=ALU.is_equal)
+            high = keep.tile([P, 1], F32, name="high%d" % m)
+            nc.gpsimd.tensor_single_scalar(out=high[:], in_=part[:], scalar=float(64 + m), op=ALU.is_equal)
+            both = keep.tile([P, 1], F32, name="both%d" % m)
+            nc.gpsimd.tensor_tensor(out=both[:], in0=low[:], in1=high[:], op=ALU.add)
+            rows_of.append(both)
+        nc.vector.tensor_tensor(
+            out=dist_bf[64:P, :], in0=dist[64:P, :], in1=dist_bf[64:P, :], op=ALU.subtract
+        )
+        rest = amp
+        parts = []
+        for m in range(3):
+            rounded = keep.tile([P, HEADS], BF16, name="rounded%d" % m)
+            nc.gpsimd.tensor_copy(out=rounded[:], in_=rest[:])
+            placed = keep.tile([P, HEADS], F32, name="placed%d" % m)
+            nc.gpsimd.tensor_scalar_mul(out=placed[:], in0=rounded[:], scalar1=rows_of[m][:])
+            parts.append(placed)
+            if m < 2:
+                left = keep.tile([P, HEADS], F32, name="left%d" % m)
+                nc.gpsimd.tensor_tensor(out=left[:], in0=rest[:], in1=rounded[:], op=ALU.subtract)
+                rest = left
+        coef_a = keep.tile([P, HEADS], F32)
+        nc.gpsimd.tensor_tensor(out=coef_a[:], in0=parts[0][:], in1=parts[1][:], op=ALU.add)
+        coef = keep.tile([P, HEADS], BF16)
+        nc.gpsimd.tensor_tensor(out=coef[:], in0=coef_a[:], in1=parts[2][:], op=ALU.add)
 
         k_first_codes = keep.tile([P, 1 + GROUPS, N_OUT], U32, align_bytes=64)
         k_first_scales = keep.tile([P, 1 + GROUPS, N_OUT], U8, align_bytes=64)
@@ -267,7 +266,7 @@ def tile_mptattentionfused_pa_kernel(tc, xq, xk, xv, mask, w_out, out):
             copies.append(lambda copy: copy(out=q_t[:], in_=q_ps[:]))
 
         def bias_form(n, b):
-            if n < PRODUCT_BOTH or (b == 1 and n < PRODUCT_UNITS):
+            if b == 1 and n >= P0 and (n not in project_in or n in PX):
                 return "product"
             if b == 0 and BE <= n < BROADCAST_UNITS:
                 return "broadcast"
@@ -283,22 +282,26 @@ def tile_mptattentionfused_pa_kernel(tc, xq, xk, xv, mask, w_out, out):
                 for t in range(TILES):
                     out_t = bias_of[n][:, b, t, :]
                     alibi_t = alibi[:, pair * PAIR + b, t : t + 1]
-                    if b == 1 and t >= TB:
+                    if b == 1 and t >= TB and n < TBN:
                         nc.scalar.activation(out=out_t, in_=mask_t[:, it, t, :], func=ACT.Identity, bias=alibi_t)
                     else:
                         nc.vector.tensor_scalar_add(out=out_t, in0=mask_t[:, it, t, :], scalar1=alibi_t)
 
+        def open_group(n):
+            scores_of.setdefault(n, []).append(psum.tile([P, SEQ], F32, tag="s", bufs=4, name="s_ps"))
+
         def multiply_scores(n, b):
             h = (n % PAIRS) * PAIR + b
-            s_ps = psum.tile([P, SEQ], F32, tag="s", bufs=4, name="s_ps")
+            product = bias_form(n, b) == "product"
+            if not product:
+                open_group(n)
             nc.tensor.matmul(
-                out=s_ps[:],
+                out=scores_of[n][b][:],
                 lhsT=q_t_of[n // HALF_UNITS][:, h % HALF_HEADS, :],
                 rhs=k_t[:, h, :],
-                start=True,
+                start=not product,
                 stop=False,
             )
-            scores_of.setdefault(n, []).append(s_ps)
 
         def add_bias(n, b):
             it, pair = divmod(n, PAIRS)
@@ -322,12 +325,13 @@ def tile_mptattentionfused_pa_kernel(tc, xq, xk, xv, mask, w_out, out):
             for b in range(PAIR):
                 if bias_form(n, b) == "product":
                     h = (n % PAIRS) * PAIR + b
+                    open_group(n)
                     nc.tensor.matmul(
                         out=scores_of[n][b][:],
                         lhsT=coef[:, h : h + 1].to_broadcast([P, P]),
                         rhs=dist_bf[:],
-                        start=False,
-                        stop=not PRODF,
+                        start=True,
+                        stop=False,
                     )
 
         def row_maxima(n):
@@ -464,6 +468,8 @@ def tile_mptattentionfused_pa_kernel(tc, xq, xk, xv, mask, w_out, out):
         last_round_of = {}
         for r in range(60):
             for engine, first_round, last_round in ENGINE_ROUNDS:
+                if engine == "scalar" and r % SSTEP != SPH:
+                    continue
                 if not first_round <= r < last_round and in_hand[engine] is None:
                     continue
                 if in_hand[engine] is None and next_chunk < CHUNKS:
@@ -497,15 +503,18 @@ def tile_mptattentionfused_pa_kernel(tc, xq, xk, xv, mask, w_out, out):
         assert max(project_in) < UNITS + 7
         o_words_of = {}
         e_words_of = {}
-        if WARM:
-            warm = psum.tile([P, P], F32, tag="pv", bufs=1, name="warm")
-            for m in range(WARM):
+        def warm_up(passes):
+            warm = psum.tile([P, P], F32, tag="acc", bufs=1, name="warm")
+            for m in range(passes):
                 nc.tensor.matmul(out=warm[:], lhsT=ident_f[:], rhs=ident_f[:], start=True, stop=True)
+
+        warm_up(WARM)
         transpose_mask(0)
         transpose_k(0)
         transpose_q(0)
-        for m in range(WARM2):
-            nc.tensor.matmul(out=warm[:], lhsT=ident_f[:], rhs=ident_f[:], start=True, stop=True)
+        transpose_k(1)
+        if WARM2:
+            warm_up(WARM2)
         for n, move in enumerate(copies):
             move(nc.vector.tensor_copy if n == 2 else nc.scalar.copy)
         copies.clear()
@@ -552,13 +561,17 @@ def tile_mptattentionfused_pa_kernel(tc, xq, xk, xv, mask, w_out, out):
                 quantise_chunk(*jobs["gpsimd"][r])
             if r < UNITS and not SPLIT:
                 multiply_scores(r, 0)
-            for m in range(WR[r] if r < len(WR) else 0):
-                nc.tensor.matmul(out=warm[:], lhsT=ident_f[:], rhs=ident_f[:], start=True, stop=True)
+            if r < len(WR) and WR[r]:
+                warm_up(WR[r])
             if r < UNITS and SPLIT:
                 multiply_scores(r, 0)
                 add_bias(r, 0)
+                if EARLYP:
+                    close_scores(r)
                 if 0 <= r - 2 < UNITS:
                     e_words_of[r - 2] = rows_to_words([e[:] for e in e_of[r - 2]])
+                if not EARLYP:
+                    close_scores(r)
                 multiply_scores(r, 1)
             if 0 <= r - 4 < UNITS:
                 weighted_values(r - 4)
@@ -567,8 +580,6 @@ def tile_mptattentionfused_pa_kernel(tc, xq, xk, xv, mask, w_out, out):
             if H3 <= r < H3 + 4:
                 project(TILES - 1, r - H3, ALL[:2], "s", 4)
             if r < UNITS and SPLIT:
-                if PRODF:
-                    close_scores(r)
                 add_bias(r, 1)
             elif r < UNITS:
                 multiply_scores(r, 1)
@@ -581,8 +592,6 @@ def tile_mptattentionfused_pa_kernel(tc, xq, xk, xv, mask, w_out, out):
                 o_words_of[j] = rows_to_words(
                     [o_of[j][:, a * GROUP_HEADS : (a + 1) * GROUP_HEADS, :].rearrange("p h d -> p (h d)") for a in range(2)]
                 )
-            if r == 0:
-                transpose_k(1)
             if r + 2 < PAIRS:
                 transpose_k(r + 2)
             if r % HALF_UNITS == Q_PHASE and r // HALF_UNITS + 1 < 2 * TILES:

@@ -44,7 +44,7 @@ WR = ()
 WARM2 = 2
 SPLIT = True
 PRODF = True
-TB = 2
+TB = 3
 TBN = 99
 STORE_FIRST = True
 EARLY = 99
@@ -54,7 +54,7 @@ Q_PHASE = 2
 H3 = 34
 GS, SS, SE, VE = 2, 99, 99, 16
 MASK_ROUNDS = (3, 9, 17)
-V_OUT = 33
+V_OUT = 32
 GROUPED_BUFS = {"gpsimd": 1, "vector": 2, "scalar": 3}
 WIDTH = {"gpsimd": 256, "vector": 128, "scalar": 128}
 ENGINE_ROUNDS = (("vector", 0, VE), ("gpsimd", GS, 40), ("scalar", SS, SE))
@@ -361,8 +361,8 @@ def tile_mptattentionfused_pa_kernel(tc, xq, xk, xv, mask, w_out, out):
                 e_of[n].append(e_sb)
 
         def rows_to_words(rows):
-            words_ps = psum.tile([P, 2, 2, P], F32, tag="tr", bufs=2, name="words_ps")
-            for a in range(2):
+            words_ps = psum.tile([P, len(rows), 2, P], F32, tag="tr", bufs=2, name="words_ps")
+            for a in range(len(rows)):
                 for u in range(2):
                     nc.tensor.transpose(
                         words_ps[:, a, u, :], rows[a].bitcast(F32)[:, u * P : (u + 1) * P], ident_f[:]
@@ -370,9 +370,10 @@ def tile_mptattentionfused_pa_kernel(tc, xq, xk, xv, mask, w_out, out):
             return words_ps
 
         def words_to_grouped(words_ps, tag):
-            grouped = work.tile([P, 2 * P * PACK], BF16, tag=tag, bufs=2, align_bytes=64, name=tag)
+            tiles = words_ps[:].shape[1]
+            grouped = work.tile([P, tiles * P * PACK], BF16, tag=tag, bufs=2, align_bytes=64, name=tag)
             nc.scalar.copy(
-                out=grouped[:].bitcast(F32).rearrange("p (a i u) -> p a i u", a=2, u=2),
+                out=grouped[:].bitcast(F32).rearrange("p (a i u) -> p a i u", a=tiles, u=2),
                 in_=words_ps[:].rearrange("p a u i -> p a i u"),
             )
             return grouped
@@ -419,16 +420,16 @@ def tile_mptattentionfused_pa_kernel(tc, xq, xk, xv, mask, w_out, out):
                 op=ALU.mult,
             )
 
-        def quantise_o(j):
+        def quantise_o(j, first, last):
             it, half = divmod(j, 2)
             if half == 0:
                 o_codes = work.tile([P, GROUPS * P], U32, tag="o_codes", bufs=4, align_bytes=64, name="o_codes")
                 o_scales = work.tile([P, GROUPS * P], U8, tag="o_scales", bufs=4, align_bytes=64, name="o_scales")
                 o_mx_of[it] = (o_codes, o_scales)
             o_codes, o_scales = o_mx_of[it]
-            cols = slice(half * HALF_GROUPS * P, (half + 1) * HALF_GROUPS * P)
+            cols = slice((half * HALF_GROUPS + first) * P, (half * HALF_GROUPS + last) * P)
             nc.vector.quantize_mx(
-                out=o_codes[:, cols].bitcast(FP8X4), scales=o_scales[:, cols], in_=o_grouped_of[j][:]
+                out=o_codes[:, cols].bitcast(FP8X4), scales=o_scales[:, cols], in_=o_grouped_of[j, first][:]
             )
 
         acc_of = {}
@@ -501,6 +502,26 @@ def tile_mptattentionfused_pa_kernel(tc, xq, xk, xv, mask, w_out, out):
             r += 1
 
         assert max(project_in) < UNITS + 7
+        o_jobs = {2 * HALF_UNITS + HALF_UNITS * j: (j, 0, HALF_GROUPS) for j in range(2 * TILES - 1)}
+        o_jobs[UNITS + 2] = (2 * TILES - 1, 0, 1)
+        o_jobs[UNITS + 4] = (2 * TILES - 1, 1, 2)
+        late_tiles = [project_in.pop(r)[0] for r in sorted(project_in) if r > UNITS + 2]
+
+        def copy_o(r):
+            if r - 1 in o_jobs:
+                j, first, last = o_jobs[r - 1]
+                o_grouped_of[j, first] = words_to_grouped(o_words_of[j, first], "o_grouped")
+
+        def start_o_words(r):
+            if r in o_jobs:
+                j, first, last = o_jobs[r]
+                o_words_of[j, first] = rows_to_words(
+                    [
+                        o_of[j][:, a * GROUP_HEADS : (a + 1) * GROUP_HEADS, :].rearrange("p h d -> p (h d)")
+                        for a in range(first, last)
+                    ]
+                )
+
         o_words_of = {}
         e_words_of = {}
         def warm_up(passes):
@@ -519,7 +540,9 @@ def tile_mptattentionfused_pa_kernel(tc, xq, xk, xv, mask, w_out, out):
             move(nc.vector.tensor_copy if n == 2 else nc.scalar.copy)
         copies.clear()
         build_bias(0)
-        for r in range(UNITS + 7):
+        for r in range(UNITS + 6):
+            if r > UNITS:
+                copy_o(r)
             if r <= V_OUT and STORE_FIRST:
                 store_tiles(r - 1, nc.scalar.copy)
             if 0 <= r - 3 < UNITS:
@@ -527,9 +550,8 @@ def tile_mptattentionfused_pa_kernel(tc, xq, xk, xv, mask, w_out, out):
             for move in copies:
                 move(nc.scalar.copy)
             copies.clear()
-            if r >= 9 and (r - 9) % HALF_UNITS == 0 and (r - 9) // HALF_UNITS < 2 * TILES:
-                j = (r - 9) // HALF_UNITS
-                o_grouped_of[j] = words_to_grouped(o_words_of[j], "o_grouped")
+            if r <= UNITS:
+                copy_o(r)
             if r <= V_OUT and not STORE_FIRST:
                 store_tiles(r - 1, nc.scalar.copy)
             if r in jobs["gpsimd"]:
@@ -549,21 +571,24 @@ def tile_mptattentionfused_pa_kernel(tc, xq, xk, xv, mask, w_out, out):
                 quantise_chunk(*jobs["vector"][r - 1])
             if r + 1 < UNITS:
                 build_bias(r + 1)
-            if 0 <= r - 3 < UNITS:
-                quantise_e(r - 3)
             if r in jobs["vector"]:
                 regroup(*jobs["vector"][r], "vector")
             if r - 1 in jobs["scalar"]:
                 quantise_chunk(*jobs["scalar"][r - 1])
-            if r >= 9 and (r - 9) % HALF_UNITS == 0 and (r - 9) // HALF_UNITS < 2 * TILES:
-                quantise_o((r - 9) // HALF_UNITS)
+            if r - 1 in o_jobs:
+                quantise_o(*o_jobs[r - 1])
+            if r == UNITS + 5:
+                for n, (it, col) in enumerate(late_tiles):
+                    store(it, col, nc.scalar.copy if n % 2 == 0 else nc.vector.tensor_copy)
             if r in jobs["gpsimd"]:
                 quantise_chunk(*jobs["gpsimd"][r])
+            if 0 <= r - 3 < UNITS:
+                quantise_e(r - 3)
             if r < UNITS and not SPLIT:
                 multiply_scores(r, 0)
             if r < len(WR) and WR[r]:
                 warm_up(WR[r])
-            if r < UNITS and SPLIT:
+            if r < UNITS:
                 multiply_scores(r, 0)
                 add_bias(r, 0)
                 if EARLYP:
@@ -573,36 +598,38 @@ def tile_mptattentionfused_pa_kernel(tc, xq, xk, xv, mask, w_out, out):
                 if not EARLYP:
                     close_scores(r)
                 multiply_scores(r, 1)
+            if r == UNITS + 3:
+                project(TILES - 1, 3, ALL[:2], "s", 4)
             if 0 <= r - 4 < UNITS:
                 weighted_values(r - 4)
             if r in project_in:
                 project(*project_in[r][0], project_in[r][1], "acc", 1)
-            if H3 <= r < H3 + 4:
-                project(TILES - 1, r - H3, ALL[:2], "s", 4)
-            if r < UNITS and SPLIT:
-                add_bias(r, 1)
-            elif r < UNITS:
-                multiply_scores(r, 1)
-                add_bias(r, 0)
-                add_bias(r, 1)
-            if 0 <= r - 2 < UNITS and r - 2 not in e_words_of:
+            if UNITS <= r < UNITS + 2:
                 e_words_of[r - 2] = rows_to_words([e[:] for e in e_of[r - 2]])
-            if r >= 8 and (r - 8) % HALF_UNITS == 0 and (r - 8) // HALF_UNITS < 2 * TILES:
-                j = (r - 8) // HALF_UNITS
-                o_words_of[j] = rows_to_words(
-                    [o_of[j][:, a * GROUP_HEADS : (a + 1) * GROUP_HEADS, :].rearrange("p h d -> p (h d)") for a in range(2)]
-                )
+            if r == UNITS + 1:
+                for n in (0, 1):
+                    project(TILES - 1, n, ALL[:2], "s", 4)
+            if r == UNITS + 2:
+                project(TILES - 1, 2, ALL[:2], "s", 4)
+            if r == UNITS + 3:
+                project(*late_tiles[0], ALL, "acc", 1)
+            if r < UNITS:
+                add_bias(r, 1)
+            start_o_words(r)
+            if r == UNITS + 4:
+                for it, col in late_tiles[1:]:
+                    project(it, col, ALL, "tr", 2)
+                for n in range(N_TILES):
+                    project(TILES - 1, n, ALL[2:3], "s", 4)
             if r + 2 < PAIRS:
                 transpose_k(r + 2)
             if r % HALF_UNITS == Q_PHASE and r // HALF_UNITS + 1 < 2 * TILES:
                 transpose_q(r // HALF_UNITS + 1)
             if r in MASK_ROUNDS:
                 transpose_mask(1 + MASK_ROUNDS.index(r))
-            if r < UNITS and not (SPLIT and PRODF):
-                close_scores(r)
             if r >= V_OUT:
                 store_tiles(r, nc.vector.tensor_copy)
 
         for n in range(N_TILES):
-            project(TILES - 1, n, ALL[2:], "s", 4)
+            project(TILES - 1, n, ALL[3:], "s", 4)
             store(TILES - 1, n, nc.scalar.copy if n % 2 == 0 else nc.vector.tensor_copy)

@@ -37,6 +37,8 @@ SQRT_DIM = math.sqrt(HEAD_DIM)
 P0 = 2
 PX = ()
 WARM = 3
+SB = 4
+KV = 0
 EARLYP = True
 SSTEP, SPH = 2, 0
 BE = 6
@@ -211,7 +213,7 @@ def tile_mptattentionfused_pa_kernel(tc, xq, xk, xv, mask, w_out, out):
         o_mx_of = {}
 
         def transpose_mask(it):
-            mask_ps = psum.tile([P, TILES, P], BF16, tag="tr", bufs=2, name="mask_ps")
+            mask_ps = psum.tile([P, TILES, P], BF16, tag="tr", bufs=3, name="mask_ps")
             for t in range(TILES):
                 nc.tensor.transpose(mask_ps[:, t, :], mask_sb[:, it, t * P : (t + 1) * P], ident_bf[:])
             copies.append(lambda copy: nc.scalar.mul(out=mask_t[:, it, :, :], in_=mask_ps[:], mul=SQRT_DIM))
@@ -245,7 +247,7 @@ def tile_mptattentionfused_pa_kernel(tc, xq, xk, xv, mask, w_out, out):
             )
 
         def transpose_k(pair):
-            k_ps = psum.tile([P, PAIR, TILES, P], BF16, tag="tr", bufs=2, name="k_ps")
+            k_ps = psum.tile([P, PAIR, TILES, P], BF16, tag="tr", bufs=3, name="k_ps")
             for b in range(PAIR):
                 cols = slice(b * HEAD_DIM, (b + 1) * HEAD_DIM)
                 for t in range(TILES):
@@ -258,41 +260,45 @@ def tile_mptattentionfused_pa_kernel(tc, xq, xk, xv, mask, w_out, out):
             )
 
         def transpose_q(j):
-            q_ps = psum.tile([P, HALF_HEADS, P], BF16, tag="tr", bufs=2, name="q_ps")
+            q_ps = psum.tile([P, HALF_HEADS, P], BF16, tag="tr", bufs=3, name="q_ps")
             for a in range(HALF_HEADS):
                 nc.tensor.transpose(q_ps[:, a, :], q_raw[j][:, a * HEAD_DIM : (a + 1) * HEAD_DIM], ident_bf[:])
             q_t = work.tile([P, HALF_HEADS, P], BF16, tag="q_t", bufs=3, name="q_t")
             q_t_of[j] = q_t
             copies.append(lambda copy: copy(out=q_t[:], in_=q_ps[:]))
 
-        def bias_form(n, b):
-            if b == 1 and n >= P0 and (n not in project_in or n in PX):
-                return "product"
+        def has_product(n, b):
+            return b == 1 and n >= P0 and n not in project_in
+
+        def builder(n, b, t):
+            if has_product(n, b):
+                return None
             if b == 0 and BE <= n < BROADCAST_UNITS:
-                return "broadcast"
-            return "built"
+                return "scalar" if t >= SB else None
+            if b == 1 and t >= TB:
+                return "scalar"
+            return "vector"
 
         def build_bias(n):
             it, pair = divmod(n, PAIRS)
-            heads = [b for b in range(PAIR) if bias_form(n, b) == "built"]
-            if not heads:
+            blocks = [(b, t, builder(n, b, t)) for b in range(PAIR) for t in range(TILES) if builder(n, b, t)]
+            if not blocks:
                 return
             bias_of[n] = work.tile([P, PAIR, TILES, P], F32, tag="bias_t", bufs=3, name="bias_t")
-            for b in heads:
-                for t in range(TILES):
-                    out_t = bias_of[n][:, b, t, :]
-                    alibi_t = alibi[:, pair * PAIR + b, t : t + 1]
-                    if b == 1 and t >= TB and n < TBN:
-                        nc.scalar.activation(out=out_t, in_=mask_t[:, it, t, :], func=ACT.Identity, bias=alibi_t)
-                    else:
-                        nc.vector.tensor_scalar_add(out=out_t, in0=mask_t[:, it, t, :], scalar1=alibi_t)
+            for b, t, engine in blocks:
+                out_t = bias_of[n][:, b, t, :]
+                alibi_t = alibi[:, pair * PAIR + b, t : t + 1]
+                if engine == "scalar":
+                    nc.scalar.activation(out=out_t, in_=mask_t[:, it, t, :], func=ACT.Identity, bias=alibi_t)
+                else:
+                    nc.vector.tensor_scalar_add(out=out_t, in0=mask_t[:, it, t, :], scalar1=alibi_t)
 
         def open_group(n):
             scores_of.setdefault(n, []).append(psum.tile([P, SEQ], F32, tag="s", bufs=4, name="s_ps"))
 
         def multiply_scores(n, b):
             h = (n % PAIRS) * PAIR + b
-            product = bias_form(n, b) == "product"
+            product = has_product(n, b)
             if not product:
                 open_group(n)
             nc.tensor.matmul(
@@ -305,12 +311,14 @@ def tile_mptattentionfused_pa_kernel(tc, xq, xk, xv, mask, w_out, out):
 
         def add_bias(n, b):
             it, pair = divmod(n, PAIRS)
-            form = bias_form(n, b)
             added = []
             for t in range(TILES):
-                if form == "broadcast":
-                    added.append((t, alibi[:, pair * PAIR + b, t : t + 1].to_broadcast([P, P])))
-                added.append((t, bias_of[n][:, b, t, :] if form == "built" else mask_t[:, it, t, :]))
+                if builder(n, b, t):
+                    added.append((t, bias_of[n][:, b, t, :]))
+                else:
+                    added.append((t, mask_t[:, it, t, :]))
+                    if not has_product(n, b):
+                        added.append((t, alibi[:, pair * PAIR + b, t : t + 1].to_broadcast([P, P])))
             for m, (t, rows) in enumerate(added):
                 nc.tensor.matmul(
                     out=scores_of[n][b][:, t * P : (t + 1) * P],
@@ -318,12 +326,12 @@ def tile_mptattentionfused_pa_kernel(tc, xq, xk, xv, mask, w_out, out):
                     rhs=ident_f[:],
                     is_transpose=True,
                     start=False,
-                    stop=((PRODF or form != "product") and m == len(added) - 1),
+                    stop=(m == len(added) - 1),
                 )
 
         def close_scores(n):
             for b in range(PAIR):
-                if bias_form(n, b) == "product":
+                if has_product(n, b):
                     h = (n % PAIRS) * PAIR + b
                     open_group(n)
                     nc.tensor.matmul(
@@ -361,7 +369,7 @@ def tile_mptattentionfused_pa_kernel(tc, xq, xk, xv, mask, w_out, out):
                 e_of[n].append(e_sb)
 
         def rows_to_words(rows):
-            words_ps = psum.tile([P, len(rows), 2, P], F32, tag="tr", bufs=2, name="words_ps")
+            words_ps = psum.tile([P, len(rows), 2, P], F32, tag="tr", bufs=3, name="words_ps")
             for a in range(len(rows)):
                 for u in range(2):
                     nc.tensor.transpose(
@@ -525,7 +533,7 @@ def tile_mptattentionfused_pa_kernel(tc, xq, xk, xv, mask, w_out, out):
         o_words_of = {}
         e_words_of = {}
         def warm_up(passes):
-            warm = psum.tile([P, P], F32, tag="acc", bufs=1, name="warm")
+            warm = psum.tile([P, P], F32, tag="tr", bufs=3, name="warm")
             for m in range(passes):
                 nc.tensor.matmul(out=warm[:], lhsT=ident_f[:], rhs=ident_f[:], start=True, stop=True)
 
@@ -548,7 +556,7 @@ def tile_mptattentionfused_pa_kernel(tc, xq, xk, xv, mask, w_out, out):
             if 0 <= r - 3 < UNITS:
                 e_grouped_of[r - 3] = words_to_grouped(e_words_of[r - 3], "e_grouped")
             for move in copies:
-                move(nc.scalar.copy)
+                move(nc.vector.tensor_copy if r <= KV else nc.scalar.copy)
             copies.clear()
             if r <= UNITS:
                 copy_o(r)
@@ -603,7 +611,7 @@ def tile_mptattentionfused_pa_kernel(tc, xq, xk, xv, mask, w_out, out):
             if 0 <= r - 4 < UNITS:
                 weighted_values(r - 4)
             if r in project_in:
-                project(*project_in[r][0], project_in[r][1], "acc", 1)
+                project(*project_in[r][0], project_in[r][1], "tr", 3)
             if UNITS <= r < UNITS + 2:
                 e_words_of[r - 2] = rows_to_words([e[:] for e in e_of[r - 2]])
             if r == UNITS + 1:
@@ -612,13 +620,13 @@ def tile_mptattentionfused_pa_kernel(tc, xq, xk, xv, mask, w_out, out):
             if r == UNITS + 2:
                 project(TILES - 1, 2, ALL[:2], "s", 4)
             if r == UNITS + 3:
-                project(*late_tiles[0], ALL, "acc", 1)
+                project(*late_tiles[0], ALL, "tr", 3)
             if r < UNITS:
                 add_bias(r, 1)
             start_o_words(r)
             if r == UNITS + 4:
                 for it, col in late_tiles[1:]:
-                    project(it, col, ALL, "tr", 2)
+                    project(it, col, ALL, "tr", 3)
                 for n in range(N_TILES):
                     project(TILES - 1, n, ALL[2:3], "s", 4)
             if r + 2 < PAIRS:

@@ -35,18 +35,21 @@ N_TILE = 512
 N_TILES = N_OUT // N_TILE
 SQRT_DIM = math.sqrt(HEAD_DIM)
 P0 = 2
+PM = 29
 PX = ()
 WARM = 3
+WS = (0, 0, 0)
+VB = 0
 SB = 4
 KV = 0
 EARLYP = True
 SSTEP, SPH = 2, 0
-BE = 6
-WR = ()
+BE = 8
+WR = (0,0,2,2)
 WARM2 = 2
 SPLIT = True
 PRODF = True
-TB = 3
+TB = 2
 TBN = 99
 STORE_FIRST = True
 EARLY = 99
@@ -55,7 +58,7 @@ WHOLE_FROM = 34
 Q_PHASE = 2
 H3 = 34
 GS, SS, SE, VE = 2, 99, 99, 16
-MASK_ROUNDS = (3, 9, 17)
+MASK_ROUNDS = (3, 12, 20)
 V_OUT = 32
 GROUPED_BUFS = {"gpsimd": 1, "vector": 2, "scalar": 3}
 WIDTH = {"gpsimd": 256, "vector": 128, "scalar": 128}
@@ -196,6 +199,7 @@ def tile_mptattentionfused_pa_kernel(tc, xq, xk, xv, mask, w_out, out):
         mask_t = keep.tile([P, TILES, TILES, P], F32)
 
         grouped_of = {}
+        warm_of = []
         copies = []
         q_t_of = {}
         bias_of = {}
@@ -268,15 +272,15 @@ def tile_mptattentionfused_pa_kernel(tc, xq, xk, xv, mask, w_out, out):
             copies.append(lambda copy: copy(out=q_t[:], in_=q_ps[:]))
 
         def has_product(n, b):
-            return b == 1 and n >= P0 and n not in project_in
+            return b == 1 and P0 <= n < PM and n not in project_in
 
         def builder(n, b, t):
             if has_product(n, b):
                 return None
             if b == 0 and BE <= n < BROADCAST_UNITS:
-                return "scalar" if t >= SB else None
+                return "scalar" if t >= SB else ("vector" if t < VB else None)
             if b == 1 and t >= TB:
-                return "scalar"
+                return None
             return "vector"
 
         def build_bias(n):
@@ -354,7 +358,9 @@ def tile_mptattentionfused_pa_kernel(tc, xq, xk, xv, mask, w_out, out):
             shift_of[n] = shift
 
         def exponentials(n):
-            sums_of[n] = work.tile([P, PAIR], F32, tag="row_sum", bufs=6, name="row_sum")
+            k, m = divmod(n, 2)
+            if m == 0:
+                sums_of[k] = work.tile([P, 2, PAIR], F32, tag="row_sum", bufs=4, name="row_sum")
             e_of[n] = []
             for b in range(PAIR):
                 e_sb = work.tile([P, SEQ], BF16, tag="e_sb", bufs=6, name="e_sb")
@@ -364,7 +370,7 @@ def tile_mptattentionfused_pa_kernel(tc, xq, xk, xv, mask, w_out, out):
                     func=ACT.Exp,
                     bias=shift_of[n][:, b : b + 1],
                     scale=1.0 / SQRT_DIM,
-                    accum_out=sums_of[n][:, b : b + 1],
+                    accum_out=sums_of[k][:, m, b : b + 1],
                 )
                 e_of[n].append(e_sb)
 
@@ -387,8 +393,8 @@ def tile_mptattentionfused_pa_kernel(tc, xq, xk, xv, mask, w_out, out):
             return grouped
 
         def quantise_e(n):
-            e_codes = work.tile([P, PAIR * P], U32, tag="e_codes", bufs=2, align_bytes=64, name="e_codes")
-            e_scales = work.tile([P, PAIR * P], U8, tag="e_scales", bufs=2, align_bytes=64, name="e_scales")
+            e_codes = work.tile([P, PAIR * P], U32, tag="e_codes", bufs=4, align_bytes=64, name="e_codes")
+            e_scales = work.tile([P, PAIR * P], U8, tag="e_scales", bufs=4, align_bytes=64, name="e_scales")
             nc.vector.quantize_mx(out=e_codes[:].bitcast(FP8X4), scales=e_scales[:], in_=e_grouped_of[n][:])
             e_mx_of[n] = (e_codes, e_scales)
 
@@ -411,10 +417,10 @@ def tile_mptattentionfused_pa_kernel(tc, xq, xk, xv, mask, w_out, out):
                     stop=True,
                 )
 
-        def invert_sums(n):
-            inv_sum = work.tile([P, PAIR], F32, tag="inv_sum", bufs=3, name="inv_sum")
-            nc.vector.reciprocal(out=inv_sum[:], in_=sums_of[n][:])
-            inv_of[n] = inv_sum
+        def invert_sums(k):
+            inv_sum = work.tile([P, 2, PAIR], F32, tag="inv_sum", bufs=3, name="inv_sum")
+            nc.vector.reciprocal(out=inv_sum[:], in_=sums_of[k][:])
+            inv_of[k] = inv_sum
 
         def normalise(n):
             k, m = divmod(n, 2)
@@ -424,7 +430,7 @@ def tile_mptattentionfused_pa_kernel(tc, xq, xk, xv, mask, w_out, out):
             nc.vector.tensor_tensor(
                 out=o_of[j][:, u * PAIR : (u + 1) * PAIR, :],
                 in0=pv_of[k][:, m, :, :],
-                in1=inv_of[n][:].unsqueeze(2).to_broadcast([P, PAIR, HEAD_DIM]),
+                in1=inv_of[k][:, m, :].unsqueeze(2).to_broadcast([P, PAIR, HEAD_DIM]),
                 op=ALU.mult,
             )
 
@@ -493,7 +499,7 @@ def tile_mptattentionfused_pa_kernel(tc, xq, xk, xv, mask, w_out, out):
 
         project_in = {}
         waiting = sorted(
-            (max(PAIRS * it + 14, 2 + max(last_round_of[N_TILES + GROUPS * n + g] for g in range(GROUPS))), it, n)
+            (max(PAIRS * it + 15, 2 + max(last_round_of[N_TILES + GROUPS * n + g] for g in range(GROUPS))), it, n)
             for it in range(TILES - 1)
             for n in range(N_TILES)
         )
@@ -510,10 +516,22 @@ def tile_mptattentionfused_pa_kernel(tc, xq, xk, xv, mask, w_out, out):
             r += 1
 
         assert max(project_in) < UNITS + 7
-        o_jobs = {2 * HALF_UNITS + HALF_UNITS * j: (j, 0, HALF_GROUPS) for j in range(2 * TILES - 1)}
+        o_jobs = {2 * HALF_UNITS + HALF_UNITS * j + (1 if j < 6 else 0): (j, 0, HALF_GROUPS) for j in range(2 * TILES - 1)}
         o_jobs[UNITS + 2] = (2 * TILES - 1, 0, 1)
         o_jobs[UNITS + 4] = (2 * TILES - 1, 1, 2)
         late_tiles = [project_in.pop(r)[0] for r in sorted(project_in) if r > UNITS + 2]
+
+        def pv_units(r):
+            if r >= UNITS:
+                return [r - 4] if r - 4 < UNITS else []
+            return [r - 5, r - 4] if r % 2 == 1 and r >= 5 else []
+
+        def norm_units(r):
+            if r > UNITS:
+                return [r - 5] if r - 5 < UNITS else []
+            if r == UNITS:
+                return [r - 6, r - 5]
+            return [r - 6] if r >= 6 else []
 
         def copy_o(r):
             if r - 1 in o_jobs:
@@ -533,14 +551,18 @@ def tile_mptattentionfused_pa_kernel(tc, xq, xk, xv, mask, w_out, out):
         o_words_of = {}
         e_words_of = {}
         def warm_up(passes):
-            warm = psum.tile([P, P], F32, tag="tr", bufs=3, name="warm")
+            if passes:
+                warm_of.append(psum.tile([P, P], F32, tag="pv", bufs=1, name="warm") if not warm_of else warm_of[0])
             for m in range(passes):
-                nc.tensor.matmul(out=warm[:], lhsT=ident_f[:], rhs=ident_f[:], start=True, stop=True)
+                nc.tensor.matmul(out=warm_of[0][:], lhsT=ident_f[:], rhs=ident_f[:], start=True, stop=True)
 
         warm_up(WARM)
         transpose_mask(0)
+        warm_up(WS[0])
         transpose_k(0)
+        warm_up(WS[1])
         transpose_q(0)
+        warm_up(WS[2])
         transpose_k(1)
         if WARM2:
             warm_up(WARM2)
@@ -564,8 +586,8 @@ def tile_mptattentionfused_pa_kernel(tc, xq, xk, xv, mask, w_out, out):
                 store_tiles(r - 1, nc.scalar.copy)
             if r in jobs["gpsimd"]:
                 regroup(*jobs["gpsimd"][r], "gpsimd")
-            if 0 <= r - 5 < UNITS:
-                normalise(r - 5)
+            for n in norm_units(r):
+                normalise(n)
             if 0 <= r - 1 < UNITS:
                 row_maxima(r - 1)
             if 0 <= r - 1 < UNITS:
@@ -573,8 +595,8 @@ def tile_mptattentionfused_pa_kernel(tc, xq, xk, xv, mask, w_out, out):
                 exponentials(r - 1)
             if r in jobs["scalar"]:
                 regroup(*jobs["scalar"][r], "scalar")
-            if 0 <= r - 4 < UNITS:
-                invert_sums(r - 4)
+            if 0 <= r - 4 < UNITS and r % 2 == 0:
+                invert_sums((r - 4) // 2)
             if r - 1 in jobs["vector"]:
                 quantise_chunk(*jobs["vector"][r - 1])
             if r + 1 < UNITS:
@@ -608,8 +630,8 @@ def tile_mptattentionfused_pa_kernel(tc, xq, xk, xv, mask, w_out, out):
                 multiply_scores(r, 1)
             if r == UNITS + 3:
                 project(TILES - 1, 3, ALL[:2], "s", 4)
-            if 0 <= r - 4 < UNITS:
-                weighted_values(r - 4)
+            for n in pv_units(r):
+                weighted_values(n)
             if r in project_in:
                 project(*project_in[r][0], project_in[r][1], "tr", 3)
             if UNITS <= r < UNITS + 2:

@@ -34,36 +34,17 @@ HALF_GROUPS = HALF_HEADS // GROUP_HEADS
 N_TILE = 512
 N_TILES = N_OUT // N_TILE
 SQRT_DIM = math.sqrt(HEAD_DIM)
-P0 = 2
-PM = 29
-PX = ()
-WARM = 3
-WS = (0, 0, 0)
-VB = 0
-SB = 4
-KV = 0
-EARLYP = True
-SSTEP, SPH = 2, 0
-BE = 8
-WR = (0,0,2,2)
-WARM2 = 2
-SPLIT = True
-PRODF = True
+P0, PM = 2, 29
+BE, BU = 8, 18
 TB = 2
-TBN = 99
-STORE_FIRST = True
-EARLY = 99
-BC_STEP = 99
-WHOLE_FROM = 34
+TE, TA = 4, 3
+WIDTH = {"gpsimd": 256, "vector": 128}
+GROUPED_BUFS = {"gpsimd": 1, "vector": 2}
+VE, GS = 16, 2
 Q_PHASE = 2
-H3 = 34
-GS, SS, SE, VE = 2, 99, 99, 16
 MASK_ROUNDS = (3, 12, 20)
-V_OUT = 32
-GROUPED_BUFS = {"gpsimd": 1, "vector": 2, "scalar": 3}
-WIDTH = {"gpsimd": 256, "vector": 128, "scalar": 128}
-ENGINE_ROUNDS = (("vector", 0, VE), ("gpsimd", GS, 40), ("scalar", SS, SE))
-BROADCAST_UNITS = 18
+WARM_ROUNDS = (2, 3)
+WARM, WARM2 = 3, 2
 
 FLOPS = 2 * 2 * HEADS * SEQ * SEQ * HEAD_DIM + 2 * SEQ * FEATURES * N_OUT
 
@@ -144,6 +125,9 @@ def tile_mptattentionfused_pa_kernel(tc, xq, xk, xv, mask, w_out, out):
         ident_bf = keep.tile([P, P], BF16)
         make_identity(nc, ident_bf[:])
 
+        table = keep.tile([P, 1], F32)
+        nc.scalar.activation(out=table[:], in_=ones[:], func=ACT.Exp)
+
         amp = keep.tile([P, HEADS], F32)
         for h in range(HEADS):
             nc.scalar.mul(out=amp[:, h : h + 1], in_=ones[:], mul=2.0 ** (-(h + 1) / 2) * SQRT_DIM)
@@ -215,6 +199,9 @@ def tile_mptattentionfused_pa_kernel(tc, xq, xk, xv, mask, w_out, out):
         o_of = {}
         o_grouped_of = {}
         o_mx_of = {}
+        e_words_of = {}
+        o_words_of = {}
+        acc_of = {}
 
         def transpose_mask(it):
             mask_ps = psum.tile([P, TILES, P], BF16, tag="tr", bufs=3, name="mask_ps")
@@ -231,10 +218,8 @@ def tile_mptattentionfused_pa_kernel(tc, xq, xk, xv, mask, w_out, out):
                 nc.gpsimd.tensor_scalar(
                     out=grouped[:], in0=rows, scalar1=1.0, scalar2=0.0, op0=ALU.mult, op1=ALU.add
                 )
-            elif engine == "vector":
-                nc.vector.tensor_copy(out=grouped[:], in_=rows)
             else:
-                nc.scalar.copy(out=grouped[:], in_=rows)
+                nc.vector.tensor_copy(out=grouped[:], in_=rows)
             grouped_of[c, first] = grouped
 
         def quantise_chunk(c, first, width):
@@ -274,28 +259,25 @@ def tile_mptattentionfused_pa_kernel(tc, xq, xk, xv, mask, w_out, out):
         def has_product(n, b):
             return b == 1 and P0 <= n < PM and n not in project_in
 
-        def builder(n, b, t):
+        def is_built(n, b, t):
             if has_product(n, b):
-                return None
-            if b == 0 and BE <= n < BROADCAST_UNITS:
-                return "scalar" if t >= SB else ("vector" if t < VB else None)
-            if b == 1 and t >= TB:
-                return None
-            return "vector"
+                return False
+            if b == 1:
+                return t < TB
+            return t < TE if n < BE else n >= BU and t < TA
 
         def build_bias(n):
             it, pair = divmod(n, PAIRS)
-            blocks = [(b, t, builder(n, b, t)) for b in range(PAIR) for t in range(TILES) if builder(n, b, t)]
+            blocks = [(b, t) for b in range(PAIR) for t in range(TILES) if is_built(n, b, t)]
             if not blocks:
                 return
             bias_of[n] = work.tile([P, PAIR, TILES, P], F32, tag="bias_t", bufs=3, name="bias_t")
-            for b, t, engine in blocks:
-                out_t = bias_of[n][:, b, t, :]
-                alibi_t = alibi[:, pair * PAIR + b, t : t + 1]
-                if engine == "scalar":
-                    nc.scalar.activation(out=out_t, in_=mask_t[:, it, t, :], func=ACT.Identity, bias=alibi_t)
-                else:
-                    nc.vector.tensor_scalar_add(out=out_t, in0=mask_t[:, it, t, :], scalar1=alibi_t)
+            for b, t in blocks:
+                nc.vector.tensor_scalar_add(
+                    out=bias_of[n][:, b, t, :],
+                    in0=mask_t[:, it, t, :],
+                    scalar1=alibi[:, pair * PAIR + b, t : t + 1],
+                )
 
         def open_group(n):
             scores_of.setdefault(n, []).append(psum.tile([P, SEQ], F32, tag="s", bufs=4, name="s_ps"))
@@ -317,7 +299,7 @@ def tile_mptattentionfused_pa_kernel(tc, xq, xk, xv, mask, w_out, out):
             it, pair = divmod(n, PAIRS)
             added = []
             for t in range(TILES):
-                if builder(n, b, t):
+                if is_built(n, b, t):
                     added.append((t, bias_of[n][:, b, t, :]))
                 else:
                     added.append((t, mask_t[:, it, t, :]))
@@ -446,7 +428,6 @@ def tile_mptattentionfused_pa_kernel(tc, xq, xk, xv, mask, w_out, out):
                 out=o_codes[:, cols].bitcast(FP8X4), scales=o_scales[:, cols], in_=o_grouped_of[j, first][:]
             )
 
-        acc_of = {}
 
         def project(it, n, groups, tag, bufs):
             o_codes, o_scales = o_mx_of[it]
@@ -470,32 +451,26 @@ def tile_mptattentionfused_pa_kernel(tc, xq, xk, xv, mask, w_out, out):
             copy(out=result[:], in_=acc_of[it, n][:])
             nc.sync.dma_start(out=out_rows[it][:, n * N_TILE : (n + 1) * N_TILE], in_=result[:])
 
-        def store_tiles(r, copy):
-            if r in project_in and project_in[r][1][-1] == GROUPS - 1:
-                store(*project_in[r][0], copy)
-
         CHUNKS = (1 + GROUPS) * N_TILES
         ALL = tuple(range(GROUPS))
-        HALF_CHUNK = N_TILE // 2
-        jobs = {"gpsimd": {}, "vector": {}, "scalar": {}}
-        in_hand = {"gpsimd": None, "vector": None, "scalar": None}
-        next_chunk = 0
+
+        jobs = {"vector": {}, "gpsimd": {}}
+        in_hand = {}
         last_round_of = {}
-        for r in range(60):
-            for engine, first_round, last_round in ENGINE_ROUNDS:
-                if engine == "scalar" and r % SSTEP != SPH:
-                    continue
-                if not first_round <= r < last_round and in_hand[engine] is None:
-                    continue
-                if in_hand[engine] is None and next_chunk < CHUNKS:
+        next_chunk = 0
+        for r in range(UNITS + 4):
+            for engine, first_round, last_round in (("vector", 0, VE), ("gpsimd", GS, UNITS + 4)):
+                if engine not in in_hand and first_round <= r < last_round and next_chunk < CHUNKS:
                     in_hand[engine] = (next_chunk, 0)
                     next_chunk += 1
-                if in_hand[engine] is not None:
+                if engine in in_hand:
                     c, first = in_hand[engine]
-                    width = WIDTH[engine]
-                    jobs[engine][r] = (c, first, width)
+                    jobs[engine][r] = (c, first, WIDTH[engine])
                     last_round_of[c] = r
-                    in_hand[engine] = (c, first + width) if first + width < N_TILE else None
+                    if first + WIDTH[engine] < N_TILE:
+                        in_hand[engine] = (c, first + WIDTH[engine])
+                    else:
+                        in_hand.pop(engine)
 
         project_in = {}
         waiting = sorted(
@@ -503,35 +478,25 @@ def tile_mptattentionfused_pa_kernel(tc, xq, xk, xv, mask, w_out, out):
             for it in range(TILES - 1)
             for n in range(N_TILES)
         )
+        late_tiles = []
         r = 0
         while waiting:
             if waiting[0][0] <= r:
-                ready, it, n = waiting.pop(0)
-                if r + 1 + len(waiting) < WHOLE_FROM:
-                    project_in[r] = ((it, n), ALL[:2])
-                    project_in[r + 1] = ((it, n), ALL[2:])
+                it, n = waiting.pop(0)[1:]
+                if r + 1 + len(waiting) < UNITS + 2:
+                    project_in[r] = (it, n, ALL[:2])
+                    project_in[r + 1] = (it, n, ALL[2:])
                     r += 1
+                elif r <= UNITS + 2:
+                    project_in[r] = (it, n, ALL)
                 else:
-                    project_in[r] = ((it, n), ALL)
+                    late_tiles.append((it, n))
             r += 1
 
-        assert max(project_in) < UNITS + 7
-        o_jobs = {2 * HALF_UNITS + HALF_UNITS * j + (1 if j < 6 else 0): (j, 0, HALF_GROUPS) for j in range(2 * TILES - 1)}
+        o_jobs = {9 + HALF_UNITS * j: (j, 0, HALF_GROUPS) for j in range(2 * TILES - 2)}
+        o_jobs[UNITS] = (2 * TILES - 2, 0, HALF_GROUPS)
         o_jobs[UNITS + 2] = (2 * TILES - 1, 0, 1)
         o_jobs[UNITS + 4] = (2 * TILES - 1, 1, 2)
-        late_tiles = [project_in.pop(r)[0] for r in sorted(project_in) if r > UNITS + 2]
-
-        def pv_units(r):
-            if r >= UNITS:
-                return [r - 4] if r - 4 < UNITS else []
-            return [r - 5, r - 4] if r % 2 == 1 and r >= 5 else []
-
-        def norm_units(r):
-            if r > UNITS:
-                return [r - 5] if r - 5 < UNITS else []
-            if r == UNITS:
-                return [r - 6, r - 5]
-            return [r - 6] if r >= 6 else []
 
         def copy_o(r):
             if r - 1 in o_jobs:
@@ -548,53 +513,41 @@ def tile_mptattentionfused_pa_kernel(tc, xq, xk, xv, mask, w_out, out):
                     ]
                 )
 
-        o_words_of = {}
-        e_words_of = {}
-        def warm_up(passes):
-            if passes:
-                warm_of.append(psum.tile([P, P], F32, tag="pv", bufs=1, name="warm") if not warm_of else warm_of[0])
-            for m in range(passes):
-                nc.tensor.matmul(out=warm_of[0][:], lhsT=ident_f[:], rhs=ident_f[:], start=True, stop=True)
+        def start_e_words(n):
+            if 0 <= n < UNITS:
+                e_words_of[n] = rows_to_words([e[:] for e in e_of[n]])
 
-        warm_up(WARM)
-        transpose_mask(0)
-        warm_up(WS[0])
-        transpose_k(0)
-        warm_up(WS[1])
-        transpose_q(0)
-        warm_up(WS[2])
-        transpose_k(1)
-        if WARM2:
-            warm_up(WARM2)
-        for n, move in enumerate(copies):
-            move(nc.vector.tensor_copy if n == 2 else nc.scalar.copy)
-        copies.clear()
-        build_bias(0)
-        for r in range(UNITS + 6):
+        def last_tile(n, groups):
+            project(TILES - 1, n, groups, "s", 4)
+
+        def store_finished(r, copy):
+            if r in project_in:
+                it, n, groups = project_in[r]
+                if groups[-1] == GROUPS - 1:
+                    store(it, n, copy)
+
+        def scalar_copies(r):
             if r > UNITS:
                 copy_o(r)
-            if r <= V_OUT and STORE_FIRST:
-                store_tiles(r - 1, nc.scalar.copy)
+            if r <= UNITS:
+                store_finished(r - 1, nc.scalar.copy)
             if 0 <= r - 3 < UNITS:
                 e_grouped_of[r - 3] = words_to_grouped(e_words_of[r - 3], "e_grouped")
             for move in copies:
-                move(nc.vector.tensor_copy if r <= KV else nc.scalar.copy)
+                move(nc.scalar.copy)
             copies.clear()
             if r <= UNITS:
                 copy_o(r)
-            if r <= V_OUT and not STORE_FIRST:
-                store_tiles(r - 1, nc.scalar.copy)
+
+        def vector_and_softmax(r):
             if r in jobs["gpsimd"]:
                 regroup(*jobs["gpsimd"][r], "gpsimd")
             for n in norm_units(r):
                 normalise(n)
             if 0 <= r - 1 < UNITS:
                 row_maxima(r - 1)
-            if 0 <= r - 1 < UNITS:
                 shifts(r - 1)
                 exponentials(r - 1)
-            if r in jobs["scalar"]:
-                regroup(*jobs["scalar"][r], "scalar")
             if 0 <= r - 4 < UNITS and r % 2 == 0:
                 invert_sums((r - 4) // 2)
             if r - 1 in jobs["vector"]:
@@ -603,63 +556,97 @@ def tile_mptattentionfused_pa_kernel(tc, xq, xk, xv, mask, w_out, out):
                 build_bias(r + 1)
             if r in jobs["vector"]:
                 regroup(*jobs["vector"][r], "vector")
-            if r - 1 in jobs["scalar"]:
-                quantise_chunk(*jobs["scalar"][r - 1])
             if r - 1 in o_jobs:
                 quantise_o(*o_jobs[r - 1])
             if r == UNITS + 5:
-                for n, (it, col) in enumerate(late_tiles):
-                    store(it, col, nc.scalar.copy if n % 2 == 0 else nc.vector.tensor_copy)
+                for m, (it, n) in enumerate(late_tiles):
+                    store(it, n, nc.scalar.copy if m % 2 == 0 else nc.vector.tensor_copy)
             if r in jobs["gpsimd"]:
                 quantise_chunk(*jobs["gpsimd"][r])
             if 0 <= r - 3 < UNITS:
                 quantise_e(r - 3)
-            if r < UNITS and not SPLIT:
-                multiply_scores(r, 0)
-            if r < len(WR) and WR[r]:
-                warm_up(WR[r])
-            if r < UNITS:
-                multiply_scores(r, 0)
-                add_bias(r, 0)
-                if EARLYP:
-                    close_scores(r)
-                if 0 <= r - 2 < UNITS:
-                    e_words_of[r - 2] = rows_to_words([e[:] for e in e_of[r - 2]])
-                if not EARLYP:
-                    close_scores(r)
-                multiply_scores(r, 1)
-            if r == UNITS + 3:
-                project(TILES - 1, 3, ALL[:2], "s", 4)
+
+        def mx_passes(r):
             for n in pv_units(r):
                 weighted_values(n)
             if r in project_in:
-                project(*project_in[r][0], project_in[r][1], "tr", 3)
-            if UNITS <= r < UNITS + 2:
-                e_words_of[r - 2] = rows_to_words([e[:] for e in e_of[r - 2]])
-            if r == UNITS + 1:
-                for n in (0, 1):
-                    project(TILES - 1, n, ALL[:2], "s", 4)
-            if r == UNITS + 2:
-                project(TILES - 1, 2, ALL[:2], "s", 4)
-            if r == UNITS + 3:
-                project(*late_tiles[0], ALL, "tr", 3)
-            if r < UNITS:
-                add_bias(r, 1)
+                project(*project_in[r], "tr", 3)
+
+        def pv_units(r):
+            if r >= UNITS:
+                return [r - 4] if r - 4 < UNITS else []
+            return [r - 5, r - 4] if r % 2 == 1 and r >= 5 else []
+
+        def norm_units(r):
+            if r > UNITS:
+                return [r - 5] if r - 5 < UNITS else []
+            if r == UNITS:
+                return [r - 6, r - 5]
+            return [r - 6] if r >= 6 else []
+
+        def tensor_round(r):
+            if r in WARM_ROUNDS:
+                warm_up(2)
+            multiply_scores(r, 0)
+            add_bias(r, 0)
+            close_scores(r)
+            start_e_words(r - 2)
+            multiply_scores(r, 1)
+            mx_passes(r)
+            add_bias(r, 1)
             start_o_words(r)
-            if r == UNITS + 4:
-                for it, col in late_tiles[1:]:
-                    project(it, col, ALL, "tr", 3)
-                for n in range(N_TILES):
-                    project(TILES - 1, n, ALL[2:3], "s", 4)
             if r + 2 < PAIRS:
                 transpose_k(r + 2)
             if r % HALF_UNITS == Q_PHASE and r // HALF_UNITS + 1 < 2 * TILES:
                 transpose_q(r // HALF_UNITS + 1)
             if r in MASK_ROUNDS:
                 transpose_mask(1 + MASK_ROUNDS.index(r))
-            if r >= V_OUT:
-                store_tiles(r, nc.vector.tensor_copy)
+
+        def tensor_drain(r):
+            m = r - UNITS
+            if m == 3:
+                last_tile(3, ALL[:2])
+            mx_passes(r)
+            start_e_words(r - 2)
+            if m == 1:
+                last_tile(0, ALL[:2])
+                last_tile(1, ALL[:2])
+            if m == 2:
+                last_tile(2, ALL[:2])
+            if m == 3:
+                for it, n in late_tiles[:1]:
+                    project(it, n, ALL, "tr", 3)
+            start_o_words(r)
+            if m == 4:
+                for it, n in late_tiles[1:]:
+                    project(it, n, ALL, "tr", 3)
+                for n in range(N_TILES):
+                    last_tile(n, ALL[2:3])
+            store_finished(r, nc.vector.tensor_copy)
+
+        def warm_up(passes):
+            warm = psum.tile([P, P], F32, tag="tr", bufs=3, name="warm")
+            for m in range(passes):
+                nc.tensor.matmul(out=warm[:], lhsT=ident_f[:], rhs=ident_f[:], start=True, stop=True)
+
+        warm_up(WARM)
+        transpose_mask(0)
+        transpose_k(0)
+        transpose_q(0)
+        transpose_k(1)
+        warm_up(WARM2)
+        for m, move in enumerate(copies):
+            move(nc.vector.tensor_copy if m == 2 else nc.scalar.copy)
+        copies.clear()
+        build_bias(0)
+        for r in range(UNITS + 6):
+            scalar_copies(r)
+            vector_and_softmax(r)
+            if r < UNITS:
+                tensor_round(r)
+            else:
+                tensor_drain(r)
 
         for n in range(N_TILES):
-            project(TILES - 1, n, ALL[3:], "s", 4)
+            last_tile(n, ALL[3:])
             store(TILES - 1, n, nc.scalar.copy if n % 2 == 0 else nc.vector.tensor_copy)

@@ -219,7 +219,10 @@ def tile_mptattentionfused_pa_kernel(tc, xq, xk, xv, mask, w_out, out):
                     out=grouped[:], in0=rows, scalar1=1.0, scalar2=0.0, op0=ALU.mult, op1=ALU.add
                 )
             else:
-                nc.vector.tensor_copy(out=grouped[:], in_=rows)
+                nc.vector.tensor_copy(
+                    out=grouped[:].rearrange("p (c i) t -> p c t i", i=4),
+                    in_=k_first_raw[c][:, :, first : first + width].rearrange("p t (c i) -> p c t i", i=4),
+                )
             grouped_of[c, first] = grouped
 
         def quantise_chunk(c, first, width):

import math
from contextlib import ExitStack

import concourse.mybir as mybir
from concourse.masks import make_identity

F32 = mybir.dt.float32
BF16 = mybir.dt.bfloat16
I32 = mybir.dt.int32
U32 = mybir.dt.uint32
U8 = mybir.dt.uint8
FP8X4 = mybir.dt.float8_e4m3fn_x4
ALU = mybir.AluOpType
ACT = mybir.ActivationFunctionType
AXIS = mybir.AxisListType

P = 128
PACK = 4
K_PASS = P * PACK
SEQ = 512
HEADS = 16
HEAD_DIM = 128
FEATURES = HEADS * HEAD_DIM
N_OUT = 2048
TILES = SEQ // P
GROUP_HEADS = K_PASS // HEAD_DIM
GROUPS = HEADS // GROUP_HEADS
PAIR = 2
PAIRS = HEADS // PAIR
UNITS = TILES * PAIRS
HALF_UNITS = 4
HALF_HEADS = HALF_UNITS * PAIR
HALF_GROUPS = HALF_HEADS // GROUP_HEADS
N_TILE = 512
N_TILES = N_OUT // N_TILE
SQRT_DIM = math.sqrt(HEAD_DIM)
P0, PM = 2, 29
BE, BU = 8, 18
TB = 2
TE, TA = 4, 3
WIDTH = {"gpsimd": 256, "vector": 128}
GROUPED_BUFS = {"gpsimd": 1, "vector": 2}
VE, GS = 16, 2
Q_PHASE = 2
MASK_ROUNDS = (3, 12, 20)
WARM_ROUNDS = (2, 3)
WARM, WARM2 = 3, 2

FLOPS = 2 * 2 * HEADS * SEQ * SEQ * HEAD_DIM + 2 * SEQ * FEATURES * N_OUT


def tile_mptattentionfused_pa_kernel(tc, xq, xk, xv, mask, w_out, out):
    nc = tc.nc
    xq_rows = xq.rearrange("b (t p) h d -> p (b t) (h d)", p=P)
    xk_rows = xk.rearrange("b (t p) h d -> p (b t) (h d)", p=P)
    xv_rows = xv.rearrange("b (u p e) h d -> p (b u) e (h d)", p=P, e=2)
    w_rows = w_out.rearrange("(g u p e) n -> g p u e n", u=2, p=P, e=2)
    mask_rows = mask.rearrange("a b (t p) j -> p (a b t) j", p=P)
    out_rows = out.rearrange("b (t p) n -> (b t) p n", p=P)

    with ExitStack() as stack:
        keep = stack.enter_context(tc.tile_pool(name="keep", bufs=1))
        work = stack.enter_context(tc.tile_pool(name="work", bufs=2))
        psum = stack.enter_context(tc.psum_pool(name="psum", bufs=1))
        stack.enter_context(tc.manual_schedule())

        mask_sb = keep.tile([P, TILES, SEQ], BF16)
        k_raw = []
        q_raw = {}
        k_first_raw = []

        def load_k(pair, pairs):
            width = PAIR * HEAD_DIM
            tile = work.tile([P, TILES, pairs * width], BF16, tag="k_raw%d" % pairs, bufs=2, name="k_raw")
            nc.sync.dma_start(out=tile[:], in_=xk_rows[:, :, pair * width : (pair + pairs) * width])
            for m in range(pairs):
                k_raw.append(tile[:, :, m * width : (m + 1) * width])

        def load_q(j):
            it, half = divmod(j, 2)
            width = HALF_HEADS * HEAD_DIM
            tile = work.tile([P, width], BF16, tag="q_raw", bufs=4, name="q_raw%d" % j)
            nc.sync.dma_start(out=tile[:], in_=xq_rows[:, it, half * width : (half + 1) * width])
            q_raw[j] = tile

        def load_chunk(rows, name):
            raw = work.tile([P, PACK, N_TILE], BF16, tag="raw", bufs=8, name=name)
            for u in range(2):
                nc.sync.dma_start(out=raw[:, 2 * u : 2 * u + 2, :], in_=rows[:, u, :, :])
            k_first_raw.append(raw)

        def load_xv(c):
            load_chunk(xv_rows[:, :, :, c * N_TILE : (c + 1) * N_TILE], "xv_raw%d" % c)

        nc.sync.dma_start(out=mask_sb[:, 0, :], in_=mask_rows[:, 0, :])
        load_k(0, 1)
        load_q(0)
        load_k(1, 1)
        load_xv(0)
        load_k(2, 2)
        load_xv(1)
        load_q(1)
        load_k(4, 2)
        load_xv(2)
        load_k(6, 2)
        load_xv(3)
        nc.sync.dma_start(out=mask_sb[:, 1:TILES, :], in_=mask_rows[:, 1:TILES, :])
        load_q(2)
        load_q(3)
        for n in range(N_TILES):
            for g in range(GROUPS):
                load_chunk(w_rows[g][:, :, :, n * N_TILE : (n + 1) * N_TILE], "w_raw%d_%d" % (n, g))
            load_q(4 + n)

        ones = keep.tile([P, 1], F32)
        nc.vector.memset(ones[:], 1.0)
        dist_i = keep.tile([P, SEQ], I32)
        nc.gpsimd.iota(dist_i[:], pattern=[[1, SEQ]], base=1 - SEQ, channel_multiplier=0)
        part_i = keep.tile([P, 1], I32)
        nc.gpsimd.iota(part_i[:], pattern=[[1, 1]], base=0, channel_multiplier=1)
        key_dist_i = keep.tile([P, TILES], I32)
        nc.gpsimd.iota(key_dist_i[:], pattern=[[P, TILES]], base=1 - SEQ, channel_multiplier=1)
        ident_f = keep.tile([P, P], F32)
        make_identity(nc, ident_f[:])
        ident_bf = keep.tile([P, P], BF16)
        make_identity(nc, ident_bf[:])

        table = keep.tile([P, 1], F32)
        nc.scalar.activation(out=table[:], in_=ones[:], func=ACT.Exp)

        amp = keep.tile([P, HEADS], F32)
        for h in range(HEADS):
            nc.scalar.mul(out=amp[:, h : h + 1], in_=ones[:], mul=2.0 ** (-(h + 1) / 2) * SQRT_DIM)
        key_dist = keep.tile([P, TILES], F32)

        nc.vector.tensor_copy(out=key_dist[:], in_=key_dist_i[:])
        part = keep.tile([P, 1], F32)
        nc.vector.tensor_copy(out=part[:], in_=part_i[:])
        dist = keep.tile([P, SEQ], F32)
        nc.vector.tensor_copy(out=dist[:], in_=dist_i[:])
        alibi = keep.tile([P, HEADS, TILES], F32)
        nc.vector.tensor_tensor(
            out=alibi[:],
            in0=amp[:].unsqueeze(2).to_broadcast([P, HEADS, TILES]),
            in1=key_dist[:].unsqueeze(1).to_broadcast([P, HEADS, TILES]),
            op=ALU.mult,
        )

        dist_bf = keep.tile([P, SEQ], BF16)
        nc.vector.tensor_copy(out=dist_bf[:], in_=dist[:])
        rows_of = []
        for m in range(3):
            low = keep.tile([P, 1], F32, name="low%d" % m)
            nc.gpsimd.tensor_single_scalar(out=low[:], in_=part[:], scalar=float(m), op=ALU.is_equal)
            high = keep.tile([P, 1], F32, name="high%d" % m)
            nc.gpsimd.tensor_single_scalar(out=high[:], in_=part[:], scalar=float(64 + m), op=ALU.is_equal)
            both = keep.tile([P, 1], F32, name="both%d" % m)
            nc.gpsimd.tensor_tensor(out=both[:], in0=low[:], in1=high[:], op=ALU.add)
            rows_of.append(both)
        nc.vector.tensor_tensor(
            out=dist_bf[64:P, :], in0=dist[64:P, :], in1=dist_bf[64:P, :], op=ALU.subtract
        )
        rest = amp
        parts = []
        for m in range(3):
            rounded = keep.tile([P, HEADS], BF16, name="rounded%d" % m)
            nc.gpsimd.tensor_copy(out=rounded[:], in_=rest[:])
            placed = keep.tile([P, HEADS], F32, name="placed%d" % m)
            nc.gpsimd.tensor_scalar_mul(out=placed[:], in0=rounded[:], scalar1=rows_of[m][:])
            parts.append(placed)
            if m < 2:
                left = keep.tile([P, HEADS], F32, name="left%d" % m)
                nc.gpsimd.tensor_tensor(out=left[:], in0=rest[:], in1=rounded[:], op=ALU.subtract)
                rest = left
        coef_a = keep.tile([P, HEADS], F32)
        nc.gpsimd.tensor_tensor(out=coef_a[:], in0=parts[0][:], in1=parts[1][:], op=ALU.add)
        coef = keep.tile([P, HEADS], BF16)
        nc.gpsimd.tensor_tensor(out=coef[:], in0=coef_a[:], in1=parts[2][:], op=ALU.add)

        k_first_codes = keep.tile([P, 1 + GROUPS, N_OUT], U32, align_bytes=64)
        k_first_scales = keep.tile([P, 1 + GROUPS, N_OUT], U8, align_bytes=64)
        k_t = keep.tile([P, HEADS, SEQ], BF16)
        mask_t = keep.tile([P, TILES, TILES, P], F32)

        grouped_of = {}
        warm_of = []
        copies = []
        q_t_of = {}
        bias_of = {}
        scores_of = {}
        row_max_of = {}
        shift_of = {}
        e_of = {}
        e_grouped_of = {}
        e_mx_of = {}
        sums_of = {}
        inv_of = {}
        pv_of = {}
        o_of = {}
        o_grouped_of = {}
        o_mx_of = {}
        e_words_of = {}
        o_words_of = {}
        acc_of = {}

        def transpose_mask(it):
            mask_ps = psum.tile([P, TILES, P], BF16, tag="tr", bufs=3, name="mask_ps")
            for t in range(TILES):
                nc.tensor.transpose(mask_ps[:, t, :], mask_sb[:, it, t * P : (t + 1) * P], ident_bf[:])
            copies.append(lambda copy: nc.scalar.mul(out=mask_t[:, it, :, :], in_=mask_ps[:], mul=SQRT_DIM))

        def regroup(c, first, width, engine):
            grouped = work.tile(
                [P, width, PACK], BF16, tag="grouped_" + engine, bufs=GROUPED_BUFS[engine], align_bytes=64, name="grouped"
            )
            rows = k_first_raw[c][:, :, first : first + width].rearrange("p t c -> p c t")
            if engine == "gpsimd":
                nc.gpsimd.tensor_scalar(
                    out=grouped[:], in0=rows, scalar1=1.0, scalar2=0.0, op0=ALU.mult, op1=ALU.add
                )
            else:
                nc.vector.tensor_copy(
                    out=grouped[:].rearrange("p (c i) t -> p c t i", i=4),
                    in_=k_first_raw[c][:, :, first : first + width].rearrange("p t (c i) -> p c t i", i=4),
                )
            grouped_of[c, first] = grouped

        def quantise_chunk(c, first, width):
            if c < N_TILES:
                r, n = 0, c
            else:
                n, g = divmod(c - N_TILES, GROUPS)
                r = 1 + g
            cols = slice(n * N_TILE + first, n * N_TILE + first + width)
            nc.vector.quantize_mx(
                out=k_first_codes[:, r, cols].bitcast(FP8X4),
                scales=k_first_scales[:, r, cols],
                in_=grouped_of[c, first][:].rearrange("p c t -> p (c t)"),
            )

        def transpose_k(pair):
            k_ps = psum.tile([P, PAIR, TILES, P], BF16, tag="tr", bufs=3, name="k_ps")
            for b in range(PAIR):
                cols = slice(b * HEAD_DIM, (b + 1) * HEAD_DIM)
                for t in range(TILES):
                    nc.tensor.transpose(k_ps[:, b, t, :], k_raw[pair][:, t, cols], ident_bf[:])
            copies.append(
                lambda copy: copy(
                    out=k_t[:, pair * PAIR : (pair + 1) * PAIR, :],
                    in_=k_ps[:].rearrange("p b t j -> p b (t j)"),
                )
            )

        def transpose_q(j):
            q_ps = psum.tile([P, HALF_HEADS, P], BF16, tag="tr", bufs=3, name="q_ps")
            for a in range(HALF_HEADS):
                nc.tensor.transpose(q_ps[:, a, :], q_raw[j][:, a * HEAD_DIM : (a + 1) * HEAD_DIM], ident_bf[:])
            q_t = work.tile([P, HALF_HEADS, P], BF16, tag="q_t", bufs=3, name="q_t")
            q_t_of[j] = q_t
            copies.append(lambda copy: copy(out=q_t[:], in_=q_ps[:]))

        def has_product(n, b):
            return b == 1 and P0 <= n < PM and n not in project_in

        def is_built(n, b, t):
            if has_product(n, b):
                return False
            if b == 1:
                return t < TB
            return t < TE if n < BE else n >= BU and t < TA

        def build_bias(n):
            it, pair = divmod(n, PAIRS)
            blocks = [(b, t) for b in range(PAIR) for t in range(TILES) if is_built(n, b, t)]
            if not blocks:
                return
            bias_of[n] = work.tile([P, PAIR, TILES, P], F32, tag="bias_t", bufs=3, name="bias_t")
            for b, t in blocks:
                nc.vector.tensor_scalar_add(
                    out=bias_of[n][:, b, t, :],
                    in0=mask_t[:, it, t, :],
                    scalar1=alibi[:, pair * PAIR + b, t : t + 1],
                )

        def open_group(n):
            scores_of.setdefault(n, []).append(psum.tile([P, SEQ], F32, tag="s", bufs=4, name="s_ps"))

        def multiply_scores(n, b):
            h = (n % PAIRS) * PAIR + b
            product = has_product(n, b)
            if not product:
                open_group(n)
            nc.tensor.matmul(
                out=scores_of[n][b][:],
                lhsT=q_t_of[n // HALF_UNITS][:, h % HALF_HEADS, :],
                rhs=k_t[:, h, :],
                start=not product,
                stop=False,
            )

        def add_bias(n, b):
            it, pair = divmod(n, PAIRS)
            added = []
            for t in range(TILES):
                if is_built(n, b, t):
                    added.append((t, bias_of[n][:, b, t, :]))
                else:
                    added.append((t, mask_t[:, it, t, :]))
                    if not has_product(n, b):
                        added.append((t, alibi[:, pair * PAIR + b, t : t + 1].to_broadcast([P, P])))
            for m, (t, rows) in enumerate(added):
                nc.tensor.matmul(
                    out=scores_of[n][b][:, t * P : (t + 1) * P],
                    lhsT=rows,
                    rhs=ident_f[:],
                    is_transpose=True,
                    start=False,
                    stop=(m == len(added) - 1),
                )

        def close_scores(n):
            for b in range(PAIR):
                if has_product(n, b):
                    h = (n % PAIRS) * PAIR + b
                    open_group(n)
                    nc.tensor.matmul(
                        out=scores_of[n][b][:],
                        lhsT=coef[:, h : h + 1].to_broadcast([P, P]),
                        rhs=dist_bf[:],
                        start=True,
                        stop=False,
                    )

        def row_maxima(n):
            row_max = work.tile([P, PAIR], F32, tag="row_max", bufs=3, name="row_max")
            for b in range(PAIR):
                nc.vector.tensor_reduce(out=row_max[:, b : b + 1], in_=scores_of[n][b][:], axis=AXIS.X, op=ALU.max)
            row_max_of[n] = row_max

        def shifts(n):
            shift = work.tile([P, PAIR], F32, tag="shift", bufs=3, name="shift")
            nc.scalar.mul(out=shift[:], in_=row_max_of[n][:], mul=-1.0 / SQRT_DIM)
            shift_of[n] = shift

        def exponentials(n):
            k, m = divmod(n, 2)
            if m == 0:
                sums_of[k] = work.tile([P, 2, PAIR], F32, tag="row_sum", bufs=4, name="row_sum")
            e_of[n] = []
            for b in range(PAIR):
                e_sb = work.tile([P, SEQ], BF16, tag="e_sb", bufs=6, name="e_sb")
                nc.scalar.activation(
                    out=e_sb[:],
                    in_=scores_of[n][b][:],
                    func=ACT.Exp,
                    bias=shift_of[n][:, b : b + 1],
                    scale=1.0 / SQRT_DIM,
                    accum_out=sums_of[k][:, m, b : b + 1],
                )
                e_of[n].append(e_sb)

        def rows_to_words(rows):
            words_ps = psum.tile([P, len(rows), 2, P], F32, tag="tr", bufs=3, name="words_ps")
            for a in range(len(rows)):
                for u in range(2):
                    nc.tensor.transpose(
                        words_ps[:, a, u, :], rows[a].bitcast(F32)[:, u * P : (u + 1) * P], ident_f[:]
                    )
            return words_ps

        def words_to_grouped(words_ps, tag):
            tiles = words_ps[:].shape[1]
            grouped = work.tile([P, tiles * P * PACK], BF16, tag=tag, bufs=2, align_bytes=64, name=tag)
            nc.scalar.copy(
                out=grouped[:].bitcast(F32).rearrange("p (a i u) -> p a i u", a=tiles, u=2),
                in_=words_ps[:].rearrange("p a u i -> p a i u"),
            )
            return grouped

        def quantise_e(n):
            e_codes = work.tile([P, PAIR * P], U32, tag="e_codes", bufs=4, align_bytes=64, name="e_codes")
            e_scales = work.tile([P, PAIR * P], U8, tag="e_scales", bufs=4, align_bytes=64, name="e_scales")
            nc.vector.quantize_mx(out=e_codes[:].bitcast(FP8X4), scales=e_scales[:], in_=e_grouped_of[n][:])
            e_mx_of[n] = (e_codes, e_scales)

        def weighted_values(n):
            k, m = divmod(n, 2)
            if m == 0:
                pv_of[k] = psum.tile([P, 2, PAIR, HEAD_DIM], F32, tag="pv", bufs=1, name="pv_ps")
            e_codes, e_scales = e_mx_of[n]
            for b in range(PAIR):
                h = (n % PAIRS) * PAIR + b
                rows = slice(b * P, (b + 1) * P)
                cols = slice(h * HEAD_DIM, (h + 1) * HEAD_DIM)
                nc.tensor.matmul_mx(
                    out=pv_of[k][:, m, b, :],
                    lhsT=e_codes[:, rows].bitcast(FP8X4),
                    lhsT_scale=e_scales[:, rows],
                    rhs=k_first_codes[:, 0, cols].bitcast(FP8X4),
                    rhs_scale=k_first_scales[:, 0, cols],
                    start=True,
                    stop=True,
                )

        def invert_sums(k):
            inv_sum = work.tile([P, 2, PAIR], F32, tag="inv_sum", bufs=3, name="inv_sum")
            nc.vector.reciprocal(out=inv_sum[:], in_=sums_of[k][:])
            inv_of[k] = inv_sum

        def normalise(n):
            k, m = divmod(n, 2)
            j, u = divmod(n, HALF_UNITS)
            if u == 0:
                o_of[j] = work.tile([P, HALF_HEADS, HEAD_DIM], BF16, tag="o_sb", bufs=2, name="o_sb")
            nc.vector.tensor_tensor(
                out=o_of[j][:, u * PAIR : (u + 1) * PAIR, :],
                in0=pv_of[k][:, m, :, :],
                in1=inv_of[k][:, m, :].unsqueeze(2).to_broadcast([P, PAIR, HEAD_DIM]),
                op=ALU.mult,
            )

        def quantise_o(j, first, last):
            it, half = divmod(j, 2)
            if half == 0:
                o_codes = work.tile([P, GROUPS * P], U32, tag="o_codes", bufs=4, align_bytes=64, name="o_codes")
                o_scales = work.tile([P, GROUPS * P], U8, tag="o_scales", bufs=4, align_bytes=64, name="o_scales")
                o_mx_of[it] = (o_codes, o_scales)
            o_codes, o_scales = o_mx_of[it]
            cols = slice((half * HALF_GROUPS + first) * P, (half * HALF_GROUPS + last) * P)
            nc.vector.quantize_mx(
                out=o_codes[:, cols].bitcast(FP8X4), scales=o_scales[:, cols], in_=o_grouped_of[j, first][:]
            )


        def project(it, n, groups, tag, bufs):
            o_codes, o_scales = o_mx_of[it]
            if groups[0] == 0:
                acc_of[it, n] = psum.tile([P, N_TILE], F32, tag=tag, bufs=bufs, name="acc")
            cols = slice(n * N_TILE, (n + 1) * N_TILE)
            for g in groups:
                rows = slice(g * P, (g + 1) * P)
                nc.tensor.matmul_mx(
                    out=acc_of[it, n][:],
                    lhsT=o_codes[:, rows].bitcast(FP8X4),
                    lhsT_scale=o_scales[:, rows],
                    rhs=k_first_codes[:, 1 + g, cols].bitcast(FP8X4),
                    rhs_scale=k_first_scales[:, 1 + g, cols],
                    start=(g == 0),
                    stop=(g == GROUPS - 1),
                )

        def store(it, n, copy):
            result = work.tile([P, N_TILE], F32, tag="result", bufs=6, name="result")
            copy(out=result[:], in_=acc_of[it, n][:])
            nc.sync.dma_start(out=out_rows[it][:, n * N_TILE : (n + 1) * N_TILE], in_=result[:])

        CHUNKS = (1 + GROUPS) * N_TILES
        ALL = tuple(range(GROUPS))

        jobs = {"vector": {}, "gpsimd": {}}
        in_hand = {}
        last_round_of = {}
        next_chunk = 0
        for r in range(UNITS + 4):
            for engine, first_round, last_round in (("vector", 0, VE), ("gpsimd", GS, UNITS + 4)):
                if engine not in in_hand and first_round <= r < last_round and next_chunk < CHUNKS:
                    in_hand[engine] = (next_chunk, 0)
                    next_chunk += 1
                if engine in in_hand:
                    c, first = in_hand[engine]
                    jobs[engine][r] = (c, first, WIDTH[engine])
                    last_round_of[c] = r
                    if first + WIDTH[engine] < N_TILE:
                        in_hand[engine] = (c, first + WIDTH[engine])
                    else:
                        in_hand.pop(engine)

        project_in = {}
        waiting = sorted(
            (max(PAIRS * it + 15, 2 + max(last_round_of[N_TILES + GROUPS * n + g] for g in range(GROUPS))), it, n)
            for it in range(TILES - 1)
            for n in range(N_TILES)
        )
        late_tiles = []
        r = 0
        while waiting:
            if waiting[0][0] <= r:
                it, n = waiting.pop(0)[1:]
                if r + 1 + len(waiting) < UNITS + 2:
                    project_in[r] = (it, n, ALL[:2])
                    project_in[r + 1] = (it, n, ALL[2:])
                    r += 1
                elif r <= UNITS + 2:
                    project_in[r] = (it, n, ALL)
                else:
                    late_tiles.append((it, n))
            r += 1

        o_jobs = {9 + HALF_UNITS * j: (j, 0, HALF_GROUPS) for j in range(2 * TILES - 2)}
        o_jobs[UNITS] = (2 * TILES - 2, 0, HALF_GROUPS)
        o_jobs[UNITS + 2] = (2 * TILES - 1, 0, 1)
        o_jobs[UNITS + 4] = (2 * TILES - 1, 1, 2)

        def copy_o(r):
            if r - 1 in o_jobs:
                j, first, last = o_jobs[r - 1]
                o_grouped_of[j, first] = words_to_grouped(o_words_of[j, first], "o_grouped")

        def start_o_words(r):
            if r in o_jobs:
                j, first, last = o_jobs[r]
                o_words_of[j, first] = rows_to_words(
                    [
                        o_of[j][:, a * GROUP_HEADS : (a + 1) * GROUP_HEADS, :].rearrange("p h d -> p (h d)")
                        for a in range(first, last)
                    ]
                )

        def start_e_words(n):
            if 0 <= n < UNITS:
                e_words_of[n] = rows_to_words([e[:] for e in e_of[n]])

        def last_tile(n, groups):
            project(TILES - 1, n, groups, "s", 4)

        def store_finished(r, copy):
            if r in project_in:
                it, n, groups = project_in[r]
                if groups[-1] == GROUPS - 1:
                    store(it, n, copy)

        def scalar_copies(r):
            if r > UNITS:
                copy_o(r)
            if r <= UNITS:
                store_finished(r - 1, nc.scalar.copy)
            if 0 <= r - 3 < UNITS:
                e_grouped_of[r - 3] = words_to_grouped(e_words_of[r - 3], "e_grouped")
            for move in copies:
                move(nc.scalar.copy)
            copies.clear()
            if r <= UNITS:
                copy_o(r)

        def vector_and_softmax(r):
            if r in jobs["gpsimd"]:
                regroup(*jobs["gpsimd"][r], "gpsimd")
            for n in norm_units(r):
                normalise(n)
            if 0 <= r - 1 < UNITS:
                row_maxima(r - 1)
                shifts(r - 1)
                exponentials(r - 1)
            if 0 <= r - 4 < UNITS and r % 2 == 0:
                invert_sums((r - 4) // 2)
            if r - 1 in jobs["vector"]:
                quantise_chunk(*jobs["vector"][r - 1])
            if r + 1 < UNITS:
                build_bias(r + 1)
            if r in jobs["vector"]:
                regroup(*jobs["vector"][r], "vector")
            if r - 1 in o_jobs:
                quantise_o(*o_jobs[r - 1])
            if r == UNITS + 5:
                for m, (it, n) in enumerate(late_tiles):
                    store(it, n, nc.scalar.copy if m % 2 == 0 else nc.vector.tensor_copy)
            if r in jobs["gpsimd"]:
                quantise_chunk(*jobs["gpsimd"][r])
            if 0 <= r - 3 < UNITS:
                quantise_e(r - 3)

        def mx_passes(r):
            for n in pv_units(r):
                weighted_values(n)
            if r in project_in:
                project(*project_in[r], "tr", 3)

        def pv_units(r):
            if r >= UNITS:
                return [r - 4] if r - 4 < UNITS else []
            return [r - 5, r - 4] if r % 2 == 1 and r >= 5 else []

        def norm_units(r):
            if r > UNITS:
                return [r - 5] if r - 5 < UNITS else []
            if r == UNITS:
                return [r - 6, r - 5]
            return [r - 6] if r >= 6 else []

        def tensor_round(r):
            if r in WARM_ROUNDS:
                warm_up(2)
            multiply_scores(r, 0)
            add_bias(r, 0)
            close_scores(r)
            start_e_words(r - 2)
            multiply_scores(r, 1)
            mx_passes(r)
            add_bias(r, 1)
            start_o_words(r)
            if r + 2 < PAIRS:
                transpose_k(r + 2)
            if r % HALF_UNITS == Q_PHASE and r // HALF_UNITS + 1 < 2 * TILES:
                transpose_q(r // HALF_UNITS + 1)
            if r in MASK_ROUNDS:
                transpose_mask(1 + MASK_ROUNDS.index(r))

        def tensor_drain(r):
            m = r - UNITS
            if m == 3:
                last_tile(3, ALL[:2])
            mx_passes(r)
            start_e_words(r - 2)
            if m == 1:
                last_tile(0, ALL[:2])
                last_tile(1, ALL[:2])
            if m == 2:
                last_tile(2, ALL[:2])
            if m == 3:
                for it, n in late_tiles[:1]:
                    project(it, n, ALL, "tr", 3)
            start_o_words(r)
            if m == 4:
                for it, n in late_tiles[1:]:
                    project(it, n, ALL, "tr", 3)
                for n in range(N_TILES):
                    last_tile(n, ALL[2:3])
            store_finished(r, nc.vector.tensor_copy)

        def warm_up(passes):
            warm = psum.tile([P, P], F32, tag="tr", bufs=3, name="warm")
            for m in range(passes):
                nc.tensor.matmul(out=warm[:], lhsT=ident_f[:], rhs=ident_f[:], start=True, stop=True)

        warm_up(WARM)
        transpose_mask(0)
        transpose_k(0)
        transpose_q(0)
        transpose_k(1)
        warm_up(WARM2)
        for m, move in enumerate(copies):
            move(nc.vector.tensor_copy if m == 2 else nc.scalar.copy)
        copies.clear()
        build_bias(0)
        for r in range(UNITS + 6):
            scalar_copies(r)
            vector_and_softmax(r)
            if r < UNITS:
                tensor_round(r)
            else:
                tensor_drain(r)

        for n in range(N_TILES):
            last_tile(n, ALL[3:])
            store(TILES - 1, n, nc.scalar.copy if n % 2 == 0 else nc.vector.tensor_copy)
